import numpy as np
import ml_dtypes


def mxq(x, axis, fmt="e4m3"):
    dtype, down = {"e4m3": (ml_dtypes.float8_e4m3fn, 7), "e5m2": (ml_dtypes.float8_e5m2, 14)}[fmt]
    v = np.moveaxis(np.asarray(x, np.float32).astype(ml_dtypes.bfloat16).astype(np.float64), axis, -1)
    blocks = v.reshape(v.shape[:-1] + (-1, 32))
    amax = np.abs(blocks).max(-1, keepdims=True)
    byte = np.maximum(np.where(amax > 0, np.frexp(amax)[1] - 1 + 127, 0) - down, 1)
    scale = np.exp2(byte - 127.0)
    codes = (blocks / scale).astype(np.float32).astype(dtype).astype(np.float64)
    return np.moveaxis((codes * scale).reshape(v.shape), -1, axis)


WIDE = False


def mx_kscale(k):
    if not WIDE:
        return np.ones(k)
    levels = np.array([10, -10, 5, -5, 0])
    if k % 512:
        return np.exp2(np.random.permutation(np.resize(levels, k // 32))).repeat(32)
    a = np.empty((k // 512, 16))
    for p in range(k // 512):
        a[p, :8] = np.random.permutation(np.resize(levels, 8))
        for g in range(8):
            far = levels[np.abs(levels - a[p, g]) >= 10]
            a[p, g + 8] = far[np.random.randint(len(far))]
    return np.exp2(a.ravel()).repeat(32)


BF16 = ml_dtypes.bfloat16


def bf(x):
    return np.asarray(x, np.float32).astype(BF16)


def f64(x):
    return np.asarray(x).astype(np.float64)


E2M1 = np.array([0.0, 0.5, 1.0, 1.5, 2.0, 3.0, 4.0, 6.0, -0.0, -0.5, -1.0, -1.5, -2.0, -3.0, -4.0, -6.0])


def pack_weight(w, fmt):
    k, n = w.shape
    w = f64(bf(w)).reshape(k // 32, 32, n)
    amax = np.abs(w).max(1)
    if fmt == "e4m3":
        byte = np.frexp(amax)[1] - 1 + 127 - 7
    else:
        mant, ex = np.frexp(amax / 6.0)
        byte = np.where(mant > 0.5, ex, ex - 1) + 127
    byte = np.clip(np.where(amax > 0, byte, 1), 1, 254)
    scaled = (w * np.exp2(127.0 - byte)[:, None, :]).reshape(k, n).astype(np.float32)
    by_word = np.ascontiguousarray(scaled.reshape(k // 512, 128, 4, n).transpose(0, 1, 3, 2))
    if fmt == "e4m3":
        words = by_word.astype(ml_dtypes.float8_e4m3fn).view(np.uint8)
    else:
        c = by_word.astype(ml_dtypes.float4_e2m1fn).view(np.uint8) & 0xF
        words = c[..., 0::2] | (c[..., 1::2] << 4)
    return np.ascontiguousarray(words), np.ascontiguousarray(byte.astype(np.uint8).reshape(k // 512, 16, n))


def unpack_weight(words, scales, fmt):
    g, p, n, _ = words.shape
    if fmt == "e4m3":
        vals = np.ascontiguousarray(words).view(ml_dtypes.float8_e4m3fn).astype(np.float64)
    else:
        nib = np.empty((g, p, n, 4), np.uint8)
        nib[..., 0::2] = words & 0xF
        nib[..., 1::2] = words >> 4
        vals = E2M1[nib]
    vals = vals * np.repeat(np.exp2(scales.astype(np.float64) - 127.0), 8, axis=1)[..., None]
    return vals.transpose(0, 1, 3, 2).reshape(g * 512, n)
def pack4(w):
    words, scales = pack_weight(w, "e2m1")
    return words.reshape(words.shape[0], 128, -1), scales


def unpack4(words, scales):
    return unpack_weight(words.reshape(words.shape[0], 128, -1, 2), scales, "e2m1")


B, IN, HID, BLK, OUT = 4096, 512, 1024, 512, 10
NB = HID // BLK


def draw0():
    s = mx_kscale(IN)
    t = np.tile(mx_kscale(BLK), NB)
    x = bf(np.random.standard_normal((B, IN)) * s)
    W1 = np.random.standard_normal((HID, IN)) / np.sqrt(IN) / s * t[:, None]
    W1_words, W1_scales = pack4(W1.T)
    return {
        "x": x,
        "W1_words": W1_words,
        "W1_scales": W1_scales,
        "b1": bf(np.random.standard_normal(HID) * 0.3 * t),
        "Wb": bf(np.random.standard_normal((NB, BLK, BLK)) * 1.4 / np.sqrt(BLK) / t.reshape(NB, 1, BLK)),
        "bb": bf(np.random.standard_normal(HID) * 0.3),
    }


def core(x, W1_words, W1_scales, b1, Wb, bb):
    h = np.maximum((mxq(f64(x), 1, "e4m3") @ unpack4(W1_words, W1_scales)) + f64(b1), 0.0)
    hb = h.reshape(B, NB, BLK)
    yb = (mxq(hb, 2, "e4m3").transpose(1, 0, 2) @ mxq(f64(Wb), 2, "e4m3").transpose(0, 2, 1)).transpose(1, 0, 2)
    return np.maximum(yb.reshape(B, HID) + f64(bb), 0.0)


def e4m3fn_bytes(y):
    return np.clip(np.asarray(y, np.float64), -448.0, 448.0).astype(np.float32).astype(ml_dtypes.float8_e4m3fn).view(np.uint8)


def e4m3fn_values(b):
    return np.asarray(b, np.uint8).view(ml_dtypes.float8_e4m3fn).astype(np.float64)


def setup_inputs():
    d = draw0()
    x0 = np.asarray(d['x']).astype(np.float64)
    s = (np.max(np.abs(x0), axis=(0,), keepdims=True) / 448.0).astype(np.float32)
    out = {}
    for k, v in d.items():
        if k == 'x':
            out['x_bytes'] = e4m3fn_bytes(x0 / s.astype(np.float64))
            out['x_scale'] = s
        else:
            out[k] = v
    return out


def reference(x_bytes, x_scale, W1_words, W1_scales, b1, Wb, bb):
    return core(e4m3fn_values(x_bytes) * x_scale.astype(np.float64), W1_words, W1_scales, b1, Wb, bb)

@@ -1,0 +1,293 @@
+from contextlib import ExitStack
+
+import concourse.mybir as mybir
+from concourse.masks import make_identity
+
+B, IN, HID, BLK = 4096, 512, 1024, 512
+FLOPS = 2 * B * IN * HID + 2 * B * HID * BLK
+
+F32 = mybir.dt.float32
+BF16 = mybir.dt.bfloat16
+U32 = mybir.dt.uint32
+I32 = mybir.dt.int32
+U8 = mybir.dt.uint8
+FP8 = mybir.dt.float8_e4m3fn
+FP8X4 = mybir.dt.float8_e4m3fn_x4
+FP4X4 = mybir.dt.float4_e2m1fn_x4
+ALU = mybir.AluOpType
+ACT = mybir.ActivationFunctionType
+
+P = 128
+GROUPS = [2, 4, 4, 4, 4, 4, 4, 4, 2]
+
+
+def tile_blockdiagmnistconvertible_pa_t_w4_kernel(tc, x_bytes, x_scale, W1_words, W1_scales, b1, Wb, bb, out):
+    nc = tc.nc
+    L = len(GROUPS)
+    first = [P * sum(GROUPS[:g]) for g in range(L)]
+
+    with ExitStack() as ctx:
+        keep = ctx.enter_context(tc.tile_pool(name="keep", bufs=1))
+        work = ctx.enter_context(tc.tile_pool(name="work", bufs=3))
+        psum = ctx.enter_context(tc.psum_pool(name="psum", bufs=2))
+
+        ident = keep.tile([P, P], F32, name="ident")
+        sc = keep.tile([P, IN], F32, name="sc")
+        w1r = keep.tile([P, 2048], U8, name="w1r")
+        w1p = keep.tile([P, 2, 4, P, 2], U8, name="w1p", align_bytes=64)
+        wsr = keep.tile([P, HID], U8, name="wsr", align_bytes=64)
+        wsp = keep.tile([P, 2, 4, P], U8, name="wsp", align_bytes=64)
+        b1c = keep.tile([P, 2, 4], BF16, name="b1c")
+        bbc = keep.tile([P, 4], BF16, name="bbc")
+        bbr = keep.tile([P, BLK], BF16, name="bbr")
+        warm = keep.tile([P, 1], F32, name="warm")
+        xb = [keep.tile([P, GROUPS[g], IN], U8, name=f"xb{g}") for g in range(L)]
+        wbr = [keep.tile([P, 4, BLK], BF16, name=f"wbr{n}") for n in range(2)]
+        wbc = [keep.tile([P, BLK], U32, name=f"wbc{n}", align_bytes=64) for n in range(2)]
+        wbs = [keep.tile([P, BLK], U8, name=f"wbs{n}", align_bytes=64) for n in range(2)]
+
+        def load_x(g):
+            src = x_bytes[first[g] : first[g] + P * GROUPS[g], :].rearrange("(p a) k -> p a k", a=GROUPS[g])
+            nc.sync.dma_start(out=xb[g][:], in_=src)
+
+        nc.vector.memset(warm[:], 0.0)
+        nc.vector.memset(wsr[:].bitcast(I32), 0)
+        nc.scalar.activation(out=warm[:], in_=warm[:], func=ACT.Relu)
+        make_identity(nc, ident[:])
+        load_x(0)
+        nc.sync.dma_start(out=sc[:], in_=x_scale.rearrange("o k -> (o k)").partition_broadcast(P))
+        nc.sync.dma_start(out=w1r[:], in_=W1_words[0])
+        for q in range(4):
+            nc.sync.dma_start(
+                out=wsr[32 * q : 32 * q + 4, :].bitcast(I32), in_=W1_scales[0, 4 * q : 4 * q + 4, :].bitcast(I32)
+            )
+        load_x(1)
+        nc.sync.dma_start(out=b1c[:], in_=b1.rearrange("(n p t) -> p n t", n=2, t=4))
+        nc.sync.dma_start(out=wbr[1][:], in_=Wb[1].rearrange("(p t) k -> p t k", t=4))
+        nc.sync.dma_start(out=bbc[:], in_=bb[BLK:HID].rearrange("(p t) -> p t", t=4))
+        nc.sync.dma_start(out=wbr[0][:], in_=Wb[0].rearrange("(t p) k -> p t k", p=P))
+        nc.sync.dma_start(out=bbr[:], in_=bb[0:BLK].partition_broadcast(P))
+        for g in range(2, L):
+            load_x(g)
+
+        xs, xg, xc, xsc = {}, {}, {}, {}
+        xt, hp, hg, hc, hs = {}, {}, {}, {}, {}
+        y1, y0, yt, tr, o = {}, {}, {}, {}, {}
+
+        def width(g):
+            return P * GROUPS[g]
+
+        def halves(g):
+            return GROUPS[g] // 2
+
+        def scale_x(g, h):
+            if h == 0:
+                xs[g] = work.tile([P, GROUPS[g], IN], BF16, name="xs", tag="xs")
+            if h >= halves(g):
+                return
+            for a in (2 * h, 2 * h + 1):
+                nc.vector.tensor_tensor(out=xs[g][:, a, :], in0=xb[g][:, a, :].bitcast(FP8), in1=sc[:], op=ALU.mult)
+
+        def turn(rows, a0, key):
+            xt[key] = psum.tile([P, 2, 2 * P], F32, name="xt", tag="xt", bufs=2)
+            for a in (0, 1):
+                words = rows[:, a0 + a, :].bitcast(F32)
+                for u in (0, 1):
+                    nc.tensor.transpose(xt[key][:, u, a * P : (a + 1) * P], words[:, u : 2 * P : 2], ident[:])
+
+        def turn_x(g, h):
+            if h < halves(g):
+                turn(xs[g], 2 * h, (g, h))
+
+        def unload(dst, h, key):
+            cols = dst[:, 2 * P * h : 2 * P * (h + 1), :].rearrange("p r t -> p (r t)").bitcast(F32)
+            nc.scalar.copy(out=cols.rearrange("p (r u) -> p r u", u=2), in_=xt[key][:].rearrange("p u r -> p r u"))
+
+        def unload_x(g, h):
+            if h == 0:
+                xg[g] = work.tile([P, width(g), 4], BF16, name="xg", tag="xg", align_bytes=64)
+            if h < halves(g):
+                unload(xg[g], h, (g, h))
+
+        def quantize(src, codes, scales):
+            nc.vector.quantize_mx(out=codes.bitcast(FP8X4), scales=scales, in_=src.rearrange("p r t -> p (r t)"))
+
+        def quant_x(g):
+            xc[g] = work.tile([P, width(g)], U32, name="xc", tag="xc", align_bytes=64)
+            xsc[g] = work.tile([P, width(g)], U8, name="xsc", tag="xsc", align_bytes=64)
+            quantize(xg[g][:], xc[g][:], xsc[g][:])
+
+        def stage1(g, n, t):
+            acc = psum.tile([P, width(g)], F32, name="h", tag="h", bufs=2)
+            nc.tensor.matmul_mx(
+                out=acc[:],
+                lhsT=w1p[:, n, t].rearrange("p m b -> p (m b)").bitcast(FP4X4),
+                lhsT_scale=wsp[:, n, t, :],
+                rhs=xc[g][:].bitcast(FP8X4),
+                rhs_scale=xsc[g][:],
+                start=True,
+                stop=True,
+            )
+            if t == 0:
+                hp[g, n] = work.tile([P, 4, width(g)], BF16, name="hp", tag="hp", bufs=4)
+            nc.scalar.activation(out=hp[g, n][:, t, :], in_=acc[:], func=ACT.Relu, bias=b1c[:, n, t : t + 1])
+
+        def interleave(g, n):
+            hg[g, n] = work.tile([P, width(g), 4], BF16, name="hg", tag="hg", align_bytes=64)
+            nc.vector.tensor_copy(
+                out=hg[g, n][:].rearrange("p (c i) t -> p c t i", i=4),
+                in_=hp[g, n][:].rearrange("p t (c i) -> p c t i", i=4),
+            )
+
+        def quant_h(g, n):
+            hc[g, n] = work.tile([P, width(g)], U32, name="hc", tag="hc", align_bytes=64, bufs=4)
+            hs[g, n] = work.tile([P, width(g)], U8, name="hs", tag="hs", align_bytes=64, bufs=4)
+            quantize(hg[g, n][:], hc[g, n][:], hs[g, n][:])
+
+        def stage2_channels(g, t):
+            y1[g, t] = psum.tile([P, width(g)], F32, name="y", tag="y", bufs=2)
+            cols = slice(t * P, (t + 1) * P)
+            nc.tensor.matmul_mx(
+                out=y1[g, t][:],
+                lhsT=wbc[1][:, cols].bitcast(FP8X4),
+                lhsT_scale=wbs[1][:, cols],
+                rhs=hc[g, 1][:].bitcast(FP8X4),
+                rhs_scale=hs[g, 1][:],
+                start=True,
+                stop=True,
+            )
+
+        def relu_channels(g, t):
+            yt[g, t] = work.tile([P, width(g)], F32, name="yt", tag="yt", bufs=8)
+            nc.scalar.activation(out=yt[g, t][:], in_=y1[g, t][:], func=ACT.Relu, bias=bbc[:, t : t + 1])
+
+        def turn_back(g, a):
+            if a >= GROUPS[g]:
+                return
+            tr[g, a] = psum.tile([P, 4, P], F32, name="tr", tag="tr", bufs=2)
+            for t in range(4):
+                nc.tensor.transpose(tr[g, a][:, t, :], yt[g, t][:, a * P : (a + 1) * P], ident[:])
+
+        def store_turned(g, a, on_vector):
+            if a >= GROUPS[g]:
+                return
+            dst = o[g][:, a, BLK:HID].rearrange("p (r t) -> p r t", t=4)
+            src = tr[g, a][:].rearrange("p t r -> p r t")
+            if on_vector:
+                nc.vector.tensor_copy(out=dst, in_=src)
+            else:
+                nc.scalar.copy(out=dst, in_=src)
+            rows = out[first[g] : first[g] + width(g), :].rearrange("(p a) c -> p a c", a=GROUPS[g])
+            nc.sync.dma_start(out=rows[:, a, :], in_=o[g][:, a, :])
+
+        def stage2_tokens(g, a):
+            if a >= GROUPS[g]:
+                return
+            y0[g, a] = psum.tile([P, BLK], F32, name="y", tag="y", bufs=2)
+            cols = slice(a * P, (a + 1) * P)
+            nc.tensor.matmul_mx(
+                out=y0[g, a][:],
+                lhsT=hc[g, 0][:, cols].bitcast(FP8X4),
+                lhsT_scale=hs[g, 0][:, cols],
+                rhs=wbc[0][:].bitcast(FP8X4),
+                rhs_scale=wbs[0][:],
+                start=True,
+                stop=True,
+            )
+
+        def bias_tokens(g, a):
+            if a >= GROUPS[g]:
+                return
+            if a == 0:
+                o[g] = work.tile([P, GROUPS[g], HID], F32, name="o", tag="o")
+            part = o[g][:, a, 0:BLK]
+            nc.vector.tensor_tensor(out=part, in0=y0[g, a][:], in1=bbr[:], op=ALU.add)
+            if a % 2 == 1:
+                pair = o[g][:, a - 1 : a + 1, 0:BLK]
+                nc.vector.tensor_scalar(out=pair, in0=pair, scalar1=0.0, scalar2=None, op0=ALU.max)
+
+        def weights2(n):
+            wg = work.tile([P, BLK, 4], BF16, name="wg", tag="wg", align_bytes=64, bufs=2)
+            for h in (0, 1):
+                turn(wbr[n], 2 * h, ("w", n, h))
+                unload(wg, h, ("w", n, h))
+            quantize(wg[:], wbc[n][:], wbs[n][:])
+
+        def permute_w1(n):
+            nc.vector.tensor_copy(
+                out=w1p[:, n], in_=w1r[:].rearrange("p (n m t b) -> p n t m b", n=2, t=4, b=2)[:, n]
+            )
+            nc.gpsimd.tensor_copy(out=wsp[:, n], in_=wsr[:].rearrange("p (n m t) -> p n t m", n=2, t=4)[:, n])
+
+        def slot(g):
+            now, prev, nxt, far = 0 <= g < L, 0 <= g - 1 < L, 0 <= g + 1 < L, 0 <= g + 2 < L
+            if prev:
+                bias_tokens(g - 1, 0)
+            if now:
+                stage1(g, 1, 0)
+                stage1(g, 1, 1)
+            if prev:
+                stage2_tokens(g - 1, 2)
+                bias_tokens(g - 1, 1)
+            if now:
+                stage1(g, 1, 2)
+            if prev:
+                stage2_tokens(g - 1, 3)
+            if now:
+                stage1(g, 1, 3)
+            if prev:
+                bias_tokens(g - 1, 2)
+                bias_tokens(g - 1, 3)
+                turn_back(g - 1, 0)
+                turn_back(g - 1, 1)
+            if now:
+                interleave(g, 1)
+                for t in range(4):
+                    stage1(g, 0, t)
+            if prev:
+                store_turned(g - 1, 0, False)
+                store_turned(g - 1, 1, GROUPS[g - 1] == 2)
+            if far:
+                scale_x(g + 2, 0)
+            if g == -2:
+                permute_w1(1)
+                permute_w1(0)
+            if now:
+                quant_h(g, 1)
+                stage2_channels(g, 0)
+                stage2_channels(g, 1)
+                interleave(g, 0)
+            if prev:
+                turn_back(g - 1, 2)
+                turn_back(g - 1, 3)
+                store_turned(g - 1, 2, False)
+            if nxt:
+                unload_x(g + 1, 0)
+                unload_x(g + 1, 1)
+            if g == -1:
+                quant_x(0)
+                weights2(1)
+            if g == 0:
+                weights2(0)
+            if far:
+                turn_x(g + 2, 0)
+                scale_x(g + 2, 1)
+                turn_x(g + 2, 1)
+            if now:
+                relu_channels(g, 0)
+                stage2_channels(g, 2)
+                relu_channels(g, 1)
+                stage2_channels(g, 3)
+                relu_channels(g, 2)
+                relu_channels(g, 3)
+                quant_h(g, 0)
+            if prev:
+                store_turned(g - 1, 3, False)
+            if nxt and g >= 0:
+                quant_x(g + 1)
+            if now:
+                stage2_tokens(g, 0)
+                stage2_tokens(g, 1)
+
+        for g in range(-2, L + 1):
+            slot(g)

@@ -18,44 +18,44 @@ ALU = mybir.AluOpType
 ACT = mybir.ActivationFunctionType
 
 P = 128
-GROUPS = [2, 4, 4, 4, 4, 4, 4, 4, 2]
+T = 512
+GROUPS = B // T
+UNITS = 2 * GROUPS
 
 
 def tile_blockdiagmnistconvertible_pa_t_w4_kernel(tc, x_bytes, x_scale, W1_words, W1_scales, b1, Wb, bb, out):
     nc = tc.nc
-    L = len(GROUPS)
-    first = [P * sum(GROUPS[:g]) for g in range(L)]
 
     with ExitStack() as ctx:
         keep = ctx.enter_context(tc.tile_pool(name="keep", bufs=1))
         work = ctx.enter_context(tc.tile_pool(name="work", bufs=3))
-        psum = ctx.enter_context(tc.psum_pool(name="psum", bufs=2))
+        psum = ctx.enter_context(tc.psum_pool(name="psum", bufs=3))
+        ctx.enter_context(tc.manual_schedule())
 
         ident = keep.tile([P, P], F32, name="ident")
-        sc = keep.tile([P, IN], F32, name="sc")
+        sc = keep.tile([P, 4], F32, name="sc")
         w1r = keep.tile([P, 2048], U8, name="w1r")
         w1p = keep.tile([P, 2, 4, P, 2], U8, name="w1p", align_bytes=64)
         wsr = keep.tile([P, HID], U8, name="wsr", align_bytes=64)
         wsp = keep.tile([P, 2, 4, P], U8, name="wsp", align_bytes=64)
         b1c = keep.tile([P, 2, 4], BF16, name="b1c")
-        bbc = keep.tile([P, 4], BF16, name="bbc")
-        bbr = keep.tile([P, BLK], BF16, name="bbr")
-        warm = keep.tile([P, 1], F32, name="warm")
-        xb = [keep.tile([P, GROUPS[g], IN], U8, name=f"xb{g}") for g in range(L)]
+        bbr = keep.tile([P, HID], BF16, name="bbr")
+        xb = [keep.tile([P, 4, IN], U8, name=f"xb{g}") for g in range(GROUPS)]
         wbr = [keep.tile([P, 4, BLK], BF16, name=f"wbr{n}") for n in range(2)]
+        wbg = [keep.tile([P, BLK, 4], BF16, name=f"wbg{n}", align_bytes=64) for n in range(2)]
         wbc = [keep.tile([P, BLK], U32, name=f"wbc{n}", align_bytes=64) for n in range(2)]
         wbs = [keep.tile([P, BLK], U8, name=f"wbs{n}", align_bytes=64) for n in range(2)]
 
         def load_x(g):
-            src = x_bytes[first[g] : first[g] + P * GROUPS[g], :].rearrange("(p a) k -> p a k", a=GROUPS[g])
-            nc.sync.dma_start(out=xb[g][:], in_=src)
+            nc.sync.dma_start(out=xb[g][:], in_=x_bytes[T * g : T * (g + 1), :].rearrange("(p a) k -> p a k", a=4))
 
-        nc.vector.memset(warm[:], 0.0)
+        def load_wb(n):
+            nc.sync.dma_start(out=wbr[n][:], in_=Wb[n].rearrange("(a p) k -> p a k", p=P))
+
         nc.vector.memset(wsr[:].bitcast(I32), 0)
-        nc.scalar.activation(out=warm[:], in_=warm[:], func=ACT.Relu)
         make_identity(nc, ident[:])
         load_x(0)
-        nc.sync.dma_start(out=sc[:], in_=x_scale.rearrange("o k -> (o k)").partition_broadcast(P))
+        nc.sync.dma_start(out=sc[:], in_=x_scale.rearrange("o (p t) -> p (o t)", t=4))
         nc.sync.dma_start(out=w1r[:], in_=W1_words[0])
         for q in range(4):
             nc.sync.dma_start(
@@ -63,231 +63,189 @@ def tile_blockdiagmnistconvertible_pa_t_w4_kernel(tc, x_bytes, x_scale, W1_words
             )
         load_x(1)
         nc.sync.dma_start(out=b1c[:], in_=b1.rearrange("(n p t) -> p n t", n=2, t=4))
-        nc.sync.dma_start(out=wbr[1][:], in_=Wb[1].rearrange("(p t) k -> p t k", t=4))
-        nc.sync.dma_start(out=bbc[:], in_=bb[BLK:HID].rearrange("(p t) -> p t", t=4))
-        nc.sync.dma_start(out=wbr[0][:], in_=Wb[0].rearrange("(t p) k -> p t k", p=P))
-        nc.sync.dma_start(out=bbr[:], in_=bb[0:BLK].partition_broadcast(P))
-        for g in range(2, L):
+        load_wb(0)
+        load_x(2)
+        nc.sync.dma_start(out=bbr[:], in_=bb.partition_broadcast(P))
+        load_wb(1)
+        for g in range(3, GROUPS):
             load_x(g)
 
-        xs, xg, xc, xsc = {}, {}, {}, {}
-        xt, hp, hg, hc, hs = {}, {}, {}, {}, {}
-        y1, y0, yt, tr, o = {}, {}, {}, {}, {}
+        xs, xt, xg, xc, xsc = {}, {}, {}, {}, {}
+        hacc, hp, hg, hc, hs = {}, {}, {}, {}, {}
+        y, o, wt = {}, {}, {}
 
-        def width(g):
-            return P * GROUPS[g]
-
-        def halves(g):
-            return GROUPS[g] // 2
-
-        def scale_x(g, h):
-            if h == 0:
-                xs[g] = work.tile([P, GROUPS[g], IN], BF16, name="xs", tag="xs")
-            if h >= halves(g):
-                return
-            for a in (2 * h, 2 * h + 1):
-                nc.vector.tensor_tensor(out=xs[g][:, a, :], in0=xb[g][:, a, :].bitcast(FP8), in1=sc[:], op=ALU.mult)
-
-        def turn(rows, a0, key):
-            xt[key] = psum.tile([P, 2, 2 * P], F32, name="xt", tag="xt", bufs=2)
-            for a in (0, 1):
-                words = rows[:, a0 + a, :].bitcast(F32)
-                for u in (0, 1):
-                    nc.tensor.transpose(xt[key][:, u, a * P : (a + 1) * P], words[:, u : 2 * P : 2], ident[:])
-
-        def turn_x(g, h):
-            if h < halves(g):
-                turn(xs[g], 2 * h, (g, h))
-
-        def unload(dst, h, key):
-            cols = dst[:, 2 * P * h : 2 * P * (h + 1), :].rearrange("p r t -> p (r t)").bitcast(F32)
-            nc.scalar.copy(out=cols.rearrange("p (r u) -> p r u", u=2), in_=xt[key][:].rearrange("p u r -> p r u"))
-
-        def unload_x(g, h):
-            if h == 0:
-                xg[g] = work.tile([P, width(g), 4], BF16, name="xg", tag="xg", align_bytes=64)
-            if h < halves(g):
-                unload(xg[g], h, (g, h))
+        def live(u):
+            return 0 <= u < UNITS
 
         def quantize(src, codes, scales):
             nc.vector.quantize_mx(out=codes.bitcast(FP8X4), scales=scales, in_=src.rearrange("p r t -> p (r t)"))
 
-        def quant_x(g):
-            xc[g] = work.tile([P, width(g)], U32, name="xc", tag="xc", align_bytes=64)
-            xsc[g] = work.tile([P, width(g)], U8, name="xsc", tag="xsc", align_bytes=64)
-            quantize(xg[g][:], xc[g][:], xsc[g][:])
+        def turn(bank, rows):
+            for a in (0, 1):
+                words = rows[:, a, :].bitcast(F32)
+                for u in (0, 1):
+                    nc.tensor.transpose(bank[:, u, a * P : (a + 1) * P], words[:, u : 2 * P : 2], ident[:])
 
-        def stage1(g, n, t):
-            acc = psum.tile([P, width(g)], F32, name="h", tag="h", bufs=2)
-            nc.tensor.matmul_mx(
-                out=acc[:],
-                lhsT=w1p[:, n, t].rearrange("p m b -> p (m b)").bitcast(FP4X4),
-                lhsT_scale=wsp[:, n, t, :],
-                rhs=xc[g][:].bitcast(FP8X4),
-                rhs_scale=xsc[g][:],
-                start=True,
-                stop=True,
-            )
-            if t == 0:
-                hp[g, n] = work.tile([P, 4, width(g)], BF16, name="hp", tag="hp", bufs=4)
-            nc.scalar.activation(out=hp[g, n][:, t, :], in_=acc[:], func=ACT.Relu, bias=b1c[:, n, t : t + 1])
+        def widen_x(j):
+            if live(j):
+                xs[j] = work.tile([P, 2, IN], BF16, name="xs", tag="xs")
+                src = xb[j // 2][:, 2 * (j % 2) : 2 * (j % 2) + 2, :].rearrange("p a k -> p (a k)").bitcast(FP8)
+                nc.scalar.copy(out=xs[j][:].rearrange("p a k -> p (a k)"), in_=src)
 
-        def interleave(g, n):
-            hg[g, n] = work.tile([P, width(g), 4], BF16, name="hg", tag="hg", align_bytes=64)
-            nc.vector.tensor_copy(
-                out=hg[g, n][:].rearrange("p (c i) t -> p c t i", i=4),
-                in_=hp[g, n][:].rearrange("p t (c i) -> p c t i", i=4),
-            )
+        def turn_x(j):
+            if live(j):
+                xt[j] = psum.tile([P, 2, 2 * P], F32, name="xt", tag="xt", bufs=2)
+                turn(xt[j], xs[j])
 
-        def quant_h(g, n):
-            hc[g, n] = work.tile([P, width(g)], U32, name="hc", tag="hc", align_bytes=64, bufs=4)
-            hs[g, n] = work.tile([P, width(g)], U8, name="hs", tag="hs", align_bytes=64, bufs=4)
-            quantize(hg[g, n][:], hc[g, n][:], hs[g, n][:])
+        def scale_x(j):
+            if live(j):
+                g, h = divmod(j, 2)
+                if h == 0:
+                    xg[g] = work.tile([P, T, 4], BF16, name="xg", tag="xg", align_bytes=64, bufs=2)
+                nc.vector.tensor_tensor(
+                    out=xg[g][:, 2 * P * h : 2 * P * (h + 1), :].rearrange("p r (u e) -> p r u e", u=2),
+                    in0=xt[j][:].bitcast(BF16).rearrange("p u (r e) -> p r u e", e=2),
+                    in1=sc[:].rearrange("p (u e) -> p u e", u=2).unsqueeze(1).to_broadcast([P, 2 * P, 2, 2]),
+                    op=ALU.mult,
+                )
 
-        def stage2_channels(g, t):
-            y1[g, t] = psum.tile([P, width(g)], F32, name="y", tag="y", bufs=2)
-            cols = slice(t * P, (t + 1) * P)
-            nc.tensor.matmul_mx(
-                out=y1[g, t][:],
-                lhsT=wbc[1][:, cols].bitcast(FP8X4),
-                lhsT_scale=wbs[1][:, cols],
-                rhs=hc[g, 1][:].bitcast(FP8X4),
-                rhs_scale=hs[g, 1][:],
-                start=True,
-                stop=True,
-            )
+        def quant_x(j):
+            if live(j) and j % 2 == 1:
+                g = j // 2
+                xc[g] = work.tile([P, T], U32, name="xc", tag="xc", align_bytes=64)
+                xsc[g] = work.tile([P, T], U8, name="xsc", tag="xsc", align_bytes=64)
+                quantize(xg[g][:], xc[g][:], xsc[g][:])
 
-        def relu_channels(g, t):
-            yt[g, t] = work.tile([P, width(g)], F32, name="yt", tag="yt", bufs=8)
-            nc.scalar.activation(out=yt[g, t][:], in_=y1[g, t][:], func=ACT.Relu, bias=bbc[:, t : t + 1])
+        def stage1(u, t):
+            if live(u):
+                g, n = divmod(u, 2)
+                hacc[u, t] = psum.tile([P, T], F32, name="h", tag="h")
+                nc.tensor.matmul_mx(
+                    out=hacc[u, t][:],
+                    lhsT=w1p[:, n, t].rearrange("p m b -> p (m b)").bitcast(FP4X4),
+                    lhsT_scale=wsp[:, n, t, :],
+                    rhs=xc[g][:].bitcast(FP8X4),
+                    rhs_scale=xsc[g][:],
+                    start=True,
+                    stop=True,
+                )
 
-        def turn_back(g, a):
-            if a >= GROUPS[g]:
-                return
-            tr[g, a] = psum.tile([P, 4, P], F32, name="tr", tag="tr", bufs=2)
-            for t in range(4):
-                nc.tensor.transpose(tr[g, a][:, t, :], yt[g, t][:, a * P : (a + 1) * P], ident[:])
+        def relu_h(u, t):
+            if live(u):
+                if t == 0:
+                    hp[u] = work.tile([P, 4, T], BF16, name="hp", tag="hp")
+                nc.scalar.activation(out=hp[u][:, t, :], in_=hacc[u, t][:], func=ACT.Relu, bias=b1c[:, u % 2, t : t + 1])
 
-        def store_turned(g, a, on_vector):
-            if a >= GROUPS[g]:
-                return
-            dst = o[g][:, a, BLK:HID].rearrange("p (r t) -> p r t", t=4)
-            src = tr[g, a][:].rearrange("p t r -> p r t")
-            if on_vector:
-                nc.vector.tensor_copy(out=dst, in_=src)
-            else:
-                nc.scalar.copy(out=dst, in_=src)
-            rows = out[first[g] : first[g] + width(g), :].rearrange("(p a) c -> p a c", a=GROUPS[g])
-            nc.sync.dma_start(out=rows[:, a, :], in_=o[g][:, a, :])
+        def interleave(u):
+            if live(u):
+                hg[u] = work.tile([P, T, 4], BF16, name="hg", tag="hg", align_bytes=64, bufs=1)
+                if u == 0:
+                    nc.vector.tensor_copy(
+                        out=hg[u][:].rearrange("p (c i) t -> p c t i", i=4),
+                        in_=hp[u][:].rearrange("p t (c i) -> p c t i", i=4),
+                    )
+                else:
+                    nc.gpsimd.tensor_scalar(
+                        out=hg[u][:],
+                        in0=hp[u][:].rearrange("p t r -> p r t"),
+                        scalar1=1.0,
+                        scalar2=0.0,
+                        op0=ALU.mult,
+                        op1=ALU.add,
+                    )
 
-        def stage2_tokens(g, a):
-            if a >= GROUPS[g]:
-                return
-            y0[g, a] = psum.tile([P, BLK], F32, name="y", tag="y", bufs=2)
-            cols = slice(a * P, (a + 1) * P)
-            nc.tensor.matmul_mx(
-                out=y0[g, a][:],
-                lhsT=hc[g, 0][:, cols].bitcast(FP8X4),
-                lhsT_scale=hs[g, 0][:, cols],
-                rhs=wbc[0][:].bitcast(FP8X4),
-                rhs_scale=wbs[0][:],
-                start=True,
-                stop=True,
-            )
+        def quant_h(u):
+            if live(u):
+                hc[u] = work.tile([P, T], U32, name="hc", tag="hc", align_bytes=64, bufs=2)
+                hs[u] = work.tile([P, T], U8, name="hs", tag="hs", align_bytes=64, bufs=2)
+                quantize(hg[u][:], hc[u][:], hs[u][:])
 
-        def bias_tokens(g, a):
-            if a >= GROUPS[g]:
-                return
-            if a == 0:
-                o[g] = work.tile([P, GROUPS[g], HID], F32, name="o", tag="o")
-            part = o[g][:, a, 0:BLK]
-            nc.vector.tensor_tensor(out=part, in0=y0[g, a][:], in1=bbr[:], op=ALU.add)
-            if a % 2 == 1:
-                pair = o[g][:, a - 1 : a + 1, 0:BLK]
-                nc.vector.tensor_scalar(out=pair, in0=pair, scalar1=0.0, scalar2=None, op0=ALU.max)
+        def stage2(u, a):
+            if live(u):
+                n = u % 2
+                y[u, a] = psum.tile([P, BLK], F32, name="y", tag="y")
+                cols = slice(a * P, (a + 1) * P)
+                nc.tensor.matmul_mx(
+                    out=y[u, a][:],
+                    lhsT=hc[u][:, cols].bitcast(FP8X4),
+                    lhsT_scale=hs[u][:, cols],
+                    rhs=wbc[n][:].bitcast(FP8X4),
+                    rhs_scale=wbs[n][:],
+                    start=True,
+                    stop=True,
+                )
 
-        def weights2(n):
-            wg = work.tile([P, BLK, 4], BF16, name="wg", tag="wg", align_bytes=64, bufs=2)
-            for h in (0, 1):
-                turn(wbr[n], 2 * h, ("w", n, h))
-                unload(wg, h, ("w", n, h))
-            quantize(wg[:], wbc[n][:], wbs[n][:])
+        def bias_y(u, a):
+            if live(u):
+                n = u % 2
+                if a == 0:
+                    o[u] = work.tile([P, 4, BLK], F32, name="o", tag="o", bufs=4)
+                nc.vector.tensor_tensor(out=o[u][:, a, :], in0=y[u, a][:], in1=bbr[:, n * BLK : (n + 1) * BLK], op=ALU.add)
+
+        def relu_y_vector(u):
+            if live(u):
+                part = o[u][:, 0, :]
+                nc.vector.tensor_scalar(out=part, in0=part, scalar1=0.0, scalar2=None, op0=ALU.max)
+
+        def relu_y_scalar(u):
+            if live(u):
+                part = o[u][:, 1:4, :]
+                nc.scalar.activation(out=part, in_=part, func=ACT.Relu)
+
+        def store(u):
+            if live(u):
+                g, n = divmod(u, 2)
+                rows = out[T * g : T * (g + 1), n * BLK : (n + 1) * BLK].rearrange("(p a) c -> p a c", a=4)
+                nc.sync.dma_start(out=rows, in_=o[u][:])
 
         def permute_w1(n):
             nc.vector.tensor_copy(
                 out=w1p[:, n], in_=w1r[:].rearrange("p (n m t b) -> p n t m b", n=2, t=4, b=2)[:, n]
             )
-            nc.gpsimd.tensor_copy(out=wsp[:, n], in_=wsr[:].rearrange("p (n m t) -> p n t m", n=2, t=4)[:, n])
+            nc.vector.tensor_copy(out=wsp[:, n], in_=wsr[:].rearrange("p (n m t) -> p n t m", n=2, t=4)[:, n])
 
-        def slot(g):
-            now, prev, nxt, far = 0 <= g < L, 0 <= g - 1 < L, 0 <= g + 1 < L, 0 <= g + 2 < L
-            if prev:
-                bias_tokens(g - 1, 0)
-            if now:
-                stage1(g, 1, 0)
-                stage1(g, 1, 1)
-            if prev:
-                stage2_tokens(g - 1, 2)
-                bias_tokens(g - 1, 1)
-            if now:
-                stage1(g, 1, 2)
-            if prev:
-                stage2_tokens(g - 1, 3)
-            if now:
-                stage1(g, 1, 3)
-            if prev:
-                bias_tokens(g - 1, 2)
-                bias_tokens(g - 1, 3)
-                turn_back(g - 1, 0)
-                turn_back(g - 1, 1)
-            if now:
-                interleave(g, 1)
-                for t in range(4):
-                    stage1(g, 0, t)
-            if prev:
-                store_turned(g - 1, 0, False)
-                store_turned(g - 1, 1, GROUPS[g - 1] == 2)
-            if far:
-                scale_x(g + 2, 0)
-            if g == -2:
-                permute_w1(1)
+        def turn_wb(n):
+            for h in (0, 1):
+                wt[n, h] = psum.tile([P, 2, 2 * P], F32, name="wt", tag="y")
+                turn(wt[n, h], wbr[n][:, 2 * h : 2 * h + 2, :])
+                cols = wbg[n][:, 2 * P * h : 2 * P * (h + 1), :].rearrange("p r t -> p (r t)").bitcast(F32)
+                nc.scalar.copy(out=cols.rearrange("p (r u) -> p r u", u=2), in_=wt[n, h][:].rearrange("p u r -> p r u"))
+
+        def slot(s):
+            if s + 1 > 0:
+                interleave(s + 1)
+            for a in range(3):
+                stage2(s, a)
+            scale_x(s + 5)
+            relu_h(s + 2, 0)
+            stage1(s + 2, 3)
+            for t in range(1, 4):
+                relu_h(s + 2, t)
+            bias_y(s, 0)
+            stage2(s, 3)
+            for a in range(1, 4):
+                bias_y(s, a)
+            turn_x(s + 6)
+            if s == -6:
                 permute_w1(0)
-            if now:
-                quant_h(g, 1)
-                stage2_channels(g, 0)
-                stage2_channels(g, 1)
-                interleave(g, 0)
-            if prev:
-                turn_back(g - 1, 2)
-                turn_back(g - 1, 3)
-                store_turned(g - 1, 2, False)
-            if nxt:
-                unload_x(g + 1, 0)
-                unload_x(g + 1, 1)
-            if g == -1:
-                quant_x(0)
-                weights2(1)
-            if g == 0:
-                weights2(0)
-            if far:
-                turn_x(g + 2, 0)
-                scale_x(g + 2, 1)
-                turn_x(g + 2, 1)
-            if now:
-                relu_channels(g, 0)
-                stage2_channels(g, 2)
-                relu_channels(g, 1)
-                stage2_channels(g, 3)
-                relu_channels(g, 2)
-                relu_channels(g, 3)
-                quant_h(g, 0)
-            if prev:
-                store_turned(g - 1, 3, False)
-            if nxt and g >= 0:
-                quant_x(g + 1)
-            if now:
-                stage2_tokens(g, 0)
-                stage2_tokens(g, 1)
+            if s == -4:
+                turn_wb(0)
+            if s == -1:
+                turn_wb(1)
+            for t in range(3):
+                stage1(s + 3, t)
+            relu_y_scalar(s - 1)
+            store(s - 1)
+            widen_x(s + 7)
+            relu_y_vector(s)
+            quant_x(s + 5)
+            if s == -4:
+                permute_w1(1)
+            if s in (-2, 0):
+                quantize(wbg[s // 2 + 1][:], wbc[s // 2 + 1][:], wbs[s // 2 + 1][:])
+            if s + 1 == 0:
+                interleave(0)
+            quant_h(s + 1)
 
-        for g in range(-2, L + 1):
-            slot(g)
+        for s in range(-7, UNITS + 1):
+            slot(s)

@@ -57,16 +57,16 @@ def tile_blockdiagmnistconvertible_pa_t_w4_kernel(tc, x_bytes, x_scale, W1_words
         load_x(0)
         nc.sync.dma_start(out=sc[:], in_=x_scale.rearrange("o (p t) -> p (o t)", t=4))
         nc.sync.dma_start(out=w1r[:], in_=W1_words[0])
+        load_x(1)
         for q in range(4):
             nc.sync.dma_start(
                 out=wsr[32 * q : 32 * q + 4, :].bitcast(I32), in_=W1_scales[0, 4 * q : 4 * q + 4, :].bitcast(I32)
             )
-        load_x(1)
-        nc.sync.dma_start(out=b1c[:], in_=b1.rearrange("(n p t) -> p n t", n=2, t=4))
-        load_wb(0)
         load_x(2)
-        nc.sync.dma_start(out=bbr[:], in_=bb.partition_broadcast(P))
+        load_wb(0)
+        nc.sync.dma_start(out=b1c[:], in_=b1.rearrange("(n p t) -> p n t", n=2, t=4))
         load_wb(1)
+        nc.sync.dma_start(out=bbr[:], in_=bb.partition_broadcast(P))
         for g in range(3, GROUPS):
             load_x(g)
 
@@ -88,13 +88,20 @@ def tile_blockdiagmnistconvertible_pa_t_w4_kernel(tc, x_bytes, x_scale, W1_words
 
         def widen_x(j):
             if live(j):
-                xs[j] = work.tile([P, 2, IN], BF16, name="xs", tag="xs")
+                xs[j] = work.tile([P, 2, IN], BF16, name="xs", tag="xs", bufs=4)
                 src = xb[j // 2][:, 2 * (j % 2) : 2 * (j % 2) + 2, :].rearrange("p a k -> p (a k)").bitcast(FP8)
-                nc.scalar.copy(out=xs[j][:].rearrange("p a k -> p (a k)"), in_=src)
+                dst = xs[j][:].rearrange("p a k -> p (a k)")
+                if j == 0:
+                    nc.vector.tensor_copy(out=dst, in_=src)
+                else:
+                    nc.scalar.copy(out=dst, in_=src)
 
-        def turn_x(j):
+        def bank(tag):
+            return psum.tile([P, 2, 2 * P], F32, name="bank", tag=tag, bufs=1 if tag == "xt" else 3)
+
+        def turn_x(j, tag="xt"):
             if live(j):
-                xt[j] = psum.tile([P, 2, 2 * P], F32, name="xt", tag="xt", bufs=2)
+                xt[j] = bank(tag)
                 turn(xt[j], xs[j])
 
         def scale_x(j):
@@ -119,7 +126,7 @@ def tile_blockdiagmnistconvertible_pa_t_w4_kernel(tc, x_bytes, x_scale, W1_words
         def stage1(u, t):
             if live(u):
                 g, n = divmod(u, 2)
-                hacc[u, t] = psum.tile([P, T], F32, name="h", tag="h")
+                hacc[u, t] = psum.tile([P, T], F32, name="h", tag="h", bufs=4)
                 nc.tensor.matmul_mx(
                     out=hacc[u, t][:],
                     lhsT=w1p[:, n, t].rearrange("p m b -> p (m b)").bitcast(FP4X4),
@@ -136,23 +143,32 @@ def tile_blockdiagmnistconvertible_pa_t_w4_kernel(tc, x_bytes, x_scale, W1_words
                     hp[u] = work.tile([P, 4, T], BF16, name="hp", tag="hp")
                 nc.scalar.activation(out=hp[u][:, t, :], in_=hacc[u, t][:], func=ACT.Relu, bias=b1c[:, u % 2, t : t + 1])
 
-        def interleave(u):
+        def gpsimd_tokens(u):
+            if u == 0:
+                return 0
+            return T if u + 4 < UNITS else 3 * P
+
+        def interleave_gpsimd(u):
             if live(u):
                 hg[u] = work.tile([P, T, 4], BF16, name="hg", tag="hg", align_bytes=64, bufs=1)
-                if u == 0:
-                    nc.vector.tensor_copy(
-                        out=hg[u][:].rearrange("p (c i) t -> p c t i", i=4),
-                        in_=hp[u][:].rearrange("p t (c i) -> p c t i", i=4),
-                    )
-                else:
+                cut = gpsimd_tokens(u)
+                if cut > 0:
                     nc.gpsimd.tensor_scalar(
-                        out=hg[u][:],
-                        in0=hp[u][:].rearrange("p t r -> p r t"),
+                        out=hg[u][:, :cut, :],
+                        in0=hp[u][:, :, :cut].rearrange("p t r -> p r t"),
                         scalar1=1.0,
                         scalar2=0.0,
                         op0=ALU.mult,
                         op1=ALU.add,
                     )
+
+        def interleave_vector(u):
+            if live(u) and gpsimd_tokens(u) < T:
+                cut = gpsimd_tokens(u)
+                nc.vector.tensor_copy(
+                    out=hg[u][:, cut:, :].rearrange("p (c i) t -> p c t i", i=4),
+                    in_=hp[u][:, :, cut:].rearrange("p t (c i) -> p c t i", i=4),
+                )
 
         def quant_h(u):
             if live(u):
@@ -182,70 +198,165 @@ def tile_blockdiagmnistconvertible_pa_t_w4_kernel(tc, x_bytes, x_scale, W1_words
                     o[u] = work.tile([P, 4, BLK], F32, name="o", tag="o", bufs=4)
                 nc.vector.tensor_tensor(out=o[u][:, a, :], in0=y[u, a][:], in1=bbr[:, n * BLK : (n + 1) * BLK], op=ALU.add)
 
-        def relu_y_vector(u):
-            if live(u):
-                part = o[u][:, 0, :]
-                nc.vector.tensor_scalar(out=part, in0=part, scalar1=0.0, scalar2=None, op0=ALU.max)
+        def rows_of(u):
+            g, n = divmod(u, 2)
+            return out[T * g : T * (g + 1), n * BLK : (n + 1) * BLK].rearrange("(p a) c -> p a c", a=4)
 
-        def relu_y_scalar(u):
-            if live(u):
-                part = o[u][:, 1:4, :]
-                nc.scalar.activation(out=part, in_=part, func=ACT.Relu)
+        def relu_y_vector(u, a0, a1):
+            part = o[u][:, a0:a1, :]
+            nc.vector.tensor_scalar(out=part, in0=part, scalar1=0.0, scalar2=None, op0=ALU.max)
 
-        def store(u):
-            if live(u):
-                g, n = divmod(u, 2)
-                rows = out[T * g : T * (g + 1), n * BLK : (n + 1) * BLK].rearrange("(p a) c -> p a c", a=4)
-                nc.sync.dma_start(out=rows, in_=o[u][:])
+        def relu_y_scalar(u, a0, a1):
+            part = o[u][:, a0:a1, :]
+            nc.scalar.activation(out=part, in_=part, func=ACT.Relu)
 
-        def permute_w1(n):
+        def store(u, a0, a1):
+            nc.sync.dma_start(out=rows_of(u)[:, a0:a1, :], in_=o[u][:, a0:a1, :])
+
+        def permute_words(n):
             nc.vector.tensor_copy(
                 out=w1p[:, n], in_=w1r[:].rearrange("p (n m t b) -> p n t m b", n=2, t=4, b=2)[:, n]
             )
+
+        def permute_scales(n):
             nc.vector.tensor_copy(out=wsp[:, n], in_=wsr[:].rearrange("p (n m t) -> p n t m", n=2, t=4)[:, n])
 
-        def turn_wb(n):
-            for h in (0, 1):
-                wt[n, h] = psum.tile([P, 2, 2 * P], F32, name="wt", tag="y")
-                turn(wt[n, h], wbr[n][:, 2 * h : 2 * h + 2, :])
-                cols = wbg[n][:, 2 * P * h : 2 * P * (h + 1), :].rearrange("p r t -> p (r t)").bitcast(F32)
-                nc.scalar.copy(out=cols.rearrange("p (r u) -> p r u", u=2), in_=wt[n, h][:].rearrange("p u r -> p r u"))
+        def turn_wb(n, h, tag):
+            wt[n, h] = bank(tag)
+            turn(wt[n, h], wbr[n][:, 2 * h : 2 * h + 2, :])
+
+        def unload_wb(n, h, copy):
+            cols = wbg[n][:, 2 * P * h : 2 * P * (h + 1), :].rearrange("p r t -> p (r t)").bitcast(F32)
+            copy(out=cols.rearrange("p (r u) -> p r u", u=2), in_=wt[n, h][:].rearrange("p u r -> p r u"))
+
+        def quant_wb(n):
+            quantize(wbg[n][:], wbc[n][:], wbs[n][:])
+
+        widen_x(0)
+        widen_x(1)
+        turn_x(0)
+        turn_x(1, "y")
+        permute_words(0)
+        permute_words(1)
+        widen_x(2)
+        widen_x(3)
+        turn_x(2, "y")
+        turn_x(3, "y")
+        scale_x(0)
+        scale_x(1)
+        permute_scales(0)
+        quant_x(1)
+        permute_scales(1)
+        widen_x(4)
+        widen_x(5)
+        for t in range(4):
+            stage1(0, t)
+        scale_x(2)
+        scale_x(3)
+        quant_x(3)
+        turn_wb(0, 0, "xt")
+        for t in range(4):
+            relu_h(0, t)
+        unload_wb(0, 0, nc.scalar.copy)
+        stage1(1, 0)
+        stage1(1, 1)
+        turn_wb(0, 1, "y")
+        stage1(1, 2)
+        stage1(1, 3)
+        turn_x(4, "y")
+        turn_x(5, "y")
+        relu_h(1, 0)
+        relu_h(1, 1)
+        unload_wb(0, 1, nc.scalar.copy)
+        relu_h(1, 2)
+        relu_h(1, 3)
+        interleave_gpsimd(0)
+        interleave_vector(0)
+        quant_h(0)
+        quant_wb(0)
+        scale_x(4)
+        widen_x(6)
+
+        interleave_gpsimd(1)
+        stage2(0, 0)
+        stage1(2, 0)
+        stage1(2, 1)
+        turn_wb(1, 0, "xt")
+        stage2(0, 1)
+        stage1(2, 2)
+        stage1(2, 3)
+        unload_wb(1, 0, nc.scalar.copy)
+        bias_y(0, 0)
+        scale_x(5)
+        bias_y(0, 1)
+        turn_wb(1, 1, "xt")
+        stage2(0, 2)
+        stage2(0, 3)
+        relu_h(2, 0)
+        relu_h(2, 1)
+        unload_wb(1, 1, nc.scalar.copy)
+        relu_h(2, 2)
+        relu_h(2, 3)
+        stage1(3, 0)
+        stage1(3, 1)
+        turn_x(6)
+        stage1(3, 2)
+        stage1(3, 3)
+        widen_x(7)
+        relu_y_vector(0, 0, 1)
+        store(0, 0, 1)
+        quant_x(5)
+        quant_wb(1)
+        quant_h(1)
+
+        def vector_tiles(u):
+            return 1 if live(u + 5) else 2
+
+        def finish(u, a):
+            relu_y_scalar(u, a, a + 1)
+            store(u, a, a + 1)
 
         def slot(s):
-            if s + 1 > 0:
-                interleave(s + 1)
-            for a in range(3):
-                stage2(s, a)
+            draining = not live(s + 2)
+            interleave_gpsimd(s + 1)
+            stage2(s, 0)
+            bias_y(s - 1, 2)
+            stage2(s, 1)
+            bias_y(s - 1, 3)
+            stage2(s, 2)
             scale_x(s + 5)
-            relu_h(s + 2, 0)
-            stage1(s + 2, 3)
-            for t in range(1, 4):
+            for t in range(4):
                 relu_h(s + 2, t)
+            if draining:
+                finish(s - 1, 2)
+                finish(s - 1, 3)
+            else:
+                relu_y_scalar(s - 1, vector_tiles(s - 1), 4)
+                store(s - 1, vector_tiles(s - 1), 4)
+            stage1(s + 3, 0)
+            stage1(s + 3, 1)
+            turn_x(s + 6)
+            widen_x(s + 7)
             bias_y(s, 0)
             stage2(s, 3)
-            for a in range(1, 4):
-                bias_y(s, a)
-            turn_x(s + 6)
-            if s == -6:
-                permute_w1(0)
-            if s == -4:
-                turn_wb(0)
-            if s == -1:
-                turn_wb(1)
-            for t in range(3):
-                stage1(s + 3, t)
-            relu_y_scalar(s - 1)
-            store(s - 1)
-            widen_x(s + 7)
-            relu_y_vector(s)
+            stage1(s + 3, 2)
+            stage1(s + 3, 3)
+            bias_y(s, 1)
+            interleave_vector(s + 1)
+            if draining:
+                finish(s, 0)
+                finish(s, 1)
+            else:
+                relu_y_vector(s, 0, vector_tiles(s))
+                store(s, 0, vector_tiles(s))
             quant_x(s + 5)
-            if s == -4:
-                permute_w1(1)
-            if s in (-2, 0):
-                quantize(wbg[s // 2 + 1][:], wbc[s // 2 + 1][:], wbs[s // 2 + 1][:])
-            if s + 1 == 0:
-                interleave(0)
             quant_h(s + 1)
 
-        for s in range(-7, UNITS + 1):
+        for s in range(1, UNITS):
             slot(s)
+        last = UNITS - 1
+        bias_y(last, 2)
+        finish(last, 2)
+        bias_y(last, 3)
+        relu_y_vector(last, 3, 4)
+        store(last, 3, 4)

@@ -21,6 +21,7 @@ P = 128
 T = 512
 GROUPS = B // T
 UNITS = 2 * GROUPS
+LEAD = 6
 
 
 def tile_blockdiagmnistconvertible_pa_t_w4_kernel(tc, x_bytes, x_scale, W1_words, W1_scales, b1, Wb, bb, out):
@@ -57,21 +58,22 @@ def tile_blockdiagmnistconvertible_pa_t_w4_kernel(tc, x_bytes, x_scale, W1_words
         load_x(0)
         nc.sync.dma_start(out=sc[:], in_=x_scale.rearrange("o (p t) -> p (o t)", t=4))
         nc.sync.dma_start(out=w1r[:], in_=W1_words[0])
-        load_x(1)
         for q in range(4):
             nc.sync.dma_start(
                 out=wsr[32 * q : 32 * q + 4, :].bitcast(I32), in_=W1_scales[0, 4 * q : 4 * q + 4, :].bitcast(I32)
             )
-        load_x(2)
+        load_x(1)
         load_wb(0)
+        load_x(2)
         nc.sync.dma_start(out=b1c[:], in_=b1.rearrange("(n p t) -> p n t", n=2, t=4))
+        load_x(3)
         load_wb(1)
         nc.sync.dma_start(out=bbr[:], in_=bb.partition_broadcast(P))
-        for g in range(3, GROUPS):
+        for g in range(4, GROUPS):
             load_x(g)
 
         xs, xt, xg, xc, xsc = {}, {}, {}, {}, {}
-        hacc, hp, hg, hc, hs = {}, {}, {}, {}, {}
+        hacc, hp, hg, hv, hc, hs = {}, {}, {}, {}, {}, {}
         y, o, wt = {}, {}, {}
 
         def live(u):
@@ -88,13 +90,10 @@ def tile_blockdiagmnistconvertible_pa_t_w4_kernel(tc, x_bytes, x_scale, W1_words
 
         def widen_x(j):
             if live(j):
-                xs[j] = work.tile([P, 2, IN], BF16, name="xs", tag="xs", bufs=4)
+                xs[j] = work.tile([P, 2, IN], BF16, name="xs", tag="xs", bufs=6)
                 src = xb[j // 2][:, 2 * (j % 2) : 2 * (j % 2) + 2, :].rearrange("p a k -> p (a k)").bitcast(FP8)
                 dst = xs[j][:].rearrange("p a k -> p (a k)")
-                if j == 0:
-                    nc.vector.tensor_copy(out=dst, in_=src)
-                else:
-                    nc.scalar.copy(out=dst, in_=src)
+                nc.scalar.copy(out=dst, in_=src)
 
         def bank(tag):
             return psum.tile([P, 2, 2 * P], F32, name="bank", tag=tag, bufs=1 if tag == "xt" else 3)
@@ -116,12 +115,14 @@ def tile_blockdiagmnistconvertible_pa_t_w4_kernel(tc, x_bytes, x_scale, W1_words
                     op=ALU.mult,
                 )
 
-        def quant_x(j):
-            if live(j) and j % 2 == 1:
-                g = j // 2
-                xc[g] = work.tile([P, T], U32, name="xc", tag="xc", align_bytes=64)
-                xsc[g] = work.tile([P, T], U8, name="xsc", tag="xsc", align_bytes=64)
-                quantize(xg[g][:], xc[g][:], xsc[g][:])
+        def quant_x(j, halves=1):
+            if live(j):
+                g, h = divmod(j, 2)
+                if h == 0:
+                    xc[g] = work.tile([P, T], U32, name="xc", tag="xc", align_bytes=64, bufs=4)
+                    xsc[g] = work.tile([P, T], U8, name="xsc", tag="xsc", align_bytes=64, bufs=4)
+                cols = slice(2 * P * h, 2 * P * (h + halves))
+                quantize(xg[g][:, cols, :], xc[g][:, cols], xsc[g][:, cols])
 
         def stage1(u, t):
             if live(u):
@@ -145,36 +146,39 @@ def tile_blockdiagmnistconvertible_pa_t_w4_kernel(tc, x_bytes, x_scale, W1_words
 
         def gpsimd_tokens(u):
             if u == 0:
-                return 0
-            return T if u + 4 < UNITS else 3 * P
+                return 2 * P
+            return T if live(u + LEAD - 1) else 3 * P
 
         def interleave_gpsimd(u):
             if live(u):
-                hg[u] = work.tile([P, T, 4], BF16, name="hg", tag="hg", align_bytes=64, bufs=1)
                 cut = gpsimd_tokens(u)
-                if cut > 0:
-                    nc.gpsimd.tensor_scalar(
-                        out=hg[u][:, :cut, :],
-                        in0=hp[u][:, :, :cut].rearrange("p t r -> p r t"),
-                        scalar1=1.0,
-                        scalar2=0.0,
-                        op0=ALU.mult,
-                        op1=ALU.add,
-                    )
+                hg[u] = work.tile([P, cut, 4], BF16, name="hg", tag="hg", align_bytes=64, bufs=1)
+                nc.gpsimd.tensor_scalar(
+                    out=hg[u][:],
+                    in0=hp[u][:, :, :cut].rearrange("p t r -> p r t"),
+                    scalar1=1.0,
+                    scalar2=0.0,
+                    op0=ALU.mult,
+                    op1=ALU.add,
+                )
 
         def interleave_vector(u):
             if live(u) and gpsimd_tokens(u) < T:
                 cut = gpsimd_tokens(u)
+                hv[u] = work.tile([P, T - cut, 4], BF16, name="hv", tag="hv", align_bytes=64, bufs=2)
                 nc.vector.tensor_copy(
-                    out=hg[u][:, cut:, :].rearrange("p (c i) t -> p c t i", i=4),
+                    out=hv[u][:].rearrange("p (c i) t -> p c t i", i=4),
                     in_=hp[u][:, :, cut:].rearrange("p t (c i) -> p c t i", i=4),
                 )
 
         def quant_h(u):
             if live(u):
+                cut = gpsimd_tokens(u)
                 hc[u] = work.tile([P, T], U32, name="hc", tag="hc", align_bytes=64, bufs=2)
                 hs[u] = work.tile([P, T], U8, name="hs", tag="hs", align_bytes=64, bufs=2)
-                quantize(hg[u][:], hc[u][:], hs[u][:])
+                quantize(hg[u][:], hc[u][:, :cut], hs[u][:, :cut])
+                if cut < T:
+                    quantize(hv[u][:], hc[u][:, cut:], hs[u][:, cut:])
 
         def stage2(u, a):
             if live(u):
@@ -202,8 +206,8 @@ def tile_blockdiagmnistconvertible_pa_t_w4_kernel(tc, x_bytes, x_scale, W1_words
             g, n = divmod(u, 2)
             return out[T * g : T * (g + 1), n * BLK : (n + 1) * BLK].rearrange("(p a) c -> p a c", a=4)
 
-        def relu_y_vector(u, a0, a1):
-            part = o[u][:, a0:a1, :]
+        def relu_y_vector(u, a):
+            part = o[u][:, a, :]
             nc.vector.tensor_scalar(out=part, in0=part, scalar1=0.0, scalar2=None, op0=ALU.max)
 
         def relu_y_scalar(u, a0, a1):
@@ -245,72 +249,44 @@ def tile_blockdiagmnistconvertible_pa_t_w4_kernel(tc, x_bytes, x_scale, W1_words
         scale_x(0)
         scale_x(1)
         permute_scales(0)
-        quant_x(1)
+        quant_x(0, 2)
         permute_scales(1)
         widen_x(4)
         widen_x(5)
+        widen_x(6)
+        turn_wb(0, 0, "xt")
+        unload_wb(0, 0, nc.scalar.copy)
         for t in range(4):
             stage1(0, t)
         scale_x(2)
         scale_x(3)
-        quant_x(3)
-        turn_wb(0, 0, "xt")
+        quant_x(2, 2)
+        turn_x(4, "y")
+        turn_wb(0, 1, "xt")
         for t in range(4):
             relu_h(0, t)
-        unload_wb(0, 0, nc.scalar.copy)
         stage1(1, 0)
         stage1(1, 1)
-        turn_wb(0, 1, "y")
+        turn_x(5, "y")
         stage1(1, 2)
         stage1(1, 3)
-        turn_x(4, "y")
-        turn_x(5, "y")
-        relu_h(1, 0)
-        relu_h(1, 1)
         unload_wb(0, 1, nc.scalar.copy)
-        relu_h(1, 2)
-        relu_h(1, 3)
-        interleave_gpsimd(0)
-        interleave_vector(0)
-        quant_h(0)
-        quant_wb(0)
-        scale_x(4)
-        widen_x(6)
-
-        interleave_gpsimd(1)
-        stage2(0, 0)
-        stage1(2, 0)
-        stage1(2, 1)
         turn_wb(1, 0, "xt")
-        stage2(0, 1)
-        stage1(2, 2)
-        stage1(2, 3)
-        unload_wb(1, 0, nc.scalar.copy)
-        bias_y(0, 0)
+        turn_wb(1, 1, "y")
+        for t in range(4):
+            relu_h(1, t)
+            stage1(2, t)
+        interleave_gpsimd(0)
+        scale_x(4)
         scale_x(5)
-        bias_y(0, 1)
-        turn_wb(1, 1, "xt")
-        stage2(0, 2)
-        stage2(0, 3)
-        relu_h(2, 0)
-        relu_h(2, 1)
+        interleave_vector(0)
+        quant_wb(0)
+        quant_h(0)
+        quant_x(4, 2)
+        unload_wb(1, 0, nc.scalar.copy)
         unload_wb(1, 1, nc.scalar.copy)
-        relu_h(2, 2)
-        relu_h(2, 3)
-        stage1(3, 0)
-        stage1(3, 1)
         turn_x(6)
-        stage1(3, 2)
-        stage1(3, 3)
         widen_x(7)
-        relu_y_vector(0, 0, 1)
-        store(0, 0, 1)
-        quant_x(5)
-        quant_wb(1)
-        quant_h(1)
-
-        def vector_tiles(u):
-            return 1 if live(u + 5) else 2
 
         def finish(u, a):
             relu_y_scalar(u, a, a + 1)
@@ -324,39 +300,41 @@ def tile_blockdiagmnistconvertible_pa_t_w4_kernel(tc, x_bytes, x_scale, W1_words
             stage2(s, 1)
             bias_y(s - 1, 3)
             stage2(s, 2)
-            scale_x(s + 5)
+            scale_x(s + LEAD)
             for t in range(4):
                 relu_h(s + 2, t)
-            if draining:
-                finish(s - 1, 2)
-                finish(s - 1, 3)
-            else:
-                relu_y_scalar(s - 1, vector_tiles(s - 1), 4)
-                store(s - 1, vector_tiles(s - 1), 4)
+            if not live(s + LEAD):
+                for a in range(2 if s == UNITS - 1 else 1, 4):
+                    finish(s - 1, a)
+            elif s > 0:
+                relu_y_scalar(s - 1, 1, 4)
+                store(s - 1, 1, 4)
             stage1(s + 3, 0)
             stage1(s + 3, 1)
-            turn_x(s + 6)
-            widen_x(s + 7)
+            turn_x(s + LEAD + 1)
+            widen_x(s + LEAD + 2)
             bias_y(s, 0)
             stage2(s, 3)
             stage1(s + 3, 2)
             stage1(s + 3, 3)
             bias_y(s, 1)
-            interleave_vector(s + 1)
             if draining:
                 finish(s, 0)
                 finish(s, 1)
             else:
-                relu_y_vector(s, 0, vector_tiles(s))
-                store(s, 0, vector_tiles(s))
-            quant_x(s + 5)
+                relu_y_vector(s, 0)
+                store(s, 0, 1)
             quant_h(s + 1)
+            quant_x(s + LEAD)
+            if s == 0:
+                quant_wb(1)
+            interleave_vector(s + 2)
 
-        for s in range(1, UNITS):
+        for s in range(UNITS):
             slot(s)
         last = UNITS - 1
         bias_y(last, 2)
         finish(last, 2)
         bias_y(last, 3)
-        relu_y_vector(last, 3, 4)
+        relu_y_vector(last, 3)
         store(last, 3, 4)

@@ -236,16 +236,26 @@ def tile_blockdiagmnistconvertible_pa_t_w4_kernel(tc, x_bytes, x_scale, W1_words
         def quant_wb(n):
             quantize(wbg[n][:], wbc[n][:], wbs[n][:])
 
+        def warm():
+            idle = psum.tile([P, 2, P], F32, name="idle", tag="h", bufs=4)
+            nc.tensor.matmul(
+                out=idle[:], lhsT=ident[:], rhs=ident[:].unsqueeze(1).to_broadcast([P, 2, P]), start=True, stop=True
+            )
+
+        warm()
+        warm()
         widen_x(0)
         widen_x(1)
         turn_x(0)
         turn_x(1, "y")
+        warm()
         permute_words(0)
         permute_words(1)
         widen_x(2)
         widen_x(3)
         turn_x(2, "y")
         turn_x(3, "y")
+        warm()
         scale_x(0)
         scale_x(1)
         permute_scales(0)

@@ -22,6 +22,7 @@ T = 512
 GROUPS = B // T
 UNITS = 2 * GROUPS
 LEAD = 6
+FULL_SLOTS = 4
 
 
 def tile_blockdiagmnistconvertible_pa_t_w4_kernel(tc, x_bytes, x_scale, W1_words, W1_scales, b1, Wb, bb, out):
@@ -145,9 +146,7 @@ def tile_blockdiagmnistconvertible_pa_t_w4_kernel(tc, x_bytes, x_scale, W1_words
                 nc.scalar.activation(out=hp[u][:, t, :], in_=hacc[u, t][:], func=ACT.Relu, bias=b1c[:, u % 2, t : t + 1])
 
         def gpsimd_tokens(u):
-            if u == 0:
-                return 2 * P
-            return T if live(u + LEAD - 1) else 3 * P
+            return 2 * P if u == 0 else T
 
         def interleave_gpsimd(u):
             if live(u):
@@ -174,8 +173,8 @@ def tile_blockdiagmnistconvertible_pa_t_w4_kernel(tc, x_bytes, x_scale, W1_words
         def quant_h(u):
             if live(u):
                 cut = gpsimd_tokens(u)
-                hc[u] = work.tile([P, T], U32, name="hc", tag="hc", align_bytes=64, bufs=2)
-                hs[u] = work.tile([P, T], U8, name="hs", tag="hs", align_bytes=64, bufs=2)
+                hc[u] = work.tile([P, T], U32, name="hc", tag="hc", align_bytes=64, bufs=3)
+                hs[u] = work.tile([P, T], U8, name="hs", tag="hs", align_bytes=64, bufs=3)
                 quantize(hg[u][:], hc[u][:, :cut], hs[u][:, :cut])
                 if cut < T:
                     quantize(hv[u][:], hc[u][:, cut:], hs[u][:, cut:])
@@ -199,15 +198,15 @@ def tile_blockdiagmnistconvertible_pa_t_w4_kernel(tc, x_bytes, x_scale, W1_words
             if live(u):
                 n = u % 2
                 if a == 0:
-                    o[u] = work.tile([P, 4, BLK], F32, name="o", tag="o", bufs=4)
+                    o[u] = work.tile([P, 4, BLK], F32, name="o", tag="o", bufs=5)
                 nc.vector.tensor_tensor(out=o[u][:, a, :], in0=y[u, a][:], in1=bbr[:, n * BLK : (n + 1) * BLK], op=ALU.add)
 
         def rows_of(u):
             g, n = divmod(u, 2)
             return out[T * g : T * (g + 1), n * BLK : (n + 1) * BLK].rearrange("(p a) c -> p a c", a=4)
 
-        def relu_y_vector(u, a):
-            part = o[u][:, a, :]
+        def relu_y_vector(u, a0, a1):
+            part = o[u][:, a0:a1, :]
             nc.vector.tensor_scalar(out=part, in0=part, scalar1=0.0, scalar2=None, op0=ALU.max)
 
         def relu_y_scalar(u, a0, a1):
@@ -298,53 +297,87 @@ def tile_blockdiagmnistconvertible_pa_t_w4_kernel(tc, x_bytes, x_scale, W1_words
         turn_x(6)
         widen_x(7)
 
-        def finish(u, a):
-            relu_y_scalar(u, a, a + 1)
-            store(u, a, a + 1)
+        def runs(n0, n1):
+            return [(u, max(n0 - 4 * u, 0), min(n1 - 4 * u, 4)) for u in range(n0 // 4, (n1 + 3) // 4) if n1 > n0]
+
+        def finish(relu, n0, n1):
+            for u, a0, a1 in runs(n0, n1):
+                relu(u, a0, a1)
+                store(u, a0, a1)
+
+        def tiles_in(s):
+            if not live(s + LEAD):
+                return 5
+            return 4 if 0 < s <= FULL_SLOTS else 3
+
+        first = [sum(tiles_in(r) for r in range(s)) for s in range(UNITS + 1)]
+        multiplied = []
+
+        def multiply_ahead(n, s):
+            for m in range(len(multiplied), min(n + 3, 4 * (s + 1))):
+                stage2(m // 4, m % 4)
+                multiplied.append(m)
+
+        def empty(n, s):
+            bias_y(n // 4, n % 4)
+            multiply_ahead(n + 1, s)
+
+        def on_vector(s):
+            return 2 if live(s + 3) and not live(s + LEAD) else 1
+
+        def relu_halves(n0, n1, h):
+            half = (n1 - n0) * BLK // 2
+            lo = n0 * BLK + h * half
+            u, c0 = divmod(lo, 4 * BLK)
+            part = o[u][:].rearrange("p a c -> p (a c)")[:, c0 : c0 + half]
+            nc.vector.tensor_scalar(out=part, in0=part, scalar1=0.0, scalar2=None, op0=ALU.max)
 
         def slot(s):
-            draining = not live(s + 2)
+            n0, n1 = first[s], first[s + 1]
+            draining = not live(s + 3)
+            before_x = 1 if s > 0 else 0
             interleave_gpsimd(s + 1)
-            stage2(s, 0)
-            bias_y(s - 1, 2)
-            stage2(s, 1)
-            bias_y(s - 1, 3)
-            stage2(s, 2)
+            multiply_ahead(n0, s)
+            for n in range(n0, n0 + before_x):
+                empty(n, s)
             scale_x(s + LEAD)
             for t in range(4):
                 relu_h(s + 2, t)
-            if not live(s + LEAD):
-                for a in range(2 if s == UNITS - 1 else 1, 4):
-                    finish(s - 1, a)
-            elif s > 0:
-                relu_y_scalar(s - 1, 1, 4)
-                store(s - 1, 1, 4)
+            if s > 0 and live(s + 2):
+                if draining:
+                    for n in range(first[s - 1] + on_vector(s - 1), n0):
+                        finish(relu_y_scalar, n, n + 1)
+                else:
+                    finish(relu_y_scalar, first[s - 1] + on_vector(s - 1), n0)
             stage1(s + 3, 0)
             stage1(s + 3, 1)
+            empty(n0 + before_x, s)
             turn_x(s + LEAD + 1)
             widen_x(s + LEAD + 2)
-            bias_y(s, 0)
-            stage2(s, 3)
+            empty(n0 + before_x + 1, s)
             stage1(s + 3, 2)
             stage1(s + 3, 3)
-            bias_y(s, 1)
-            if draining:
-                finish(s, 0)
-                finish(s, 1)
+            for n in range(n0 + before_x + 2, n1):
+                empty(n, s)
+            if s == UNITS - 1:
+                for n in range(n0, n1 - 1):
+                    finish(relu_y_scalar, n, n + 1)
+                finish(relu_y_vector, n1 - 1, n1)
+            elif live(s + LEAD):
+                finish(relu_y_vector, n0, n0 + on_vector(s))
+                quant_h(s + 1)
+                quant_x(s + LEAD)
+                if s == 0:
+                    quant_wb(1)
             else:
-                relu_y_vector(s, 0)
-                store(s, 0, 1)
-            quant_h(s + 1)
-            quant_x(s + LEAD)
-            if s == 0:
-                quant_wb(1)
-            interleave_vector(s + 2)
+                if draining:
+                    for n in range(n0 + on_vector(s), n1):
+                        finish(relu_y_scalar, n, n + 1)
+                relu_halves(n0, n0 + on_vector(s), 0)
+                quant_h(s + 1)
+                relu_halves(n0, n0 + on_vector(s), 1)
+                for u, a0, a1 in runs(n0, n0 + on_vector(s)):
+                    store(u, a0, a1)
 
         for s in range(UNITS):
             slot(s)
-        last = UNITS - 1
-        bias_y(last, 2)
-        finish(last, 2)
-        bias_y(last, 3)
-        relu_y_vector(last, 3)
-        store(last, 3, 4)

@@ -22,7 +22,9 @@ T = 512
 GROUPS = B // T
 UNITS = 2 * GROUPS
 LEAD = 6
-FULL_SLOTS = 4
+BANKS = {"xt": 1, "y": 3, "h": 4}
+WIDEN_LEAD = 10
+EARLY_TILES = 2
 
 
 def tile_blockdiagmnistconvertible_pa_t_w4_kernel(tc, x_bytes, x_scale, W1_words, W1_scales, b1, Wb, bb, out):
@@ -59,18 +61,19 @@ def tile_blockdiagmnistconvertible_pa_t_w4_kernel(tc, x_bytes, x_scale, W1_words
         load_x(0)
         nc.sync.dma_start(out=sc[:], in_=x_scale.rearrange("o (p t) -> p (o t)", t=4))
         nc.sync.dma_start(out=w1r[:], in_=W1_words[0])
+        load_x(1)
         for q in range(4):
             nc.sync.dma_start(
                 out=wsr[32 * q : 32 * q + 4, :].bitcast(I32), in_=W1_scales[0, 4 * q : 4 * q + 4, :].bitcast(I32)
             )
-        load_x(1)
-        load_wb(0)
         load_x(2)
-        nc.sync.dma_start(out=b1c[:], in_=b1.rearrange("(n p t) -> p n t", n=2, t=4))
+        load_wb(0)
         load_x(3)
+        nc.sync.dma_start(out=b1c[:], in_=b1.rearrange("(n p t) -> p n t", n=2, t=4))
+        load_x(4)
         load_wb(1)
         nc.sync.dma_start(out=bbr[:], in_=bb.partition_broadcast(P))
-        for g in range(4, GROUPS):
+        for g in range(5, GROUPS):
             load_x(g)
 
         xs, xt, xg, xc, xsc = {}, {}, {}, {}, {}
@@ -91,13 +94,13 @@ def tile_blockdiagmnistconvertible_pa_t_w4_kernel(tc, x_bytes, x_scale, W1_words
 
         def widen_x(j):
             if live(j):
-                xs[j] = work.tile([P, 2, IN], BF16, name="xs", tag="xs", bufs=6)
+                xs[j] = work.tile([P, 2, IN], BF16, name="xs", tag="xs", bufs=8)
                 src = xb[j // 2][:, 2 * (j % 2) : 2 * (j % 2) + 2, :].rearrange("p a k -> p (a k)").bitcast(FP8)
                 dst = xs[j][:].rearrange("p a k -> p (a k)")
                 nc.scalar.copy(out=dst, in_=src)
 
         def bank(tag):
-            return psum.tile([P, 2, 2 * P], F32, name="bank", tag=tag, bufs=1 if tag == "xt" else 3)
+            return psum.tile([P, 2, 2 * P], F32, name="bank", tag=tag, bufs=BANKS[tag])
 
         def turn_x(j, tag="xt"):
             if live(j):
@@ -175,17 +178,17 @@ def tile_blockdiagmnistconvertible_pa_t_w4_kernel(tc, x_bytes, x_scale, W1_words
                 cut = gpsimd_tokens(u)
                 hc[u] = work.tile([P, T], U32, name="hc", tag="hc", align_bytes=64, bufs=3)
                 hs[u] = work.tile([P, T], U8, name="hs", tag="hs", align_bytes=64, bufs=3)
-                quantize(hg[u][:], hc[u][:, :cut], hs[u][:, :cut])
                 if cut < T:
                     quantize(hv[u][:], hc[u][:, cut:], hs[u][:, cut:])
+                quantize(hg[u][:], hc[u][:, :cut], hs[u][:, :cut])
 
         def stage2(u, a):
             if live(u):
                 n = u % 2
-                y[u, a] = psum.tile([P, BLK], F32, name="y", tag="y")
+                y[u, a] = bank(y_tag(4 * u + a))[:].rearrange("p u r -> p (u r)")
                 cols = slice(a * P, (a + 1) * P)
                 nc.tensor.matmul_mx(
-                    out=y[u, a][:],
+                    out=y[u, a],
                     lhsT=hc[u][:, cols].bitcast(FP8X4),
                     lhsT_scale=hs[u][:, cols],
                     rhs=wbc[n][:].bitcast(FP8X4),
@@ -199,19 +202,11 @@ def tile_blockdiagmnistconvertible_pa_t_w4_kernel(tc, x_bytes, x_scale, W1_words
                 n = u % 2
                 if a == 0:
                     o[u] = work.tile([P, 4, BLK], F32, name="o", tag="o", bufs=5)
-                nc.vector.tensor_tensor(out=o[u][:, a, :], in0=y[u, a][:], in1=bbr[:, n * BLK : (n + 1) * BLK], op=ALU.add)
+                nc.vector.tensor_tensor(out=o[u][:, a, :], in0=y[u, a], in1=bbr[:, n * BLK : (n + 1) * BLK], op=ALU.add)
 
         def rows_of(u):
             g, n = divmod(u, 2)
             return out[T * g : T * (g + 1), n * BLK : (n + 1) * BLK].rearrange("(p a) c -> p a c", a=4)
-
-        def relu_y_vector(u, a0, a1):
-            part = o[u][:, a0:a1, :]
-            nc.vector.tensor_scalar(out=part, in0=part, scalar1=0.0, scalar2=None, op0=ALU.max)
-
-        def relu_y_scalar(u, a0, a1):
-            part = o[u][:, a0:a1, :]
-            nc.scalar.activation(out=part, in_=part, func=ACT.Relu)
 
         def store(u, a0, a1):
             nc.sync.dma_start(out=rows_of(u)[:, a0:a1, :], in_=o[u][:, a0:a1, :])
@@ -259,19 +254,19 @@ def tile_blockdiagmnistconvertible_pa_t_w4_kernel(tc, x_bytes, x_scale, W1_words
         scale_x(1)
         permute_scales(0)
         quant_x(0, 2)
-        permute_scales(1)
         widen_x(4)
         widen_x(5)
-        widen_x(6)
         turn_wb(0, 0, "xt")
+        widen_x(6)
+        widen_x(7)
         unload_wb(0, 0, nc.scalar.copy)
         for t in range(4):
             stage1(0, t)
         scale_x(2)
         scale_x(3)
+        permute_scales(1)
         quant_x(2, 2)
         turn_x(4, "y")
-        turn_wb(0, 1, "xt")
         for t in range(4):
             relu_h(0, t)
         stage1(1, 0)
@@ -279,42 +274,64 @@ def tile_blockdiagmnistconvertible_pa_t_w4_kernel(tc, x_bytes, x_scale, W1_words
         turn_x(5, "y")
         stage1(1, 2)
         stage1(1, 3)
-        unload_wb(0, 1, nc.scalar.copy)
-        turn_wb(1, 0, "xt")
-        turn_wb(1, 1, "y")
+        turn_wb(0, 1, "xt")
+        turn_x(6, "y")
         for t in range(4):
             relu_h(1, t)
-            stage1(2, t)
+        unload_wb(0, 1, nc.scalar.copy)
+        stage1(2, 0)
+        stage1(2, 1)
+        turn_wb(1, 0, "xt")
+        stage1(2, 2)
+        stage1(2, 3)
         interleave_gpsimd(0)
         scale_x(4)
         scale_x(5)
         interleave_vector(0)
-        quant_wb(0)
-        quant_h(0)
         quant_x(4, 2)
+        quant_h(0)
+        quant_wb(0)
+        widen_x(8)
         unload_wb(1, 0, nc.scalar.copy)
-        unload_wb(1, 1, nc.scalar.copy)
-        turn_x(6)
-        widen_x(7)
+        widen_x(9)
 
-        def runs(n0, n1):
-            return [(u, max(n0 - 4 * u, 0), min(n1 - 4 * u, 4)) for u in range(n0 // 4, (n1 + 3) // 4) if n1 > n0]
+        def runs(c0, c1):
+            width = 4 * BLK
+            return [(u, max(c0 - width * u, 0), min(c1 - width * u, width)) for u in range(c0 // width, -(-c1 // width)) if c1 > c0]
 
-        def finish(relu, n0, n1):
-            for u, a0, a1 in runs(n0, n1):
-                relu(u, a0, a1)
-                store(u, a0, a1)
+        def relu_vector(c0, c1):
+            for u, lo, hi in runs(c0, c1):
+                part = o[u][:].rearrange("p a c -> p (a c)")[:, lo:hi]
+                nc.vector.tensor_scalar(out=part, in0=part, scalar1=0.0, scalar2=None, op0=ALU.max)
+
+        def relu_scalar(c0, c1):
+            for u, lo, hi in runs(c0, c1):
+                part = o[u][:].rearrange("p a c -> p (a c)")[:, lo:hi]
+                nc.scalar.activation(out=part, in_=part, func=ACT.Relu)
+
+        def store_tiles(n0, n1):
+            for u, lo, hi in runs(n0 * BLK, n1 * BLK):
+                store(u, lo // BLK, hi // BLK)
 
         def tiles_in(s):
             if not live(s + LEAD):
                 return 5
-            return 4 if 0 < s <= FULL_SLOTS else 3
+            return 3 if live(s + WIDEN_LEAD) else 4
 
         first = [sum(tiles_in(r) for r in range(s)) for s in range(UNITS + 1)]
         multiplied = []
+        x_done = first[UNITS - LEAD] + 3
+
+        def y_tag(n):
+            if n >= 4 * (UNITS - 1):
+                return "h"
+            return "xt" if n >= x_done and (n - x_done) % 4 == 0 else "y"
+
+        def ahead(n):
+            return 4 if n + 3 >= x_done else 3
 
         def multiply_ahead(n, s):
-            for m in range(len(multiplied), min(n + 3, 4 * (s + 1))):
+            for m in range(len(multiplied), min(n + ahead(n), 4 * (s + 1))):
                 stage2(m // 4, m % 4)
                 multiplied.append(m)
 
@@ -323,37 +340,44 @@ def tile_blockdiagmnistconvertible_pa_t_w4_kernel(tc, x_bytes, x_scale, W1_words
             multiply_ahead(n + 1, s)
 
         def on_vector(s):
-            return 2 if live(s + 3) and not live(s + LEAD) else 1
+            if live(s + LEAD):
+                return BLK if live(s + WIDEN_LEAD) else 384
+            return 1024 if live(s + 3) else 512
 
-        def relu_halves(n0, n1, h):
-            half = (n1 - n0) * BLK // 2
-            lo = n0 * BLK + h * half
-            u, c0 = divmod(lo, 4 * BLK)
-            part = o[u][:].rearrange("p a c -> p (a c)")[:, c0 : c0 + half]
-            nc.vector.tensor_scalar(out=part, in0=part, scalar1=0.0, scalar2=None, op0=ALU.max)
+        def finish_on_scalar(c0, n1, by_tile):
+            if by_tile:
+                for n in range(c0 // BLK, n1):
+                    relu_scalar(max(c0, n * BLK), (n + 1) * BLK)
+                    store_tiles(n, n + 1)
+            else:
+                relu_scalar(c0, n1 * BLK)
+                store_tiles(c0 // BLK, n1)
 
         def slot(s):
             n0, n1 = first[s], first[s + 1]
             draining = not live(s + 3)
             before_x = 1 if s > 0 else 0
             interleave_gpsimd(s + 1)
-            multiply_ahead(n0, s)
+            multiply_ahead(n0 if s < UNITS - 1 else n1, s)
             for n in range(n0, n0 + before_x):
                 empty(n, s)
             scale_x(s + LEAD)
+            left = first[s - 1] * BLK + on_vector(s - 1) if s > 0 else 0
+            if live(s + 2) and not live(s + LEAD):
+                finish_on_scalar(left, left // BLK + EARLY_TILES, False)
+                left = (left // BLK + EARLY_TILES) * BLK
             for t in range(4):
                 relu_h(s + 2, t)
+                if s == 0 and t == 1:
+                    turn_wb(1, 1, "xt")
+                    unload_wb(1, 1, nc.scalar.copy)
             if s > 0 and live(s + 2):
-                if draining:
-                    for n in range(first[s - 1] + on_vector(s - 1), n0):
-                        finish(relu_y_scalar, n, n + 1)
-                else:
-                    finish(relu_y_scalar, first[s - 1] + on_vector(s - 1), n0)
+                finish_on_scalar(left, n0, draining)
             stage1(s + 3, 0)
             stage1(s + 3, 1)
             empty(n0 + before_x, s)
             turn_x(s + LEAD + 1)
-            widen_x(s + LEAD + 2)
+            widen_x(s + WIDEN_LEAD)
             empty(n0 + before_x + 1, s)
             stage1(s + 3, 2)
             stage1(s + 3, 3)
@@ -361,23 +385,28 @@ def tile_blockdiagmnistconvertible_pa_t_w4_kernel(tc, x_bytes, x_scale, W1_words
                 empty(n, s)
             if s == UNITS - 1:
                 for n in range(n0, n1 - 1):
-                    finish(relu_y_scalar, n, n + 1)
-                finish(relu_y_vector, n1 - 1, n1)
+                    relu_scalar(n * BLK, (n + 1) * BLK)
+                    store_tiles(n, n + 1)
+                relu_vector((n1 - 1) * BLK, n1 * BLK)
+                store_tiles(n1 - 1, n1)
+                return
+            if draining:
+                finish_on_scalar(n0 * BLK + on_vector(s), n1, True)
+            c0, c1 = n0 * BLK, n0 * BLK + on_vector(s)
+            if s == 0:
+                relu_vector(c0, c1)
+                quant_x(s + LEAD)
+                quant_h(s + 1)
+                quant_wb(1)
             elif live(s + LEAD):
-                finish(relu_y_vector, n0, n0 + on_vector(s))
+                relu_vector(c0, c1)
                 quant_h(s + 1)
                 quant_x(s + LEAD)
-                if s == 0:
-                    quant_wb(1)
             else:
-                if draining:
-                    for n in range(n0 + on_vector(s), n1):
-                        finish(relu_y_scalar, n, n + 1)
-                relu_halves(n0, n0 + on_vector(s), 0)
+                relu_vector(c0, (c0 + c1) // 2)
                 quant_h(s + 1)
-                relu_halves(n0, n0 + on_vector(s), 1)
-                for u, a0, a1 in runs(n0, n0 + on_vector(s)):
-                    store(u, a0, a1)
+                relu_vector((c0 + c1) // 2, c1)
+            store_tiles(n0, c1 // BLK)
 
         for s in range(UNITS):
             slot(s)

@@ -24,7 +24,9 @@ UNITS = 2 * GROUPS
 LEAD = 6
 BANKS = {"xt": 1, "y": 3, "h": 4}
 WIDEN_LEAD = 10
-EARLY_TILES = 2
+X_SLOT_COLS = 1664
+LATE_SLOT_COLS = 2688
+EARLY_COLS = 1024
 
 
 def tile_blockdiagmnistconvertible_pa_t_w4_kernel(tc, x_bytes, x_scale, W1_words, W1_scales, b1, Wb, bb, out):
@@ -176,8 +178,8 @@ def tile_blockdiagmnistconvertible_pa_t_w4_kernel(tc, x_bytes, x_scale, W1_words
         def quant_h(u):
             if live(u):
                 cut = gpsimd_tokens(u)
-                hc[u] = work.tile([P, T], U32, name="hc", tag="hc", align_bytes=64, bufs=3)
-                hs[u] = work.tile([P, T], U8, name="hs", tag="hs", align_bytes=64, bufs=3)
+                hc[u] = work.tile([P, T], U32, name="hc", tag="hc", align_bytes=64, bufs=4)
+                hs[u] = work.tile([P, T], U8, name="hs", tag="hs", align_bytes=64, bufs=4)
                 if cut < T:
                     quantize(hv[u][:], hc[u][:, cut:], hs[u][:, cut:])
                 quantize(hg[u][:], hc[u][:, :cut], hs[u][:, :cut])
@@ -197,12 +199,11 @@ def tile_blockdiagmnistconvertible_pa_t_w4_kernel(tc, x_bytes, x_scale, W1_words
                     stop=True,
                 )
 
-        def bias_y(u, a):
-            if live(u):
-                n = u % 2
-                if a == 0:
-                    o[u] = work.tile([P, 4, BLK], F32, name="o", tag="o", bufs=5)
-                nc.vector.tensor_tensor(out=o[u][:, a, :], in0=y[u, a], in1=bbr[:, n * BLK : (n + 1) * BLK], op=ALU.add)
+        def bias_y(u, a, lo, hi):
+            if a == 0 and lo == 0:
+                o[u] = work.tile([P, 4, BLK], F32, name="o", tag="o", bufs=6)
+            bias = bbr[:, u % 2 * BLK + lo : u % 2 * BLK + hi]
+            nc.vector.tensor_tensor(out=o[u][:, a, lo:hi], in0=y[u, a][:, lo:hi], in1=bias, op=ALU.add)
 
         def rows_of(u):
             g, n = divmod(u, 2)
@@ -295,118 +296,118 @@ def tile_blockdiagmnistconvertible_pa_t_w4_kernel(tc, x_bytes, x_scale, W1_words
         unload_wb(1, 0, nc.scalar.copy)
         widen_x(9)
 
-        def runs(c0, c1):
-            width = 4 * BLK
-            return [(u, max(c0 - width * u, 0), min(c1 - width * u, width)) for u in range(c0 // width, -(-c1 // width)) if c1 > c0]
+        def cut(c0, c1, width):
+            return [(j, max(c0 - width * j, 0), min(c1 - width * j, width)) for j in range(c0 // width, -(-c1 // width))]
 
-        def relu_vector(c0, c1):
-            for u, lo, hi in runs(c0, c1):
+        cleared = [0] * (4 * UNITS)
+
+        def relu(engine, c0, c1):
+            for u, lo, hi in cut(c0, c1, 4 * BLK):
                 part = o[u][:].rearrange("p a c -> p (a c)")[:, lo:hi]
-                nc.vector.tensor_scalar(out=part, in0=part, scalar1=0.0, scalar2=None, op0=ALU.max)
+                if engine == "vector":
+                    nc.vector.tensor_scalar(out=part, in0=part, scalar1=0.0, scalar2=None, op0=ALU.max)
+                else:
+                    nc.scalar.activation(out=part, in_=part, func=ACT.Relu)
+                done = []
+                for a, t0, t1 in cut(lo, hi, BLK):
+                    cleared[4 * u + a] = cleared[4 * u + a] + t1 - t0
+                    if cleared[4 * u + a] == BLK:
+                        done.append(a)
+                if done:
+                    store(u, done[0], done[-1] + 1)
 
-        def relu_scalar(c0, c1):
-            for u, lo, hi in runs(c0, c1):
-                part = o[u][:].rearrange("p a c -> p (a c)")[:, lo:hi]
-                nc.scalar.activation(out=part, in_=part, func=ACT.Relu)
+        def relu_by_tile(c0, c1):
+            for n, lo, hi in cut(c0, c1, BLK):
+                relu("scalar", n * BLK + lo, n * BLK + hi)
 
-        def store_tiles(n0, n1):
-            for u, lo, hi in runs(n0 * BLK, n1 * BLK):
-                store(u, lo // BLK, hi // BLK)
-
-        def tiles_in(s):
-            if not live(s + LEAD):
-                return 5
-            return 3 if live(s + WIDEN_LEAD) else 4
-
-        first = [sum(tiles_in(r) for r in range(s)) for s in range(UNITS + 1)]
+        first = [0, 3 * BLK]
+        for s in range(1, UNITS - 1):
+            first.append(first[-1] + (X_SLOT_COLS if live(s + LEAD) else LATE_SLOT_COLS))
+        first.append(4 * UNITS * BLK)
         multiplied = []
-        x_done = first[UNITS - LEAD] + 3
+        x_done = first[UNITS - LEAD] // BLK + 3
 
         def y_tag(n):
             if n >= 4 * (UNITS - 1):
                 return "h"
             return "xt" if n >= x_done and (n - x_done) % 4 == 0 else "y"
 
-        def ahead(n):
-            return 4 if n + 3 >= x_done else 3
-
         def multiply_ahead(n, s):
-            for m in range(len(multiplied), min(n + ahead(n), 4 * (s + 1))):
+            ahead = 4 if n + 3 >= x_done else 3
+            for m in range(len(multiplied), min(n + ahead, 4 * (s + 1))):
                 stage2(m // 4, m % 4)
                 multiplied.append(m)
 
-        def empty(n, s):
-            bias_y(n // 4, n % 4)
-            multiply_ahead(n + 1, s)
+        def empty(piece, s):
+            n, lo, hi = piece
+            bias_y(n // 4, n % 4, lo, hi)
+            if hi == BLK:
+                multiply_ahead(n + 1, s)
 
         def on_vector(s):
             if live(s + LEAD):
-                return BLK if live(s + WIDEN_LEAD) else 384
-            return 1024 if live(s + 3) else 512
-
-        def finish_on_scalar(c0, n1, by_tile):
-            if by_tile:
-                for n in range(c0 // BLK, n1):
-                    relu_scalar(max(c0, n * BLK), (n + 1) * BLK)
-                    store_tiles(n, n + 1)
-            else:
-                relu_scalar(c0, n1 * BLK)
-                store_tiles(c0 // BLK, n1)
+                return 512 if live(s + WIDEN_LEAD) else 384
+            return 1024 if live(s + 3) else 768
 
         def slot(s):
-            n0, n1 = first[s], first[s + 1]
-            draining = not live(s + 3)
+            c0, c1 = first[s], first[s + 1]
+            pieces = cut(c0, c1, BLK)
             before_x = 1 if s > 0 else 0
             interleave_gpsimd(s + 1)
-            multiply_ahead(n0 if s < UNITS - 1 else n1, s)
-            for n in range(n0, n0 + before_x):
-                empty(n, s)
+            multiply_ahead(c0 // BLK if s < UNITS - 1 else 4 * UNITS, s)
+            for piece in pieces[:before_x]:
+                empty(piece, s)
             scale_x(s + LEAD)
-            left = first[s - 1] * BLK + on_vector(s - 1) if s > 0 else 0
+            left = first[s - 1] + on_vector(s - 1) if s > 0 else 0
             if live(s + 2) and not live(s + LEAD):
-                finish_on_scalar(left, left // BLK + EARLY_TILES, False)
-                left = (left // BLK + EARLY_TILES) * BLK
-            for t in range(4):
+                relu("scalar", left, left + EARLY_COLS)
+                left = left + EARLY_COLS
+            last_h = s + 2 == UNITS - 1
+            for t in range(2 if last_h else 4):
                 relu_h(s + 2, t)
                 if s == 0 and t == 1:
                     turn_wb(1, 1, "xt")
                     unload_wb(1, 1, nc.scalar.copy)
             if s > 0 and live(s + 2):
-                finish_on_scalar(left, n0, draining)
+                relu("scalar", left, c0)
             stage1(s + 3, 0)
             stage1(s + 3, 1)
-            empty(n0 + before_x, s)
+            empty(pieces[before_x], s)
             turn_x(s + LEAD + 1)
             widen_x(s + WIDEN_LEAD)
-            empty(n0 + before_x + 1, s)
+            empty(pieces[before_x + 1], s)
             stage1(s + 3, 2)
             stage1(s + 3, 3)
-            for n in range(n0 + before_x + 2, n1):
-                empty(n, s)
+            for piece in pieces[before_x + 2 :]:
+                empty(piece, s)
             if s == UNITS - 1:
-                for n in range(n0, n1 - 1):
-                    relu_scalar(n * BLK, (n + 1) * BLK)
-                    store_tiles(n, n + 1)
-                relu_vector((n1 - 1) * BLK, n1 * BLK)
-                store_tiles(n1 - 1, n1)
+                relu_by_tile(c0, c1 - BLK)
+                relu("vector", c1 - BLK, c1)
                 return
-            if draining:
-                finish_on_scalar(n0 * BLK + on_vector(s), n1, True)
-            c0, c1 = n0 * BLK, n0 * BLK + on_vector(s)
+            mine = c0 + on_vector(s)
+            if last_h:
+                split = (mine + 1024) // BLK * BLK
+                relu_by_tile(mine, split)
+                relu_h(s + 2, 2)
+                relu_h(s + 2, 3)
+            elif not live(s + 3):
+                split = (c1 - BLK) // BLK * BLK
+                relu_by_tile(mine, split)
             if s == 0:
-                relu_vector(c0, c1)
+                relu("vector", c0, mine)
                 quant_x(s + LEAD)
                 quant_h(s + 1)
                 quant_wb(1)
             elif live(s + LEAD):
-                relu_vector(c0, c1)
+                relu("vector", c0, mine)
                 quant_h(s + 1)
                 quant_x(s + LEAD)
             else:
-                relu_vector(c0, (c0 + c1) // 2)
+                relu("vector", c0, (c0 + mine) // 2)
                 quant_h(s + 1)
-                relu_vector((c0 + c1) // 2, c1)
-            store_tiles(n0, c1 // BLK)
+                relu("vector", (c0 + mine) // 2, mine)
+            if not live(s + 3):
+                relu_by_tile(split, c1)
 
         for s in range(UNITS):
             slot(s)

@@ -22,6 +22,7 @@ T = 512
 GROUPS = B // T
 UNITS = 2 * GROUPS
 LEAD = 6
+RING = 64
 BANKS = {"xt": 1, "y": 3, "h": 4}
 WIDEN_LEAD = 10
 X_SLOT_COLS = 1664
@@ -46,6 +47,7 @@ def tile_blockdiagmnistconvertible_pa_t_w4_kernel(tc, x_bytes, x_scale, W1_words
         wsp = keep.tile([P, 2, 4, P], U8, name="wsp", align_bytes=64)
         b1c = keep.tile([P, 2, 4], BF16, name="b1c")
         bbr = keep.tile([P, HID], BF16, name="bbr")
+        ring = keep.tile([P, RING * BLK], F32, name="ring")
         xb = [keep.tile([P, 4, IN], U8, name=f"xb{g}") for g in range(GROUPS)]
         wbr = [keep.tile([P, 4, BLK], BF16, name=f"wbr{n}") for n in range(2)]
         wbg = [keep.tile([P, BLK, 4], BF16, name=f"wbg{n}", align_bytes=64) for n in range(2)]
@@ -69,9 +71,9 @@ def tile_blockdiagmnistconvertible_pa_t_w4_kernel(tc, x_bytes, x_scale, W1_words
                 out=wsr[32 * q : 32 * q + 4, :].bitcast(I32), in_=W1_scales[0, 4 * q : 4 * q + 4, :].bitcast(I32)
             )
         load_x(2)
-        load_wb(0)
         load_x(3)
         nc.sync.dma_start(out=b1c[:], in_=b1.rearrange("(n p t) -> p n t", n=2, t=4))
+        load_wb(0)
         load_x(4)
         load_wb(1)
         nc.sync.dma_start(out=bbr[:], in_=bb.partition_broadcast(P))
@@ -80,7 +82,7 @@ def tile_blockdiagmnistconvertible_pa_t_w4_kernel(tc, x_bytes, x_scale, W1_words
 
         xs, xt, xg, xc, xsc = {}, {}, {}, {}, {}
         hacc, hp, hg, hv, hc, hs = {}, {}, {}, {}, {}, {}
-        y, o, wt = {}, {}, {}
+        y, wt = {}, {}
 
         def live(u):
             return 0 <= u < UNITS
@@ -96,7 +98,7 @@ def tile_blockdiagmnistconvertible_pa_t_w4_kernel(tc, x_bytes, x_scale, W1_words
 
         def widen_x(j):
             if live(j):
-                xs[j] = work.tile([P, 2, IN], BF16, name="xs", tag="xs", bufs=8)
+                xs[j] = work.tile([P, 2, IN], BF16, name="xs", tag="xs", bufs=5)
                 src = xb[j // 2][:, 2 * (j % 2) : 2 * (j % 2) + 2, :].rearrange("p a k -> p (a k)").bitcast(FP8)
                 dst = xs[j][:].rearrange("p a k -> p (a k)")
                 nc.scalar.copy(out=dst, in_=src)
@@ -169,7 +171,7 @@ def tile_blockdiagmnistconvertible_pa_t_w4_kernel(tc, x_bytes, x_scale, W1_words
         def interleave_vector(u):
             if live(u) and gpsimd_tokens(u) < T:
                 cut = gpsimd_tokens(u)
-                hv[u] = work.tile([P, T - cut, 4], BF16, name="hv", tag="hv", align_bytes=64, bufs=2)
+                hv[u] = work.tile([P, T - cut, 4], BF16, name="hv", tag="hv", align_bytes=64, bufs=1)
                 nc.vector.tensor_copy(
                     out=hv[u][:].rearrange("p (c i) t -> p c t i", i=4),
                     in_=hp[u][:, :, cut:].rearrange("p t (c i) -> p c t i", i=4),
@@ -199,18 +201,20 @@ def tile_blockdiagmnistconvertible_pa_t_w4_kernel(tc, x_bytes, x_scale, W1_words
                     stop=True,
                 )
 
+        def ring_columns(c0, c1):
+            start = c0 % (RING * BLK)
+            return ring[:, start : start + c1 - c0]
+
         def bias_y(u, a, lo, hi):
-            if a == 0 and lo == 0:
-                o[u] = work.tile([P, 4, BLK], F32, name="o", tag="o", bufs=6)
             bias = bbr[:, u % 2 * BLK + lo : u % 2 * BLK + hi]
-            nc.vector.tensor_tensor(out=o[u][:, a, lo:hi], in0=y[u, a][:, lo:hi], in1=bias, op=ALU.add)
+            nc.vector.tensor_tensor(out=ring_columns((4 * u + a) * BLK + lo, (4 * u + a) * BLK + hi), in0=y[u, a][:, lo:hi], in1=bias, op=ALU.add)
 
         def rows_of(u):
             g, n = divmod(u, 2)
             return out[T * g : T * (g + 1), n * BLK : (n + 1) * BLK].rearrange("(p a) c -> p a c", a=4)
 
         def store(u, a0, a1):
-            nc.sync.dma_start(out=rows_of(u)[:, a0:a1, :], in_=o[u][:, a0:a1, :])
+            nc.sync.dma_start(out=rows_of(u)[:, a0:a1, :], in_=ring_columns((4 * u + a0) * BLK, (4 * u + a1) * BLK).rearrange("p (a c) -> p a c", c=BLK))
 
         def permute_words(n):
             nc.vector.tensor_copy(
@@ -255,39 +259,35 @@ def tile_blockdiagmnistconvertible_pa_t_w4_kernel(tc, x_bytes, x_scale, W1_words
         scale_x(1)
         permute_scales(0)
         quant_x(0, 2)
-        widen_x(4)
-        widen_x(5)
-        turn_wb(0, 0, "xt")
-        widen_x(6)
-        widen_x(7)
-        unload_wb(0, 0, nc.scalar.copy)
+        for j in range(4, 8):
+            widen_x(j)
         for t in range(4):
             stage1(0, t)
+        turn_x(4)
+        turn_x(5, "y")
         scale_x(2)
         scale_x(3)
         permute_scales(1)
         quant_x(2, 2)
-        turn_x(4, "y")
         for t in range(4):
             relu_h(0, t)
-        stage1(1, 0)
-        stage1(1, 1)
-        turn_x(5, "y")
-        stage1(1, 2)
-        stage1(1, 3)
-        turn_wb(0, 1, "xt")
-        turn_x(6, "y")
-        for t in range(4):
-            relu_h(1, t)
-        unload_wb(0, 1, nc.scalar.copy)
-        stage1(2, 0)
-        stage1(2, 1)
-        turn_wb(1, 0, "xt")
-        stage1(2, 2)
-        stage1(2, 3)
+        for h in range(2):
+            stage1(1, 2 * h)
+            stage1(1, 2 * h + 1)
+            turn_wb(0, h, "y")
+        for h in range(2):
+            relu_h(1, 2 * h)
+            relu_h(1, 2 * h + 1)
+            unload_wb(0, h, nc.scalar.copy)
         interleave_gpsimd(0)
         scale_x(4)
+        turn_x(6)
+        stage1(2, 0)
+        stage1(2, 1)
         scale_x(5)
+        turn_wb(1, 0, "y")
+        stage1(2, 2)
+        stage1(2, 3)
         interleave_vector(0)
         quant_x(4, 2)
         quant_h(0)
@@ -302,19 +302,20 @@ def tile_blockdiagmnistconvertible_pa_t_w4_kernel(tc, x_bytes, x_scale, W1_words
         cleared = [0] * (4 * UNITS)
 
         def relu(engine, c0, c1):
-            for u, lo, hi in cut(c0, c1, 4 * BLK):
-                part = o[u][:].rearrange("p a c -> p (a c)")[:, lo:hi]
+            for j, lo, hi in cut(c0, c1, RING * BLK):
+                part = ring[:, lo:hi]
                 if engine == "vector":
                     nc.vector.tensor_scalar(out=part, in0=part, scalar1=0.0, scalar2=None, op0=ALU.max)
                 else:
                     nc.scalar.activation(out=part, in_=part, func=ACT.Relu)
-                done = []
-                for a, t0, t1 in cut(lo, hi, BLK):
-                    cleared[4 * u + a] = cleared[4 * u + a] + t1 - t0
-                    if cleared[4 * u + a] == BLK:
-                        done.append(a)
-                if done:
-                    store(u, done[0], done[-1] + 1)
+            done = []
+            for n, lo, hi in cut(c0, c1, BLK):
+                cleared[n] = cleared[n] + hi - lo
+                if cleared[n] == BLK:
+                    done.append(n)
+            if done:
+                for u, lo, hi in cut(done[0], done[-1] + 1, 4):
+                    store(u, lo, hi)
 
         def relu_by_tile(c0, c1):
             for n, lo, hi in cut(c0, c1, BLK):

@@ -21,13 +21,27 @@ P = 128
 T = 512
 GROUPS = B // T
 UNITS = 2 * GROUPS
-LEAD = 6
-RING = 64
-BANKS = {"xt": 1, "y": 3, "h": 4}
-WIDEN_LEAD = 10
-X_SLOT_COLS = 1664
-LATE_SLOT_COLS = 2688
-EARLY_COLS = 1024
+TILES = 4 * UNITS
+BANKS = 8
+RING = 56
+HEAD_X = 6
+HEAD_WIDE = 10
+FIRST_PE = 4
+X_LAG = 4
+SKIP = 99
+X_TILES = 4
+LATE_TILES = 5
+G_TILE = 512
+G_X = 1024
+G_FIX = 384
+G_END = 1536
+V_FROM = 99
+V_TO = 15
+JOINT_TILES = 3
+S_EARLY = 896
+S_X = 0
+S_LATE = 384
+BIG = 3.0e38
 
 
 def tile_blockdiagmnistconvertible_pa_t_w4_kernel(tc, x_bytes, x_scale, W1_words, W1_scales, b1, Wb, bb, out):
@@ -36,10 +50,11 @@ def tile_blockdiagmnistconvertible_pa_t_w4_kernel(tc, x_bytes, x_scale, W1_words
     with ExitStack() as ctx:
         keep = ctx.enter_context(tc.tile_pool(name="keep", bufs=1))
         work = ctx.enter_context(tc.tile_pool(name="work", bufs=3))
-        psum = ctx.enter_context(tc.psum_pool(name="psum", bufs=3))
+        psum = ctx.enter_context(tc.psum_pool(name="psum", bufs=1))
         ctx.enter_context(tc.manual_schedule())
 
         ident = keep.tile([P, P], F32, name="ident")
+        identb = keep.tile([P, P], BF16, name="identb")
         sc = keep.tile([P, 4], F32, name="sc")
         w1r = keep.tile([P, 2048], U8, name="w1r")
         w1p = keep.tile([P, 2, 4, P, 2], U8, name="w1p", align_bytes=64)
@@ -49,10 +64,9 @@ def tile_blockdiagmnistconvertible_pa_t_w4_kernel(tc, x_bytes, x_scale, W1_words
         bbr = keep.tile([P, HID], BF16, name="bbr")
         ring = keep.tile([P, RING * BLK], F32, name="ring")
         xb = [keep.tile([P, 4, IN], U8, name=f"xb{g}") for g in range(GROUPS)]
-        wbr = [keep.tile([P, 4, BLK], BF16, name=f"wbr{n}") for n in range(2)]
-        wbg = [keep.tile([P, BLK, 4], BF16, name=f"wbg{n}", align_bytes=64) for n in range(2)]
         wbc = [keep.tile([P, BLK], U32, name=f"wbc{n}", align_bytes=64) for n in range(2)]
         wbs = [keep.tile([P, BLK], U8, name=f"wbs{n}", align_bytes=64) for n in range(2)]
+        wbr = [keep.tile([P, 4, BLK], BF16, name=f"wbr{n}") for n in range(2)]
 
         def load_x(g):
             nc.sync.dma_start(out=xb[g][:], in_=x_bytes[T * g : T * (g + 1), :].rearrange("(p a) k -> p a k", a=4))
@@ -62,6 +76,7 @@ def tile_blockdiagmnistconvertible_pa_t_w4_kernel(tc, x_bytes, x_scale, W1_words
 
         nc.vector.memset(wsr[:].bitcast(I32), 0)
         make_identity(nc, ident[:])
+        make_identity(nc, identb[:])
         load_x(0)
         nc.sync.dma_start(out=sc[:], in_=x_scale.rearrange("o (p t) -> p (o t)", t=4))
         nc.sync.dma_start(out=w1r[:], in_=W1_words[0])
@@ -80,232 +95,196 @@ def tile_blockdiagmnistconvertible_pa_t_w4_kernel(tc, x_bytes, x_scale, W1_words
         for g in range(5, GROUPS):
             load_x(g)
 
-        xs, xt, xg, xc, xsc = {}, {}, {}, {}, {}
-        hacc, hp, hg, hv, hc, hs = {}, {}, {}, {}, {}, {}
-        y, wt = {}, {}
+        xs, xg, xc, xsc = {}, {}, {}, {}
+        hp, hg, hc, hs, wbg, both = {}, {}, {}, {}, {}, {}
+        filled = {}
+        order = []
+        emptied = set()
+        permuted = set()
 
         def live(u):
             return 0 <= u < UNITS
 
-        def quantize(src, codes, scales):
-            nc.vector.quantize_mx(out=codes.bitcast(FP8X4), scales=scales, in_=src.rearrange("p r t -> p (r t)"))
+        def partner(u):
+            g = (u + X_LAG) // 2
+            return g if u >= FIRST_PE and (u + X_LAG) % 2 == 0 and g < GROUPS else None
 
-        def turn(bank, rows):
-            for a in (0, 1):
-                words = rows[:, a, :].bitcast(F32)
-                for u in (0, 1):
-                    nc.tensor.transpose(bank[:, u, a * P : (a + 1) * P], words[:, u : 2 * P : 2], ident[:])
+        def joint(u):
+            if u not in both:
+                both[u] = work.tile([P, 2, T, 4], BF16, name="joint", tag="joint", align_bytes=64, bufs=2)
+            return both[u]
+
+        def single(name):
+            return work.tile([P, T, 4], BF16, name=name, tag="single", align_bytes=64, bufs=2)
+
+        def quantize(src, codes, scales):
+            nc.vector.quantize_mx(out=codes.bitcast(FP8X4), scales=scales, in_=src)
+
+        def code_tiles(width, kind, bufs):
+            codes = work.tile([P, width], U32, name="codes", tag=f"codes_{kind}", align_bytes=64, bufs=bufs)
+            scales = work.tile([P, width], U8, name="scales", tag=f"scales_{kind}", align_bytes=64, bufs=bufs)
+            return codes, scales
+
+        def bank(key, shape, dtype):
+            filled[key] = psum.tile(shape, dtype, name="bank", tag=f"bank{len(order) % BANKS}")
+            order.append(key)
+            return filled[key]
+
+        def turns(dst, rows):
+            return [
+                (dst[:, u, a * P : (a + 1) * P], rows[:, a, :].bitcast(F32)[:, u : 2 * P : 2]) for a in (0, 1) for u in (0, 1)
+            ]
+
+        def turn(pair):
+            nc.tensor.transpose(pair[0], pair[1], ident[:])
+
+        def fill_x(j):
+            for pair in turns(bank(("x", j), [P, 2, 2 * P], F32), xs[j]):
+                turn(pair)
+
+        def fill_wb(n, h):
+            for pair in turns(bank(("wb", n, h), [P, 2, 2 * P], F32), wbr[n][:, 2 * h : 2 * h + 2, :]):
+                turn(pair)
+
+        def fill_h(u, t):
+            g, n = divmod(u, 2)
+            nc.tensor.matmul_mx(
+                out=bank(("h", u, t), [P, T], F32)[:],
+                lhsT=w1p[:, n, t].rearrange("p m b -> p (m b)").bitcast(FP4X4),
+                lhsT_scale=wsp[:, n, t, :],
+                rhs=xc[g].bitcast(FP8X4),
+                rhs_scale=xsc[g],
+                start=True,
+                stop=True,
+            )
+
+        def fill_y(n):
+            u, a = divmod(n, 4)
+            cols = slice(a * P, (a + 1) * P)
+            nc.tensor.matmul_mx(
+                out=bank(("y", n), [P, BLK], F32)[:],
+                lhsT=hc[u][:, cols].bitcast(FP8X4),
+                lhsT_scale=hs[u][:, cols],
+                rhs=wbc[u % 2][:].bitcast(FP8X4),
+                rhs_scale=wbs[u % 2][:],
+                start=True,
+                stop=True,
+            )
+
+        def fill_woven(u, j, halves):
+            pairs = []
+            for a in range(2 * halves[0], 2 * halves[-1] + 2):
+                if a % 2 == 0:
+                    dst = bank(("e", u, a // 2), [P, 2, P, 4], BF16)
+                nc.tensor.matmul(
+                    out=dst[:, a % 2].rearrange("p r t -> p (r t)"),
+                    lhsT=identb[:],
+                    rhs=hp[u][:, :, a * P : (a + 1) * P].rearrange("p t r -> p r t"),
+                    start=True,
+                    stop=True,
+                )
+                if live(j):
+                    if a == 0:
+                        pairs = turns(bank(("x", j), [P, 2, 2 * P], F32), xs[j])
+                    turn(pairs[a])
 
         def widen_x(j):
             if live(j):
                 xs[j] = work.tile([P, 2, IN], BF16, name="xs", tag="xs", bufs=5)
                 src = xb[j // 2][:, 2 * (j % 2) : 2 * (j % 2) + 2, :].rearrange("p a k -> p (a k)").bitcast(FP8)
-                dst = xs[j][:].rearrange("p a k -> p (a k)")
-                nc.scalar.copy(out=dst, in_=src)
-
-        def bank(tag):
-            return psum.tile([P, 2, 2 * P], F32, name="bank", tag=tag, bufs=BANKS[tag])
-
-        def turn_x(j, tag="xt"):
-            if live(j):
-                xt[j] = bank(tag)
-                turn(xt[j], xs[j])
+                nc.scalar.copy(out=xs[j][:].rearrange("p a k -> p (a k)"), in_=src)
 
         def scale_x(j):
-            if live(j):
-                g, h = divmod(j, 2)
-                if h == 0:
-                    xg[g] = work.tile([P, T, 4], BF16, name="xg", tag="xg", align_bytes=64, bufs=2)
-                nc.vector.tensor_tensor(
-                    out=xg[g][:, 2 * P * h : 2 * P * (h + 1), :].rearrange("p r (u e) -> p r u e", u=2),
-                    in0=xt[j][:].bitcast(BF16).rearrange("p u (r e) -> p r u e", e=2),
-                    in1=sc[:].rearrange("p (u e) -> p u e", u=2).unsqueeze(1).to_broadcast([P, 2 * P, 2, 2]),
-                    op=ALU.mult,
-                )
+            g, h = divmod(j, 2)
+            if h == 0:
+                xg[g] = joint(2 * g - X_LAG)[:, 1] if partner(2 * g - X_LAG) == g else single("xg")[:]
+            nc.vector.tensor_tensor(
+                out=xg[g][:, 2 * P * h : 2 * P * (h + 1), :].rearrange("p r (u e) -> p r u e", u=2),
+                in0=filled["x", j][:].bitcast(BF16).rearrange("p u (r e) -> p r u e", e=2),
+                in1=sc[:].rearrange("p (u e) -> p u e", u=2).unsqueeze(1).to_broadcast([P, 2 * P, 2, 2]),
+                op=ALU.mult,
+            )
 
-        def quant_x(j, halves=1):
-            if live(j):
-                g, h = divmod(j, 2)
-                if h == 0:
-                    xc[g] = work.tile([P, T], U32, name="xc", tag="xc", align_bytes=64, bufs=4)
-                    xsc[g] = work.tile([P, T], U8, name="xsc", tag="xsc", align_bytes=64, bufs=4)
-                cols = slice(2 * P * h, 2 * P * (h + halves))
-                quantize(xg[g][:, cols, :], xc[g][:, cols], xsc[g][:, cols])
-
-        def stage1(u, t):
-            if live(u):
-                g, n = divmod(u, 2)
-                hacc[u, t] = psum.tile([P, T], F32, name="h", tag="h", bufs=4)
-                nc.tensor.matmul_mx(
-                    out=hacc[u, t][:],
-                    lhsT=w1p[:, n, t].rearrange("p m b -> p (m b)").bitcast(FP4X4),
-                    lhsT_scale=wsp[:, n, t, :],
-                    rhs=xc[g][:].bitcast(FP8X4),
-                    rhs_scale=xsc[g][:],
-                    start=True,
-                    stop=True,
-                )
+        def quant_x(g):
+            codes, scales = code_tiles(T, "x", 3)
+            xc[g], xsc[g] = codes[:], scales[:]
+            quantize(xg[g].rearrange("p r t -> p (r t)"), xc[g], xsc[g])
 
         def relu_h(u, t):
-            if live(u):
-                if t == 0:
-                    hp[u] = work.tile([P, 4, T], BF16, name="hp", tag="hp")
-                nc.scalar.activation(out=hp[u][:, t, :], in_=hacc[u, t][:], func=ACT.Relu, bias=b1c[:, u % 2, t : t + 1])
+            if t == 0:
+                hp[u] = work.tile([P, 4, T], BF16, name="hp", tag="hp")
+            nc.scalar.activation(out=hp[u][:, t, :], in_=filled["h", u, t][:], func=ACT.Relu, bias=b1c[:, u % 2, t : t + 1])
 
-        def gpsimd_tokens(u):
-            return 2 * P if u == 0 else T
+        def unload_e(u, half):
+            if half == 0:
+                hg[u] = joint(u)[:, 0] if partner(u) is not None else single("hw")[:]
+            copy = nc.vector.tensor_copy if half == 1 and V_FROM <= u < V_TO else nc.scalar.copy
+            copy(
+                out=hg[u][:, 2 * P * half : 2 * P * (half + 1), :].rearrange("p r t -> p (r t)"),
+                in_=filled["e", u, half][:].rearrange("p a r t -> p (a r t)"),
+            )
 
         def interleave_gpsimd(u):
-            if live(u):
-                cut = gpsimd_tokens(u)
-                hg[u] = work.tile([P, cut, 4], BF16, name="hg", tag="hg", align_bytes=64, bufs=1)
-                nc.gpsimd.tensor_scalar(
-                    out=hg[u][:],
-                    in0=hp[u][:, :, :cut].rearrange("p t r -> p r t"),
-                    scalar1=1.0,
-                    scalar2=0.0,
-                    op0=ALU.mult,
-                    op1=ALU.add,
-                )
+            cut = 2 * P if u == 0 else T
+            hg[u] = work.tile([P, cut, 4], BF16, name="hg", tag="hg", align_bytes=64, bufs=1)[:]
+            nc.gpsimd.tensor_scalar(
+                out=hg[u], in0=hp[u][:, :, :cut].rearrange("p t r -> p r t"), scalar1=1.0, scalar2=0.0, op0=ALU.mult, op1=ALU.add
+            )
 
-        def interleave_vector(u):
-            if live(u) and gpsimd_tokens(u) < T:
-                cut = gpsimd_tokens(u)
-                hv[u] = work.tile([P, T - cut, 4], BF16, name="hv", tag="hv", align_bytes=64, bufs=1)
-                nc.vector.tensor_copy(
-                    out=hv[u][:].rearrange("p (c i) t -> p c t i", i=4),
-                    in_=hp[u][:, :, cut:].rearrange("p t (c i) -> p c t i", i=4),
-                )
+        def interleave_vector():
+            both["rest"] = work.tile([P, 2 * P, 4], BF16, name="rest", tag="rest", align_bytes=64, bufs=1)
+            nc.vector.tensor_copy(
+                out=both["rest"][:].rearrange("p (c i) t -> p c t i", i=4),
+                in_=hp[0][:, :, 2 * P :].rearrange("p t (c i) -> p c t i", i=4),
+            )
 
         def quant_h(u):
-            if live(u):
-                cut = gpsimd_tokens(u)
-                hc[u] = work.tile([P, T], U32, name="hc", tag="hc", align_bytes=64, bufs=4)
-                hs[u] = work.tile([P, T], U8, name="hs", tag="hs", align_bytes=64, bufs=4)
-                if cut < T:
-                    quantize(hv[u][:], hc[u][:, cut:], hs[u][:, cut:])
-                quantize(hg[u][:], hc[u][:, :cut], hs[u][:, :cut])
-
-        def stage2(u, a):
-            if live(u):
-                n = u % 2
-                y[u, a] = bank(y_tag(4 * u + a))[:].rearrange("p u r -> p (u r)")
-                cols = slice(a * P, (a + 1) * P)
-                nc.tensor.matmul_mx(
-                    out=y[u, a],
-                    lhsT=hc[u][:, cols].bitcast(FP8X4),
-                    lhsT_scale=hs[u][:, cols],
-                    rhs=wbc[n][:].bitcast(FP8X4),
-                    rhs_scale=wbs[n][:],
-                    start=True,
-                    stop=True,
-                )
+            g = partner(u)
+            codes, scales = code_tiles(T, "h", 4) if g is None else code_tiles(2 * T, "joint", 3)
+            hc[u], hs[u] = codes[:, :T], scales[:, :T]
+            if g is not None:
+                xc[g], xsc[g] = codes[:, T:], scales[:, T:]
+                quantize(joint(u)[:].rearrange("p s r t -> p (s r t)"), codes[:], scales[:])
+            elif u == 0:
+                quantize(both["rest"][:].rearrange("p r t -> p (r t)"), codes[:, 2 * P :], scales[:, 2 * P :])
+                quantize(hg[u].rearrange("p r t -> p (r t)"), codes[:, : 2 * P], scales[:, : 2 * P])
+            else:
+                quantize(hg[u].rearrange("p r t -> p (r t)"), hc[u], hs[u])
 
         def ring_columns(c0, c1):
             start = c0 % (RING * BLK)
             return ring[:, start : start + c1 - c0]
 
-        def bias_y(u, a, lo, hi):
-            bias = bbr[:, u % 2 * BLK + lo : u % 2 * BLK + hi]
-            nc.vector.tensor_tensor(out=ring_columns((4 * u + a) * BLK + lo, (4 * u + a) * BLK + hi), in0=y[u, a][:, lo:hi], in1=bias, op=ALU.add)
+        waiting = []
 
-        def rows_of(u):
-            g, n = divmod(u, 2)
-            return out[T * g : T * (g + 1), n * BLK : (n + 1) * BLK].rearrange("(p a) c -> p a c", a=4)
+        def bias_y(n):
+            half = n // 4 % 2
+            nc.vector.tensor_tensor(
+                out=ring_columns(n * BLK, (n + 1) * BLK), in0=filled["y", n][:], in1=bbr[:, half * BLK : (half + 1) * BLK], op=ALU.add
+            )
+            if waiting and waiting[-1][1] == n * BLK:
+                waiting[-1] = (waiting[-1][0], (n + 1) * BLK)
+            else:
+                waiting.append((n * BLK, (n + 1) * BLK))
 
         def store(u, a0, a1):
-            nc.sync.dma_start(out=rows_of(u)[:, a0:a1, :], in_=ring_columns((4 * u + a0) * BLK, (4 * u + a1) * BLK).rearrange("p (a c) -> p a c", c=BLK))
-
-        def permute_words(n):
-            nc.vector.tensor_copy(
-                out=w1p[:, n], in_=w1r[:].rearrange("p (n m t b) -> p n t m b", n=2, t=4, b=2)[:, n]
-            )
-
-        def permute_scales(n):
-            nc.vector.tensor_copy(out=wsp[:, n], in_=wsr[:].rearrange("p (n m t) -> p n t m", n=2, t=4)[:, n])
-
-        def turn_wb(n, h, tag):
-            wt[n, h] = bank(tag)
-            turn(wt[n, h], wbr[n][:, 2 * h : 2 * h + 2, :])
-
-        def unload_wb(n, h, copy):
-            cols = wbg[n][:, 2 * P * h : 2 * P * (h + 1), :].rearrange("p r t -> p (r t)").bitcast(F32)
-            copy(out=cols.rearrange("p (r u) -> p r u", u=2), in_=wt[n, h][:].rearrange("p u r -> p r u"))
-
-        def quant_wb(n):
-            quantize(wbg[n][:], wbc[n][:], wbs[n][:])
-
-        def warm():
-            idle = psum.tile([P, 2, P], F32, name="idle", tag="h", bufs=4)
-            nc.tensor.matmul(
-                out=idle[:], lhsT=ident[:], rhs=ident[:].unsqueeze(1).to_broadcast([P, 2, P]), start=True, stop=True
-            )
-
-        warm()
-        warm()
-        widen_x(0)
-        widen_x(1)
-        turn_x(0)
-        turn_x(1, "y")
-        warm()
-        permute_words(0)
-        permute_words(1)
-        widen_x(2)
-        widen_x(3)
-        turn_x(2, "y")
-        turn_x(3, "y")
-        warm()
-        scale_x(0)
-        scale_x(1)
-        permute_scales(0)
-        quant_x(0, 2)
-        for j in range(4, 8):
-            widen_x(j)
-        for t in range(4):
-            stage1(0, t)
-        turn_x(4)
-        turn_x(5, "y")
-        scale_x(2)
-        scale_x(3)
-        permute_scales(1)
-        quant_x(2, 2)
-        for t in range(4):
-            relu_h(0, t)
-        for h in range(2):
-            stage1(1, 2 * h)
-            stage1(1, 2 * h + 1)
-            turn_wb(0, h, "y")
-        for h in range(2):
-            relu_h(1, 2 * h)
-            relu_h(1, 2 * h + 1)
-            unload_wb(0, h, nc.scalar.copy)
-        interleave_gpsimd(0)
-        scale_x(4)
-        turn_x(6)
-        stage1(2, 0)
-        stage1(2, 1)
-        scale_x(5)
-        turn_wb(1, 0, "y")
-        stage1(2, 2)
-        stage1(2, 3)
-        interleave_vector(0)
-        quant_x(4, 2)
-        quant_h(0)
-        quant_wb(0)
-        widen_x(8)
-        unload_wb(1, 0, nc.scalar.copy)
-        widen_x(9)
+            g, n = divmod(u, 2)
+            rows = out[T * g : T * (g + 1), n * BLK : (n + 1) * BLK].rearrange("(p a) c -> p a c", a=4)
+            cols = ring_columns((4 * u + a0) * BLK, (4 * u + a1) * BLK)
+            nc.sync.dma_start(out=rows[:, a0:a1, :], in_=cols.rearrange("p (a c) -> p a c", c=BLK))
 
         def cut(c0, c1, width):
             return [(j, max(c0 - width * j, 0), min(c1 - width * j, width)) for j in range(c0 // width, -(-c1 // width))]
 
-        cleared = [0] * (4 * UNITS)
+        cleared = [0] * TILES
 
         def relu(engine, c0, c1):
             for j, lo, hi in cut(c0, c1, RING * BLK):
                 part = ring[:, lo:hi]
                 if engine == "vector":
                     nc.vector.tensor_scalar(out=part, in0=part, scalar1=0.0, scalar2=None, op0=ALU.max)
+                elif engine == "gpsimd":
+                    nc.gpsimd.tensor_scalar(out=part, in0=part, scalar1=BIG, scalar2=0.0, op0=ALU.min, op1=ALU.max)
                 else:
                     nc.scalar.activation(out=part, in_=part, func=ACT.Relu)
             done = []
@@ -314,101 +293,164 @@ def tile_blockdiagmnistconvertible_pa_t_w4_kernel(tc, x_bytes, x_scale, W1_words
                 if cleared[n] == BLK:
                     done.append(n)
             if done:
-                for u, lo, hi in cut(done[0], done[-1] + 1, 4):
-                    store(u, lo, hi)
+                for v, v0, v1 in cut(done[0], done[-1] + 1, 2):
+                    for r, r0, r1 in cut(2 * v + v0, 2 * v + v1, RING):
+                        store(v // 2, (RING * r + r0) % 4, (RING * r + r1 - 1) % 4 + 1)
 
-        def relu_by_tile(c0, c1):
-            for n, lo, hi in cut(c0, c1, BLK):
-                relu("scalar", n * BLK + lo, n * BLK + hi)
+        def relu_newest(engine, cols):
+            if waiting:
+                c0, c1 = waiting.pop()
+                if c1 - c0 > cols:
+                    waiting.append((c0, c1 - cols))
+                relu(engine, max(c0, c1 - cols), c1)
 
-        first = [0, 3 * BLK]
-        for s in range(1, UNITS - 1):
-            first.append(first[-1] + (X_SLOT_COLS if live(s + LEAD) else LATE_SLOT_COLS))
-        first.append(4 * UNITS * BLK)
-        multiplied = []
-        x_done = first[UNITS - LEAD] // BLK + 3
+        def relu_oldest(engine, cols):
+            if waiting and cols:
+                c0, c1 = waiting.pop(0)
+                if c1 - c0 > cols:
+                    waiting.insert(0, (c0 + cols, c1))
+                relu(engine, c0, min(c1, c0 + cols))
 
-        def y_tag(n):
-            if n >= 4 * (UNITS - 1):
-                return "h"
-            return "xt" if n >= x_done and (n - x_done) % 4 == 0 else "y"
+        def permute_words(n):
+            nc.vector.tensor_copy(out=w1p[:, n], in_=w1r[:].rearrange("p (n m t b) -> p n t m b", n=2, t=4, b=2)[:, n])
 
-        def multiply_ahead(n, s):
-            ahead = 4 if n + 3 >= x_done else 3
-            for m in range(len(multiplied), min(n + ahead, 4 * (s + 1))):
-                stage2(m // 4, m % 4)
-                multiplied.append(m)
+        def permute_scales(n):
+            nc.vector.tensor_copy(out=wsp[:, n], in_=wsr[:].rearrange("p (n m t) -> p n t m", n=2, t=4)[:, n])
+            permuted.add(n)
 
-        def empty(piece, s):
-            n, lo, hi = piece
-            bias_y(n // 4, n % 4, lo, hi)
-            if hi == BLK:
-                multiply_ahead(n + 1, s)
+        def unload_wb(n, h):
+            if h == 0:
+                wbg[n] = work.tile([P, BLK, 4], BF16, name="wbg", tag="wbg", align_bytes=64, bufs=1)
+            cols = wbg[n][:, 2 * P * h : 2 * P * (h + 1), :].rearrange("p r t -> p (r t)").bitcast(F32)
+            nc.scalar.copy(out=cols.rearrange("p (r u) -> p r u", u=2), in_=filled["wb", n, h][:].rearrange("p u r -> p r u"))
 
-        def on_vector(s):
-            if live(s + LEAD):
-                return 512 if live(s + WIDEN_LEAD) else 384
-            return 1024 if live(s + 3) else 768
+        made = set()
 
-        def slot(s):
-            c0, c1 = first[s], first[s + 1]
-            pieces = cut(c0, c1, BLK)
-            before_x = 1 if s > 0 else 0
-            interleave_gpsimd(s + 1)
-            multiply_ahead(c0 // BLK if s < UNITS - 1 else 4 * UNITS, s)
-            for piece in pieces[:before_x]:
-                empty(piece, s)
-            scale_x(s + LEAD)
-            left = first[s - 1] + on_vector(s - 1) if s > 0 else 0
-            if live(s + 2) and not live(s + LEAD):
-                relu("scalar", left, left + EARLY_COLS)
-                left = left + EARLY_COLS
-            last_h = s + 2 == UNITS - 1
-            for t in range(2 if last_h else 4):
-                relu_h(s + 2, t)
-                if s == 0 and t == 1:
-                    turn_wb(1, 1, "xt")
-                    unload_wb(1, 1, nc.scalar.copy)
-            if s > 0 and live(s + 2):
-                relu("scalar", left, c0)
-            stage1(s + 3, 0)
-            stage1(s + 3, 1)
-            empty(pieces[before_x], s)
-            turn_x(s + LEAD + 1)
-            widen_x(s + WIDEN_LEAD)
-            empty(pieces[before_x + 1], s)
-            stage1(s + 3, 2)
-            stage1(s + 3, 3)
-            for piece in pieces[before_x + 2 :]:
-                empty(piece, s)
-            if s == UNITS - 1:
-                relu_by_tile(c0, c1 - BLK)
-                relu("vector", c1 - BLK, c1)
-                return
-            mine = c0 + on_vector(s)
-            if last_h:
-                split = (mine + 1024) // BLK * BLK
-                relu_by_tile(mine, split)
-                relu_h(s + 2, 2)
-                relu_h(s + 2, 3)
-            elif not live(s + 3):
-                split = (c1 - BLK) // BLK * BLK
-                relu_by_tile(mine, split)
-            if s == 0:
-                relu("vector", c0, mine)
-                quant_x(s + LEAD)
-                quant_h(s + 1)
-                quant_wb(1)
-            elif live(s + LEAD):
-                relu("vector", c0, mine)
-                quant_h(s + 1)
-                quant_x(s + LEAD)
-            else:
-                relu("vector", c0, (c0 + mine) // 2)
-                quant_h(s + 1)
-                relu("vector", (c0 + mine) // 2, mine)
-            if not live(s + 3):
-                relu_by_tile(split, c1)
+        def warm():
+            key = ("idle", len(order))
+            idle = bank(key, [P, 2, P], F32)
+            nc.tensor.matmul(out=idle[:], lhsT=ident[:], rhs=ident[:].unsqueeze(1).to_broadcast([P, 2, P]), start=True, stop=True)
+            emptied.add(key)
 
+        def quant_wb(n):
+            quantize(wbg[n][:].rearrange("p r t -> p (r t)"), wbc[n][:], wbs[n][:])
+            made.add(n)
+
+        def x_of(s):
+            return s + HEAD_X - (s >= SKIP) if s != SKIP else -1
+
+        def do(f, *args):
+            return (None, lambda: f(*args))
+
+        def X(j):
+            return [(("x", j), lambda: scale_x(j))] if live(j) else []
+
+        def H(u, *planes):
+            return [(("h", u, t), lambda t=t: relu_h(u, t)) for t in planes] if live(u) else []
+
+        def E(u, half):
+            return [(("e", u, half), lambda: unload_e(u, half))] if FIRST_PE <= u < UNITS else []
+
+        def W(n, h):
+            return [(("wb", n, h), lambda: unload_wb(n, h))]
+
+        def R(count):
+            return [do(relu_oldest, "scalar", BLK)] * count
+
+        def tiles_of(s):
+            if s + 1 < FIRST_PE:
+                return 3
+            if live(x_of(s)):
+                return JOINT_TILES if partner(s) is not None else X_TILES
+            return LATE_TILES
+
+        taken = []
+
+        def Y(count):
+            first = len(taken)
+            taken.extend(range(first, min(first + count, TILES)))
+            return [(("y", n), lambda n=n: bias_y(n)) for n in taken[first:]]
+
+        steps = [do(warm), do(warm), do(widen_x, 0), do(widen_x, 1), do(permute_words, 0), do(warm), do(permute_words, 1)]
+        steps += [do(widen_x, 2), do(widen_x, 3), do(warm)]
+        steps += X(0) + [do(widen_x, 4)] + X(1) + [do(permute_scales, 0), do(quant_x, 0)]
+        steps += X(2) + [do(widen_x, 5), do(widen_x, 6)] + X(3) + [do(widen_x, 7), do(permute_scales, 1)] + H(0, 0, 1) + [do(quant_x, 1)]
+        steps += H(0, 2, 3) + X(4) + [do(interleave_gpsimd, 0)] + H(1, 0, 1) + X(5) + W(0, 0) + [do(interleave_vector)]
+        steps += H(1, 2, 3) + [do(quant_x, 2)] + W(0, 1) + [do(widen_x, 8), do(widen_x, 9)]
         for s in range(UNITS):
-            slot(s)
+            j = x_of(s)
+            with_x = live(j)
+            count = tiles_of(s)
+            steps += [do(quant_h, s)]
+            if s < 2:
+                steps += [do(quant_wb, s)]
+            if s == 2:
+                steps += [do(quant_x, 3)]
+            if s + 1 < FIRST_PE:
+                steps += [do(interleave_gpsimd, s + 1)]
+            else:
+                steps += [do(relu_newest, "gpsimd", G_TILE * count + (G_X if with_x else 0) - G_FIX if live(s + 2) else G_END)]
+            if s == UNITS - 1:
+                break
+            if s == 0:
+                steps += H(2, 0) + X(j) + H(2, 1, 2) + Y(1) + W(1, 0) + Y(1) + W(1, 1) + Y(1) + H(2, 3)
+            elif with_x:
+                steps += H(s + 2, 0, 1) + Y(1) + H(s + 2, 2) + Y(count - 2) + E(s + 1, 0) + X(j) + E(s + 1, 1) + H(s + 2, 3) + Y(1)
+            elif live(s + 2):
+                steps += H(s + 2, 0, 1) + Y(1) + H(s + 2, 2) + Y(1) + E(s + 1, 0) + Y(count - 3) + E(s + 1, 1) + H(s + 2, 3) + Y(1)
+            else:
+                steps += R(1) + Y(1) + E(s + 1, 0) + Y(1) + E(s + 1, 1)
+                for c in range(count - 2):
+                    steps += R(1) + Y(1)
+            steps += [do(widen_x, s + HEAD_WIDE)]
+            steps += [do(relu_oldest, "scalar", S_EARLY if s + 2 < FIRST_PE else S_X if with_x else S_LATE)]
+        while len(taken) < TILES - 1:
+            steps += R(1) + Y(1)
+        steps += R(1) + Y(1) + [do(relu_newest, "vector", BLK)] + R(8)
+
+        keys = [key for key, run in steps if key is not None]
+
+        def woven_x(u):
+            return x_of(u - 1)
+
+        def fill_next():
+            for key in keys:
+                if key not in filled:
+                    break
+            else:
+                return False
+            kind = key[0]
+            need = 1
+            if kind == "x":
+                ready = key[1] in xs
+            elif kind == "h":
+                ready = key[1] // 2 in xc and key[1] % 2 in permuted
+            elif kind == "y":
+                ready = key[1] // 4 in hc and key[1] // 4 % 2 in made
+            elif kind == "e":
+                ready = ("h", key[1], 3) in emptied
+                need = 3 if live(woven_x(key[1])) else 1
+            else:
+                ready = True
+            for k in range(len(order), len(order) + need):
+                ready = ready and (k < BANKS or order[k - BANKS] in emptied)
+            if not ready:
+                return False
+            if kind == "x":
+                fill_x(key[1])
+            elif kind == "h":
+                fill_h(key[1], key[2])
+            elif kind == "y":
+                fill_y(key[1])
+            elif kind == "e":
+                fill_woven(key[1], woven_x(key[1]), (0, 1) if need > 1 else key[2:])
+            else:
+                fill_wb(key[1], key[2])
+            return True
+
+        for key, run in steps:
+            while fill_next():
+                pass
+            run()
+            emptied.add(key)
+        assert not waiting

@@ -23,24 +23,38 @@ GROUPS = B // T
 UNITS = 2 * GROUPS
 TILES = 4 * UNITS
 BANKS = 8
-RING = 56
+RING = 64
 HEAD_X = 6
 HEAD_WIDE = 10
 FIRST_PE = 4
-X_LAG = 4
-SKIP = 99
-X_TILES = 4
-LATE_TILES = 5
-G_TILE = 512
-G_X = 1024
-G_FIX = 384
-G_END = 1536
-V_FROM = 99
-V_TO = 15
-JOINT_TILES = 3
-S_EARLY = 896
-S_X = 0
-S_LATE = 384
+EVERY = 2
+LAST_PE = 10
+A_X = 2048
+AA_X = 1536
+B_X = 1536
+A_LATE = 2688
+B_LATE = 2560
+G_X = 2176
+G_LATE = 2304
+S_EARLY = 640
+S_WIDE = 640
+S_A = 1536
+S_B = 1024
+S_A_LATE = 1024
+S_B_LATE = 512
+S_FIRST = 512
+S_SECOND = 512
+V_END = 640
+END_A = 58
+V_TURN = 1024
+V_LATE = 4096
+V_X = 0
+V_WIDE = 384
+V_BEFORE = 0
+PAIRED_FROM = 7
+SPLIT_FROM = 14
+LAST_CUT = 256
+G_END = 1024
 BIG = 3.0e38
 
 
@@ -72,7 +86,7 @@ def tile_blockdiagmnistconvertible_pa_t_w4_kernel(tc, x_bytes, x_scale, W1_words
             nc.sync.dma_start(out=xb[g][:], in_=x_bytes[T * g : T * (g + 1), :].rearrange("(p a) k -> p a k", a=4))
 
         def load_wb(n):
-            nc.sync.dma_start(out=wbr[n][:], in_=Wb[n].rearrange("(a p) k -> p a k", p=P))
+            nc.sync.dma_start(out=wbr[n][:], in_=Wb[n].rearrange("(p a) k -> p a k", a=4))
 
         nc.vector.memset(wsr[:].bitcast(I32), 0)
         make_identity(nc, ident[:])
@@ -88,8 +102,8 @@ def tile_blockdiagmnistconvertible_pa_t_w4_kernel(tc, x_bytes, x_scale, W1_words
         load_x(2)
         load_x(3)
         nc.sync.dma_start(out=b1c[:], in_=b1.rearrange("(n p t) -> p n t", n=2, t=4))
-        load_wb(0)
         load_x(4)
+        load_wb(0)
         load_wb(1)
         nc.sync.dma_start(out=bbr[:], in_=bb.partition_broadcast(P))
         for g in range(5, GROUPS):
@@ -100,19 +114,12 @@ def tile_blockdiagmnistconvertible_pa_t_w4_kernel(tc, x_bytes, x_scale, W1_words
         filled = {}
         order = []
         emptied = set()
-        permuted = set()
 
         def live(u):
             return 0 <= u < UNITS
 
-        def partner(u):
-            g = (u + X_LAG) // 2
-            return g if u >= FIRST_PE and (u + X_LAG) % 2 == 0 and g < GROUPS else None
-
-        def joint(u):
-            if u not in both:
-                both[u] = work.tile([P, 2, T, 4], BF16, name="joint", tag="joint", align_bytes=64, bufs=2)
-            return both[u]
+        def by_pe(u):
+            return live(u) and FIRST_PE <= u <= LAST_PE and (u - FIRST_PE) % EVERY == 0
 
         def single(name):
             return work.tile([P, T, 4], BF16, name=name, tag="single", align_bytes=64, bufs=2)
@@ -146,47 +153,62 @@ def tile_blockdiagmnistconvertible_pa_t_w4_kernel(tc, x_bytes, x_scale, W1_words
             for pair in turns(bank(("wb", n, h), [P, 2, 2 * P], F32), wbr[n][:, 2 * h : 2 * h + 2, :]):
                 turn(pair)
 
+        def by_tokens(u):
+            return u >= SPLIT_FROM
+
+        def parts(u):
+            if by_tokens(u):
+                return [(n, slice(2 * P * n, 2 * P * (n + 1)), slice(2 * P * (u % 2), 2 * P * (u % 2 + 1))) for n in (0, 1)]
+            return [(u % 2, slice(0, T), slice(0, T))]
+
         def fill_h(u, t):
-            g, n = divmod(u, 2)
-            nc.tensor.matmul_mx(
-                out=bank(("h", u, t), [P, T], F32)[:],
-                lhsT=w1p[:, n, t].rearrange("p m b -> p (m b)").bitcast(FP4X4),
-                lhsT_scale=wsp[:, n, t, :],
-                rhs=xc[g].bitcast(FP8X4),
-                rhs_scale=xsc[g],
-                start=True,
-                stop=True,
-            )
+            acc = bank(("h", u, t), [P, T], F32)
+            for n, cols, tokens in parts(u):
+                nc.tensor.matmul_mx(
+                    out=acc[:, cols],
+                    lhsT=w1p[:, n, t].rearrange("p m b -> p (m b)").bitcast(FP4X4),
+                    lhsT_scale=wsp[:, n, t, :],
+                    rhs=xc[u // 2][:, tokens].bitcast(FP8X4),
+                    rhs_scale=xsc[u // 2][:, tokens],
+                    start=True,
+                    stop=True,
+                )
+
+        def whole_rows(g):
+            return g >= PAIRED_FROM
+
+        def place(n):
+            g, r = divmod(n, 8)
+            if by_tokens(2 * g):
+                return 2 * g + r // 4, r % 2, (r % 2 * 2 + r % 4 // 2) * P
+            if whole_rows(g):
+                return 2 * g + r % 2, r % 2, r // 2 * P
+            return n // 4, n // 4 % 2, n % 4 * P
 
         def fill_y(n):
-            u, a = divmod(n, 4)
-            cols = slice(a * P, (a + 1) * P)
+            u, chunk, first = place(n)
+            cols = slice(first, first + P)
             nc.tensor.matmul_mx(
                 out=bank(("y", n), [P, BLK], F32)[:],
                 lhsT=hc[u][:, cols].bitcast(FP8X4),
                 lhsT_scale=hs[u][:, cols],
-                rhs=wbc[u % 2][:].bitcast(FP8X4),
-                rhs_scale=wbs[u % 2][:],
+                rhs=wbc[chunk][:].bitcast(FP8X4),
+                rhs_scale=wbs[chunk][:],
                 start=True,
                 stop=True,
             )
 
-        def fill_woven(u, j, halves):
-            pairs = []
-            for a in range(2 * halves[0], 2 * halves[-1] + 2):
-                if a % 2 == 0:
-                    dst = bank(("e", u, a // 2), [P, 2, P, 4], BF16)
-                nc.tensor.matmul(
-                    out=dst[:, a % 2].rearrange("p r t -> p (r t)"),
-                    lhsT=identb[:],
-                    rhs=hp[u][:, :, a * P : (a + 1) * P].rearrange("p t r -> p r t"),
-                    start=True,
-                    stop=True,
-                )
-                if live(j):
-                    if a == 0:
-                        pairs = turns(bank(("x", j), [P, 2, 2 * P], F32), xs[j])
-                    turn(pairs[a])
+        def fill_m(u, a):
+            if a % 2 == 0:
+                bank(("e", u, a // 2), [P, 2, P, 4], BF16)
+            filled["m", u, a] = filled["e", u, a // 2]
+            nc.tensor.matmul(
+                out=filled["m", u, a][:, a % 2].rearrange("p r t -> p (r t)"),
+                lhsT=identb[:],
+                rhs=hp[u][:, :, a * P : (a + 1) * P].rearrange("p t r -> p r t"),
+                start=True,
+                stop=True,
+            )
 
         def widen_x(j):
             if live(j):
@@ -197,7 +219,7 @@ def tile_blockdiagmnistconvertible_pa_t_w4_kernel(tc, x_bytes, x_scale, W1_words
         def scale_x(j):
             g, h = divmod(j, 2)
             if h == 0:
-                xg[g] = joint(2 * g - X_LAG)[:, 1] if partner(2 * g - X_LAG) == g else single("xg")[:]
+                xg[g] = single("xg")[:]
             nc.vector.tensor_tensor(
                 out=xg[g][:, 2 * P * h : 2 * P * (h + 1), :].rearrange("p r (u e) -> p r u e", u=2),
                 in0=filled["x", j][:].bitcast(BF16).rearrange("p u (r e) -> p r u e", e=2),
@@ -213,23 +235,33 @@ def tile_blockdiagmnistconvertible_pa_t_w4_kernel(tc, x_bytes, x_scale, W1_words
         def relu_h(u, t):
             if t == 0:
                 hp[u] = work.tile([P, 4, T], BF16, name="hp", tag="hp")
-            nc.scalar.activation(out=hp[u][:, t, :], in_=filled["h", u, t][:], func=ACT.Relu, bias=b1c[:, u % 2, t : t + 1])
+            for n, cols, tokens in parts(u):
+                nc.scalar.activation(out=hp[u][:, t, cols], in_=filled["h", u, t][:, cols], func=ACT.Relu, bias=b1c[:, n, t : t + 1])
 
         def unload_e(u, half):
             if half == 0:
-                hg[u] = joint(u)[:, 0] if partner(u) is not None else single("hw")[:]
-            copy = nc.vector.tensor_copy if half == 1 and V_FROM <= u < V_TO else nc.scalar.copy
-            copy(
+                hg[u] = work.tile([P, T, 4], BF16, name="hw", tag="hw", align_bytes=64, bufs=2)[:]
+            nc.scalar.copy(
                 out=hg[u][:, 2 * P * half : 2 * P * (half + 1), :].rearrange("p r t -> p (r t)"),
                 in_=filled["e", u, half][:].rearrange("p a r t -> p (a r t)"),
             )
 
         def interleave_gpsimd(u):
             cut = 2 * P if u == 0 else T
-            hg[u] = work.tile([P, cut, 4], BF16, name="hg", tag="hg", align_bytes=64, bufs=1)[:]
+            if u > 1:
+                hg[u] = hg[u - 1]
+            else:
+                hg[u] = work.tile([P, cut, 4], BF16, name="hg", tag="hg", align_bytes=64, bufs=1)[:]
             nc.gpsimd.tensor_scalar(
                 out=hg[u], in0=hp[u][:, :, :cut].rearrange("p t r -> p r t"), scalar1=1.0, scalar2=0.0, op0=ALU.mult, op1=ALU.add
             )
+
+        def interleave_last():
+            u = UNITS - 1
+            hg[u] = hg[u - 1]
+            planes = hp[u][:].rearrange("p t r -> p r t")
+            nc.gpsimd.tensor_scalar(out=hg[u][:, :LAST_CUT], in0=planes[:, :LAST_CUT], scalar1=1.0, scalar2=0.0, op0=ALU.mult, op1=ALU.add)
+            nc.scalar.copy(out=hg[u][:, LAST_CUT:], in_=planes[:, LAST_CUT:])
 
         def interleave_vector():
             both["rest"] = work.tile([P, 2 * P, 4], BF16, name="rest", tag="rest", align_bytes=64, bufs=1)
@@ -239,13 +271,9 @@ def tile_blockdiagmnistconvertible_pa_t_w4_kernel(tc, x_bytes, x_scale, W1_words
             )
 
         def quant_h(u):
-            g = partner(u)
-            codes, scales = code_tiles(T, "h", 4) if g is None else code_tiles(2 * T, "joint", 3)
-            hc[u], hs[u] = codes[:, :T], scales[:, :T]
-            if g is not None:
-                xc[g], xsc[g] = codes[:, T:], scales[:, T:]
-                quantize(joint(u)[:].rearrange("p s r t -> p (s r t)"), codes[:], scales[:])
-            elif u == 0:
+            codes, scales = code_tiles(T, "h", 5)
+            hc[u], hs[u] = codes[:], scales[:]
+            if u == 0:
                 quantize(both["rest"][:].rearrange("p r t -> p (r t)"), codes[:, 2 * P :], scales[:, 2 * P :])
                 quantize(hg[u].rearrange("p r t -> p (r t)"), codes[:, : 2 * P], scales[:, : 2 * P])
             else:
@@ -257,21 +285,31 @@ def tile_blockdiagmnistconvertible_pa_t_w4_kernel(tc, x_bytes, x_scale, W1_words
 
         waiting = []
 
-        def bias_y(n):
-            half = n // 4 % 2
-            nc.vector.tensor_tensor(
-                out=ring_columns(n * BLK, (n + 1) * BLK), in0=filled["y", n][:], in1=bbr[:, half * BLK : (half + 1) * BLK], op=ALU.add
-            )
-            if waiting and waiting[-1][1] == n * BLK:
-                waiting[-1] = (waiting[-1][0], (n + 1) * BLK)
+        def bias_y(n, lo, hi):
+            first = place(n)[1] * BLK
+            c0, c1 = n * BLK + lo, n * BLK + hi
+            nc.vector.tensor_tensor(out=ring_columns(c0, c1), in0=filled["y", n][:, lo:hi], in1=bbr[:, first + lo : first + hi], op=ALU.add)
+            if waiting and waiting[-1][1] == c0:
+                waiting[-1] = (waiting[-1][0], c1)
             else:
-                waiting.append((n * BLK, (n + 1) * BLK))
+                waiting.append((c0, c1))
+            if hi == BLK:
+                emptied.add(("y", n))
 
         def store(u, a0, a1):
             g, n = divmod(u, 2)
             rows = out[T * g : T * (g + 1), n * BLK : (n + 1) * BLK].rearrange("(p a) c -> p a c", a=4)
             cols = ring_columns((4 * u + a0) * BLK, (4 * u + a1) * BLK)
             nc.sync.dma_start(out=rows[:, a0:a1, :], in_=cols.rearrange("p (a c) -> p a c", c=BLK))
+
+        def store_tile(n):
+            g, r = divmod(n, 8)
+            rows = out[T * g : T * (g + 1), :].rearrange("(p a) c -> p (a c)", a=4)
+            nc.sync.dma_start(out=rows[:, r * BLK : (r + 1) * BLK], in_=ring_columns(n * BLK, (n + 1) * BLK))
+
+        def store_rows(g, a0, a1):
+            rows = out[T * g : T * (g + 1), :].rearrange("(p a) c -> p (a c)", a=4)
+            nc.sync.dma_start(out=rows[:, a0 * HID : a1 * HID], in_=ring_columns((8 * g + 2 * a0) * BLK, (8 * g + 2 * a1) * BLK))
 
         def cut(c0, c1, width):
             return [(j, max(c0 - width * j, 0), min(c1 - width * j, width)) for j in range(c0 // width, -(-c1 // width))]
@@ -293,36 +331,44 @@ def tile_blockdiagmnistconvertible_pa_t_w4_kernel(tc, x_bytes, x_scale, W1_words
                 if cleared[n] == BLK:
                     done.append(n)
             if done:
-                for v, v0, v1 in cut(done[0], done[-1] + 1, 2):
-                    for r, r0, r1 in cut(2 * v + v0, 2 * v + v1, RING):
-                        store(v // 2, (RING * r + r0) % 4, (RING * r + r1 - 1) % 4 + 1)
+                for g, lo, hi in cut(done[0], done[-1] + 1, 8):
+                    if 8 * g + hi > TILES - 2:
+                        for n in range(8 * g + lo, 8 * g + hi):
+                            store_tile(n)
+                    elif whole_rows(g):
+                        whole = [a for a in range(lo // 2, (hi + 1) // 2) if cleared[8 * g + 2 * a] + cleared[8 * g + 2 * a + 1] == HID]
+                        if whole:
+                            store_rows(g, whole[0], whole[-1] + 1)
+                    else:
+                        for u, a0, a1 in cut(8 * g + lo, 8 * g + hi, 4):
+                            store(u, a0, a1)
 
         def relu_newest(engine, cols):
-            if waiting:
+            if waiting and cols:
                 c0, c1 = waiting.pop()
                 if c1 - c0 > cols:
                     waiting.append((c0, c1 - cols))
                 relu(engine, max(c0, c1 - cols), c1)
 
         def relu_oldest(engine, cols):
-            if waiting and cols:
+            while waiting and cols > 0:
                 c0, c1 = waiting.pop(0)
                 if c1 - c0 > cols:
                     waiting.insert(0, (c0 + cols, c1))
                 relu(engine, c0, min(c1, c0 + cols))
+                cols = cols - (c1 - c0)
 
-        def permute_words(n):
-            nc.vector.tensor_copy(out=w1p[:, n], in_=w1r[:].rearrange("p (n m t b) -> p n t m b", n=2, t=4, b=2)[:, n])
+        def permute_words():
+            nc.vector.tensor_copy(out=w1p[:], in_=w1r[:].rearrange("p (n m t b) -> p n t m b", n=2, t=4, b=2))
 
-        def permute_scales(n):
-            nc.vector.tensor_copy(out=wsp[:, n], in_=wsr[:].rearrange("p (n m t) -> p n t m", n=2, t=4)[:, n])
-            permuted.add(n)
+        def permute_scales():
+            nc.vector.tensor_copy(out=wsp[:], in_=wsr[:].rearrange("p (n m t) -> p n t m", n=2, t=4))
 
         def unload_wb(n, h):
             if h == 0:
-                wbg[n] = work.tile([P, BLK, 4], BF16, name="wbg", tag="wbg", align_bytes=64, bufs=1)
-            cols = wbg[n][:, 2 * P * h : 2 * P * (h + 1), :].rearrange("p r t -> p (r t)").bitcast(F32)
-            nc.scalar.copy(out=cols.rearrange("p (r u) -> p r u", u=2), in_=filled["wb", n, h][:].rearrange("p u r -> p r u"))
+                wbg[n] = work.tile([P, BLK, 4], BF16, name="wbg", tag="wbg", align_bytes=64, bufs=2)
+            words = wbg[n][:].rearrange("p o t -> p (o t)").bitcast(F32).rearrange("p (r a u) -> p r a u", a=4, u=2)
+            nc.scalar.copy(out=words[:, :, 2 * h : 2 * h + 2, :], in_=filled["wb", n, h][:].rearrange("p u (a r) -> p r a u", a=2))
 
         made = set()
 
@@ -337,7 +383,7 @@ def tile_blockdiagmnistconvertible_pa_t_w4_kernel(tc, x_bytes, x_scale, W1_words
             made.add(n)
 
         def x_of(s):
-            return s + HEAD_X - (s >= SKIP) if s != SKIP else -1
+            return s + HEAD_X
 
         def do(f, *args):
             return (None, lambda: f(*args))
@@ -349,69 +395,76 @@ def tile_blockdiagmnistconvertible_pa_t_w4_kernel(tc, x_bytes, x_scale, W1_words
             return [(("h", u, t), lambda t=t: relu_h(u, t)) for t in planes] if live(u) else []
 
         def E(u, half):
-            return [(("e", u, half), lambda: unload_e(u, half))] if FIRST_PE <= u < UNITS else []
+            return [(("e", u, half), lambda: unload_e(u, half))] if by_pe(u) else []
+
+        def M(u, *parts):
+            return [(("m", u, a), lambda: None) for a in parts] if by_pe(u) else []
 
         def W(n, h):
             return [(("wb", n, h), lambda: unload_wb(n, h))]
 
-        def R(count):
-            return [do(relu_oldest, "scalar", BLK)] * count
-
-        def tiles_of(s):
-            if s + 1 < FIRST_PE:
-                return 3
+        def columns_of(s):
+            if s < 2:
+                return 3 * BLK
             if live(x_of(s)):
-                return JOINT_TILES if partner(s) is not None else X_TILES
-            return LATE_TILES
+                return B_X if by_pe(s + 1) else A_X if by_pe(s) else AA_X
+            return B_LATE if by_pe(s + 1) else A_LATE
 
-        taken = []
+        taken = [0, 0]
 
         def Y(count):
-            first = len(taken)
-            taken.extend(range(first, min(first + count, TILES)))
-            return [(("y", n), lambda n=n: bias_y(n)) for n in taken[first:]]
+            c0 = taken[0]
+            taken[0] = min((c0 // BLK + count) * BLK, taken[1])
+            return [(("y", n), lambda n=n, lo=lo, hi=hi: bias_y(n, lo, hi)) for n, lo, hi in cut(c0, taken[0], BLK) if hi > lo]
 
-        steps = [do(warm), do(warm), do(widen_x, 0), do(widen_x, 1), do(permute_words, 0), do(warm), do(permute_words, 1)]
-        steps += [do(widen_x, 2), do(widen_x, 3), do(warm)]
-        steps += X(0) + [do(widen_x, 4)] + X(1) + [do(permute_scales, 0), do(quant_x, 0)]
-        steps += X(2) + [do(widen_x, 5), do(widen_x, 6)] + X(3) + [do(widen_x, 7), do(permute_scales, 1)] + H(0, 0, 1) + [do(quant_x, 1)]
-        steps += H(0, 2, 3) + X(4) + [do(interleave_gpsimd, 0)] + H(1, 0, 1) + X(5) + W(0, 0) + [do(interleave_vector)]
-        steps += H(1, 2, 3) + [do(quant_x, 2)] + W(0, 1) + [do(widen_x, 8), do(widen_x, 9)]
-        for s in range(UNITS):
+        def S(cols):
+            return [do(relu_oldest, "scalar", cols)]
+
+        steps = [do(warm), do(warm), do(widen_x, 0), do(widen_x, 1), do(permute_words), do(warm), do(widen_x, 2), do(widen_x, 3), do(warm)]
+        steps += X(0) + [do(widen_x, 4)] + X(1) + [do(permute_scales), do(quant_x, 0), do(widen_x, 5), do(widen_x, 6), do(widen_x, 7)]
+        steps += X(2) + X(3) + X(4) + [do(quant_x, 1), do(widen_x, 8)] + H(0, 0, 1, 2, 3) + [do(interleave_gpsimd, 0)] + X(5) + H(1, 0, 1, 2) + W(0, 0)
+        steps += [do(interleave_vector)] + W(0, 1) + H(1, 3) + [do(quant_x, 2), do(widen_x, 9)]
+        for s in range(UNITS - 2):
             j = x_of(s)
             with_x = live(j)
-            count = tiles_of(s)
+            taken[1] = taken[0] + columns_of(s)
+            if s > 1 and live(s + 1) and not by_pe(s + 1):
+                steps += [do(relu_oldest, "vector", V_WIDE if live(s + HEAD_WIDE - 1) else V_X if with_x else V_TURN if live(x_of(s - 1)) else V_BEFORE)]
             steps += [do(quant_h, s)]
             if s < 2:
                 steps += [do(quant_wb, s)]
-            if s == 2:
-                steps += [do(quant_x, 3)]
-            if s + 1 < FIRST_PE:
+            elif s % 2 == 0 and s // 2 + 2 < GROUPS:
+                steps += [do(quant_x, s // 2 + 2)]
+            elif live(s + 1) and not by_pe(s + 1):
+                steps += [do(relu_oldest, "vector", V_LATE)]
+            if by_pe(s + 1):
+                steps += [do(relu_newest, "gpsimd", G_X if with_x else G_LATE)]
+            elif live(s + 1):
                 steps += [do(interleave_gpsimd, s + 1)]
-            else:
-                steps += [do(relu_newest, "gpsimd", G_TILE * count + (G_X if with_x else 0) - G_FIX if live(s + 2) else G_END)]
-            if s == UNITS - 1:
-                break
+            wide = [do(widen_x, s + HEAD_WIDE)]
             if s == 0:
-                steps += H(2, 0) + X(j) + H(2, 1, 2) + Y(1) + W(1, 0) + Y(1) + W(1, 1) + Y(1) + H(2, 3)
+                steps += H(2, 0) + X(j) + W(1, 0) + W(1, 1) + H(2, 1) + Y(1) + H(2, 2) + Y(1) + H(2, 3) + Y(9) + wide + S(S_EARLY)
+            elif by_pe(s + 1):
+                steps += H(s + 2, 0) + Y(1) + H(s + 2, 1) + X(j) + M(s + 1, 0, 1) + Y(1) + E(s + 1, 0) + M(s + 1, 2, 3)
+                steps += E(s + 1, 1) + H(s + 2, 2) + Y(9) + H(s + 2, 3) + wide
             elif with_x:
-                steps += H(s + 2, 0, 1) + Y(1) + H(s + 2, 2) + Y(count - 2) + E(s + 1, 0) + X(j) + E(s + 1, 1) + H(s + 2, 3) + Y(1)
-            elif live(s + 2):
-                steps += H(s + 2, 0, 1) + Y(1) + H(s + 2, 2) + Y(1) + E(s + 1, 0) + Y(count - 3) + E(s + 1, 1) + H(s + 2, 3) + Y(1)
+                share = S(S_EARLY if s < 3 else S_WIDE if live(s + HEAD_WIDE) else S_A)
+                steps += H(s + 2, 0) + Y(1) + H(s + 2, 1) + X(j) + H(s + 2, 2) + Y(1) + H(s + 2, 3) + wide + share + Y(9)
             else:
-                steps += R(1) + Y(1) + E(s + 1, 0) + Y(1) + E(s + 1, 1)
-                for c in range(count - 2):
-                    steps += R(1) + Y(1)
-            steps += [do(widen_x, s + HEAD_WIDE)]
-            steps += [do(relu_oldest, "scalar", S_EARLY if s + 2 < FIRST_PE else S_X if with_x else S_LATE)]
-        while len(taken) < TILES - 1:
-            steps += R(1) + Y(1)
-        steps += R(1) + Y(1) + [do(relu_newest, "vector", BLK)] + R(8)
+                steps += H(s + 2, 0) + Y(1) + H(s + 2, 1) + Y(1) + H(s + 2, 2) + S(S_FIRST) + Y(1) + H(s + 2, 3) + S(BLK) + Y(9) + S(S_SECOND)
+        taken[1] = TILES * BLK
+
+        def until(n):
+            run = []
+            while taken[0] < n * BLK:
+                run += S(BLK) + Y(1)
+            return run
+
+        steps += [do(quant_h, UNITS - 2), do(relu_oldest, "vector", V_END), do(interleave_last)] + until(END_A)
+        steps += [do(quant_h, UNITS - 1), do(relu_newest, "gpsimd", G_END)]
+        steps += until(TILES - 1) + S(BLK) + Y(1) + [do(relu_newest, "vector", BLK)] + S(BLK) * 4
 
         keys = [key for key, run in steps if key is not None]
-
-        def woven_x(u):
-            return x_of(u - 1)
 
         def fill_next():
             for key in keys:
@@ -424,12 +477,12 @@ def tile_blockdiagmnistconvertible_pa_t_w4_kernel(tc, x_bytes, x_scale, W1_words
             if kind == "x":
                 ready = key[1] in xs
             elif kind == "h":
-                ready = key[1] // 2 in xc and key[1] % 2 in permuted
+                ready = key[1] // 2 in xc
             elif kind == "y":
-                ready = key[1] // 4 in hc and key[1] // 4 % 2 in made
-            elif kind == "e":
+                ready = place(key[1])[0] in hc and place(key[1])[1] in made
+            elif kind == "m":
                 ready = ("h", key[1], 3) in emptied
-                need = 3 if live(woven_x(key[1])) else 1
+                need = 1 - key[2] % 2
             else:
                 ready = True
             for k in range(len(order), len(order) + need):
@@ -442,8 +495,8 @@ def tile_blockdiagmnistconvertible_pa_t_w4_kernel(tc, x_bytes, x_scale, W1_words
                 fill_h(key[1], key[2])
             elif kind == "y":
                 fill_y(key[1])
-            elif kind == "e":
-                fill_woven(key[1], woven_x(key[1]), (0, 1) if need > 1 else key[2:])
+            elif kind == "m":
+                fill_m(key[1], key[2])
             else:
                 fill_wb(key[1], key[2])
             return True
@@ -452,5 +505,6 @@ def tile_blockdiagmnistconvertible_pa_t_w4_kernel(tc, x_bytes, x_scale, W1_words
             while fill_next():
                 pass
             run()
-            emptied.add(key)
+            if key is not None and key[0] != "y":
+                emptied.add(key)
         assert not waiting

@@ -30,15 +30,15 @@ FIRST_PE = 4
 EVERY = 2
 LAST_PE = 10
 A_X = 2048
-AA_X = 1536
+AA_X = 2048
 B_X = 1536
 A_LATE = 2688
 B_LATE = 2560
-G_X = 2176
+G_X = 2048
 G_LATE = 2304
 S_EARLY = 640
 S_WIDE = 640
-S_A = 1536
+S_A = 1792
 S_B = 1024
 S_A_LATE = 1024
 S_B_LATE = 512
@@ -54,7 +54,7 @@ V_BEFORE = 0
 PAIRED_FROM = 7
 SPLIT_FROM = 14
 LAST_CUT = 256
-G_END = 1024
+G_END = 0
 BIG = 3.0e38
 
 

@@ -242,8 +242,8 @@ def tile_blockdiagmnistconvertible_pa_t_w4_kernel(tc, x_bytes, x_scale, W1_words
             if half == 0:
                 hg[u] = work.tile([P, T, 4], BF16, name="hw", tag="hw", align_bytes=64, bufs=2)[:]
             nc.scalar.copy(
-                out=hg[u][:, 2 * P * half : 2 * P * (half + 1), :].rearrange("p r t -> p (r t)"),
-                in_=filled["e", u, half][:].rearrange("p a r t -> p (a r t)"),
+                out=hg[u][:, 2 * P * half : 2 * P * (half + 1), :].rearrange("p r t -> p (r t)").bitcast(F32),
+                in_=filled["e", u, half][:].rearrange("p a r t -> p (a r t)").bitcast(F32),
             )
 
         def interleave_gpsimd(u):

@@ -55,6 +55,7 @@ PAIRED_FROM = 7
 SPLIT_FROM = 14
 LAST_CUT = 256
 G_END = 0
+T_FIRST = 1
 BIG = 3.0e38
 
 
@@ -114,6 +115,7 @@ def tile_blockdiagmnistconvertible_pa_t_w4_kernel(tc, x_bytes, x_scale, W1_words
         filled = {}
         order = []
         emptied = set()
+        woven = {}
 
         def live(u):
             return 0 <= u < UNITS
@@ -199,9 +201,14 @@ def tile_blockdiagmnistconvertible_pa_t_w4_kernel(tc, x_bytes, x_scale, W1_words
             )
 
         def fill_m(u, a):
+            j = x_of(u - 1)
             if a % 2 == 0:
                 bank(("e", u, a // 2), [P, 2, P, 4], BF16)
+            if a == 0:
+                woven[u] = turns(bank(("x", j), [P, 2, 2 * P], F32), xs[j])
             filled["m", u, a] = filled["e", u, a // 2]
+            if T_FIRST:
+                turn(woven[u][a])
             nc.tensor.matmul(
                 out=filled["m", u, a][:, a % 2].rearrange("p r t -> p (r t)"),
                 lhsT=identb[:],
@@ -209,6 +216,8 @@ def tile_blockdiagmnistconvertible_pa_t_w4_kernel(tc, x_bytes, x_scale, W1_words
                 start=True,
                 stop=True,
             )
+            if not T_FIRST:
+                turn(woven[u][a])
 
         def widen_x(j):
             if live(j):
@@ -445,8 +454,8 @@ def tile_blockdiagmnistconvertible_pa_t_w4_kernel(tc, x_bytes, x_scale, W1_words
             if s == 0:
                 steps += H(2, 0) + X(j) + W(1, 0) + W(1, 1) + H(2, 1) + Y(1) + H(2, 2) + Y(1) + H(2, 3) + Y(9) + wide + S(S_EARLY)
             elif by_pe(s + 1):
-                steps += H(s + 2, 0) + Y(1) + H(s + 2, 1) + X(j) + M(s + 1, 0, 1) + Y(1) + E(s + 1, 0) + M(s + 1, 2, 3)
-                steps += E(s + 1, 1) + H(s + 2, 2) + Y(9) + H(s + 2, 3) + wide
+                steps += H(s + 2, 0) + Y(1) + H(s + 2, 1) + Y(1) + M(s + 1, 0, 1, 2, 3) + E(s + 1, 0) + X(j)
+                steps += E(s + 1, 1) + Y(9) + H(s + 2, 2, 3) + wide
             elif with_x:
                 share = S(S_EARLY if s < 3 else S_WIDE if live(s + HEAD_WIDE) else S_A)
                 steps += H(s + 2, 0) + Y(1) + H(s + 2, 1) + X(j) + H(s + 2, 2) + Y(1) + H(s + 2, 3) + wide + share + Y(9)
@@ -482,7 +491,7 @@ def tile_blockdiagmnistconvertible_pa_t_w4_kernel(tc, x_bytes, x_scale, W1_words
                 ready = place(key[1])[0] in hc and place(key[1])[1] in made
             elif kind == "m":
                 ready = ("h", key[1], 3) in emptied
-                need = 1 - key[2] % 2
+                need = (2, 0, 1, 0)[key[2]]
             else:
                 ready = True
             for k in range(len(order), len(order) + need):

@@ -29,33 +29,31 @@ HEAD_WIDE = 10
 FIRST_PE = 4
 EVERY = 2
 LAST_PE = 10
-A_X = 2048
+A_X = 1792
 AA_X = 2048
-B_X = 1536
-A_LATE = 2688
+B_X = 1792
+A_LATE = 2624
 B_LATE = 2560
-G_X = 2048
+G_X = 2304
 G_LATE = 2304
 S_EARLY = 640
-S_WIDE = 640
-S_A = 1792
+S_WIDE = 768
+S_A = 1664
 S_B = 1024
 S_A_LATE = 1024
 S_B_LATE = 512
 S_FIRST = 512
-S_SECOND = 512
-V_END = 640
+S_SECOND = 576
+V_END = 768
 END_A = 58
 V_TURN = 1024
-V_LATE = 4096
+V_LATE = 1024
 V_X = 0
-V_WIDE = 384
+V_WIDE = 256
 V_BEFORE = 0
 PAIRED_FROM = 7
 SPLIT_FROM = 14
-LAST_CUT = 256
-G_END = 0
-T_FIRST = 1
+LATE_B = 0
 BIG = 3.0e38
 
 
@@ -86,15 +84,20 @@ def tile_blockdiagmnistconvertible_pa_t_w4_kernel(tc, x_bytes, x_scale, W1_words
         def load_x(g):
             nc.sync.dma_start(out=xb[g][:], in_=x_bytes[T * g : T * (g + 1), :].rearrange("(p a) k -> p a k", a=4))
 
+        def load_first(h):
+            rows = x_bytes[:T, :].rearrange("(p a) k -> p a k", a=4)
+            nc.sync.dma_start(out=xb[0][:, 2 * h : 2 * h + 2, :], in_=rows[:, 2 * h : 2 * h + 2, :])
+
         def load_wb(n):
             nc.sync.dma_start(out=wbr[n][:], in_=Wb[n].rearrange("(p a) k -> p a k", a=4))
 
         nc.vector.memset(wsr[:].bitcast(I32), 0)
         make_identity(nc, ident[:])
         make_identity(nc, identb[:])
-        load_x(0)
-        nc.sync.dma_start(out=sc[:], in_=x_scale.rearrange("o (p t) -> p (o t)", t=4))
+        load_first(0)
         nc.sync.dma_start(out=w1r[:], in_=W1_words[0])
+        load_first(1)
+        nc.sync.dma_start(out=sc[:], in_=x_scale.rearrange("o (p t) -> p (o t)", t=4))
         load_x(1)
         for q in range(4):
             nc.sync.dma_start(
@@ -115,6 +118,7 @@ def tile_blockdiagmnistconvertible_pa_t_w4_kernel(tc, x_bytes, x_scale, W1_words
         filled = {}
         order = []
         emptied = set()
+        permuted = set()
         woven = {}
 
         def live(u):
@@ -204,10 +208,10 @@ def tile_blockdiagmnistconvertible_pa_t_w4_kernel(tc, x_bytes, x_scale, W1_words
             j = x_of(u - 1)
             if a % 2 == 0:
                 bank(("e", u, a // 2), [P, 2, P, 4], BF16)
-            if a == 0:
+            if a == 0 and live(j):
                 woven[u] = turns(bank(("x", j), [P, 2, 2 * P], F32), xs[j])
             filled["m", u, a] = filled["e", u, a // 2]
-            if T_FIRST:
+            if live(j):
                 turn(woven[u][a])
             nc.tensor.matmul(
                 out=filled["m", u, a][:, a % 2].rearrange("p r t -> p (r t)"),
@@ -216,8 +220,6 @@ def tile_blockdiagmnistconvertible_pa_t_w4_kernel(tc, x_bytes, x_scale, W1_words
                 start=True,
                 stop=True,
             )
-            if not T_FIRST:
-                turn(woven[u][a])
 
         def widen_x(j):
             if live(j):
@@ -265,12 +267,15 @@ def tile_blockdiagmnistconvertible_pa_t_w4_kernel(tc, x_bytes, x_scale, W1_words
                 out=hg[u], in0=hp[u][:, :, :cut].rearrange("p t r -> p r t"), scalar1=1.0, scalar2=0.0, op0=ALU.mult, op1=ALU.add
             )
 
-        def interleave_last():
+        def interleave_last(engine):
             u = UNITS - 1
-            hg[u] = hg[u - 1]
             planes = hp[u][:].rearrange("p t r -> p r t")
-            nc.gpsimd.tensor_scalar(out=hg[u][:, :LAST_CUT], in0=planes[:, :LAST_CUT], scalar1=1.0, scalar2=0.0, op0=ALU.mult, op1=ALU.add)
-            nc.scalar.copy(out=hg[u][:, LAST_CUT:], in_=planes[:, LAST_CUT:])
+            if engine == "scalar":
+                both["rest"] = work.tile([P, 2 * P, 4], BF16, name="rest", tag="rest", align_bytes=64, bufs=1)
+                nc.scalar.copy(out=both["rest"][:], in_=planes[:, 2 * P :])
+            else:
+                hg[u] = hg[u - 1][:, : 2 * P]
+                nc.gpsimd.tensor_scalar(out=hg[u], in0=planes[:, : 2 * P], scalar1=1.0, scalar2=0.0, op0=ALU.mult, op1=ALU.add)
 
         def interleave_vector():
             both["rest"] = work.tile([P, 2 * P, 4], BF16, name="rest", tag="rest", align_bytes=64, bufs=1)
@@ -282,7 +287,7 @@ def tile_blockdiagmnistconvertible_pa_t_w4_kernel(tc, x_bytes, x_scale, W1_words
         def quant_h(u):
             codes, scales = code_tiles(T, "h", 5)
             hc[u], hs[u] = codes[:], scales[:]
-            if u == 0:
+            if u in (0, UNITS - 1):
                 quantize(both["rest"][:].rearrange("p r t -> p (r t)"), codes[:, 2 * P :], scales[:, 2 * P :])
                 quantize(hg[u].rearrange("p r t -> p (r t)"), codes[:, : 2 * P], scales[:, : 2 * P])
             else:
@@ -370,8 +375,9 @@ def tile_blockdiagmnistconvertible_pa_t_w4_kernel(tc, x_bytes, x_scale, W1_words
         def permute_words():
             nc.vector.tensor_copy(out=w1p[:], in_=w1r[:].rearrange("p (n m t b) -> p n t m b", n=2, t=4, b=2))
 
-        def permute_scales():
-            nc.vector.tensor_copy(out=wsp[:], in_=wsr[:].rearrange("p (n m t) -> p n t m", n=2, t=4))
+        def permute_scales(n):
+            nc.vector.tensor_copy(out=wsp[:, n], in_=wsr[:].rearrange("p (n m t) -> p n t m", n=2, t=4)[:, n])
+            permuted.add(n)
 
         def unload_wb(n, h):
             if h == 0:
@@ -430,9 +436,9 @@ def tile_blockdiagmnistconvertible_pa_t_w4_kernel(tc, x_bytes, x_scale, W1_words
             return [do(relu_oldest, "scalar", cols)]
 
         steps = [do(warm), do(warm), do(widen_x, 0), do(widen_x, 1), do(permute_words), do(warm), do(widen_x, 2), do(widen_x, 3), do(warm)]
-        steps += X(0) + [do(widen_x, 4)] + X(1) + [do(permute_scales), do(quant_x, 0), do(widen_x, 5), do(widen_x, 6), do(widen_x, 7)]
-        steps += X(2) + X(3) + X(4) + [do(quant_x, 1), do(widen_x, 8)] + H(0, 0, 1, 2, 3) + [do(interleave_gpsimd, 0)] + X(5) + H(1, 0, 1, 2) + W(0, 0)
-        steps += [do(interleave_vector)] + W(0, 1) + H(1, 3) + [do(quant_x, 2), do(widen_x, 9)]
+        steps += X(0) + [do(widen_x, 4)] + X(1) + [do(permute_scales, 0), do(quant_x, 0), do(widen_x, 5), do(widen_x, 6), do(widen_x, 7)]
+        steps += X(2) + X(3) + [do(permute_scales, 1), do(quant_x, 1)] + H(0, 0, 1, 2, 3) + [do(interleave_gpsimd, 0)] + X(4) + X(5) + H(1, 0, 1)
+        steps += W(0, 0) + [do(interleave_vector)] + H(1, 2) + W(0, 1) + H(1, 3) + [do(quant_x, 2), do(widen_x, 8), do(widen_x, 9)]
         for s in range(UNITS - 2):
             j = x_of(s)
             with_x = live(j)
@@ -452,10 +458,18 @@ def tile_blockdiagmnistconvertible_pa_t_w4_kernel(tc, x_bytes, x_scale, W1_words
                 steps += [do(interleave_gpsimd, s + 1)]
             wide = [do(widen_x, s + HEAD_WIDE)]
             if s == 0:
-                steps += H(2, 0) + X(j) + W(1, 0) + W(1, 1) + H(2, 1) + Y(1) + H(2, 2) + Y(1) + H(2, 3) + Y(9) + wide + S(S_EARLY)
+                steps += X(j) + H(2, 0, 1) + W(1, 0) + Y(1) + H(2, 2) + Y(9) + W(1, 1) + H(2, 3) + wide + S(S_EARLY)
+            elif by_pe(s + 1) and not with_x:
+                if LATE_B == 0:
+                    steps += H(s + 2, 0) + Y(1) + H(s + 2, 1) + M(s + 1, 0, 1, 2, 3) + E(s + 1, 0) + Y(1) + E(s + 1, 1) + Y(1) + H(s + 2, 2) + Y(1) + H(s + 2, 3) + Y(9)
+                else:
+                    steps += H(s + 2, 0) + Y(1) + M(s + 1, 0, 1) + H(s + 2, 1) + Y(2) + E(s + 1, 0) + M(s + 1, 2, 3) + Y(1) + E(s + 1, 1) + H(s + 2, 2) + Y(9) + H(s + 2, 3)
+                steps += S(S_B_LATE)
+            elif by_pe(s + 2) and not with_x:
+                steps += H(s + 2, 0) + Y(1) + H(s + 2, 1) + Y(1) + H(s + 2, 2) + Y(1) + H(s + 2, 3) + S(BLK) + S(S_A_LATE) + Y(9)
             elif by_pe(s + 1):
                 steps += H(s + 2, 0) + Y(1) + H(s + 2, 1) + Y(1) + M(s + 1, 0, 1, 2, 3) + E(s + 1, 0) + X(j)
-                steps += E(s + 1, 1) + Y(9) + H(s + 2, 2, 3) + wide
+                steps += E(s + 1, 1) + H(s + 2, 2) + Y(9) + H(s + 2, 3) + wide
             elif with_x:
                 share = S(S_EARLY if s < 3 else S_WIDE if live(s + HEAD_WIDE) else S_A)
                 steps += H(s + 2, 0) + Y(1) + H(s + 2, 1) + X(j) + H(s + 2, 2) + Y(1) + H(s + 2, 3) + wide + share + Y(9)
@@ -469,8 +483,8 @@ def tile_blockdiagmnistconvertible_pa_t_w4_kernel(tc, x_bytes, x_scale, W1_words
                 run += S(BLK) + Y(1)
             return run
 
-        steps += [do(quant_h, UNITS - 2), do(relu_oldest, "vector", V_END), do(interleave_last)] + until(END_A)
-        steps += [do(quant_h, UNITS - 1), do(relu_newest, "gpsimd", G_END)]
+        steps += [do(interleave_last, "scalar"), do(quant_h, UNITS - 2), do(relu_oldest, "vector", V_END), do(interleave_last, "gpsimd")] + until(END_A)
+        steps += [do(quant_h, UNITS - 1)]
         steps += until(TILES - 1) + S(BLK) + Y(1) + [do(relu_newest, "vector", BLK)] + S(BLK) * 4
 
         keys = [key for key, run in steps if key is not None]
@@ -486,12 +500,12 @@ def tile_blockdiagmnistconvertible_pa_t_w4_kernel(tc, x_bytes, x_scale, W1_words
             if kind == "x":
                 ready = key[1] in xs
             elif kind == "h":
-                ready = key[1] // 2 in xc
+                ready = key[1] // 2 in xc and key[1] % 2 in permuted
             elif kind == "y":
                 ready = place(key[1])[0] in hc and place(key[1])[1] in made
             elif kind == "m":
                 ready = ("h", key[1], 3) in emptied
-                need = (2, 0, 1, 0)[key[2]]
+                need = (1 + live(x_of(key[1] - 1)), 0, 1, 0)[key[2]]
             else:
                 ready = True
             for k in range(len(order), len(order) + need):

@@ -28,32 +28,24 @@ HEAD_X = 6
 HEAD_WIDE = 10
 FIRST_PE = 4
 EVERY = 2
-LAST_PE = 10
-A_X = 1792
-AA_X = 2048
-B_X = 1792
+LAST_PE = 12
+WIDE_14 = 5
+WIDE_15 = 7
+A_X = 1664
+AA_X = 1664
+B_X = 1920
 A_LATE = 2624
-B_LATE = 2560
-G_X = 2304
-G_LATE = 2304
-S_EARLY = 640
-S_WIDE = 768
-S_A = 1664
-S_B = 1024
-S_A_LATE = 1024
-S_B_LATE = 512
-S_FIRST = 512
-S_SECOND = 576
-V_END = 768
-END_A = 58
-V_TURN = 1024
-V_LATE = 1024
-V_X = 0
-V_WIDE = 256
-V_BEFORE = 0
-PAIRED_FROM = 7
-SPLIT_FROM = 14
-LATE_B = 0
+A_SHORT = 2688
+G_X = 2560
+S_SHARE = {0: 384, 1: 640, 2: 896, 4: 512, 5: 512, 6: 768, 7: 256, 8: 1408, 10: 1536, 11: 256, 12: 512, 13: 512}
+V_BEFORE = {2: 256, 10: 768, 12: 1280}
+V_AFTER = {13: 1152}
+V_END = 0
+B_PRE = 2
+LAST = 256
+END_A = 29696
+PAIRED_FROM = 6
+SPLIT_FROM = 12
 BIG = 3.0e38
 
 
@@ -118,6 +110,8 @@ def tile_blockdiagmnistconvertible_pa_t_w4_kernel(tc, x_bytes, x_scale, W1_words
         filled = {}
         order = []
         emptied = set()
+        coded = []
+        ready_h = []
         permuted = set()
         woven = {}
 
@@ -238,10 +232,14 @@ def tile_blockdiagmnistconvertible_pa_t_w4_kernel(tc, x_bytes, x_scale, W1_words
                 op=ALU.mult,
             )
 
-        def quant_x(g):
-            codes, scales = code_tiles(T, "x", 3)
-            xc[g], xsc[g] = codes[:], scales[:]
-            quantize(xg[g].rearrange("p r t -> p (r t)"), xc[g], xsc[g])
+        def quant_x(*halves):
+            g = halves[0] // 2
+            if halves[0] % 2 == 0:
+                codes, scales = code_tiles(T, "x", 3)
+                xc[g], xsc[g] = codes[:], scales[:]
+            cols = slice(2 * P * (halves[0] % 2), 2 * P * (halves[-1] % 2 + 1))
+            quantize(xg[g][:, cols].rearrange("p r t -> p (r t)"), xc[g][:, cols], xsc[g][:, cols])
+            coded.extend(halves)
 
         def relu_h(u, t):
             if t == 0:
@@ -258,40 +256,34 @@ def tile_blockdiagmnistconvertible_pa_t_w4_kernel(tc, x_bytes, x_scale, W1_words
             )
 
         def interleave_gpsimd(u):
-            cut = 2 * P if u == 0 else T
+            cut = 2 * P if u in (0, UNITS - 1) else T
             if u > 1:
-                hg[u] = hg[u - 1]
+                hg[u] = hg[u - 1][:, :cut]
             else:
                 hg[u] = work.tile([P, cut, 4], BF16, name="hg", tag="hg", align_bytes=64, bufs=1)[:]
             nc.gpsimd.tensor_scalar(
                 out=hg[u], in0=hp[u][:, :, :cut].rearrange("p t r -> p r t"), scalar1=1.0, scalar2=0.0, op0=ALU.mult, op1=ALU.add
             )
 
-        def interleave_last(engine):
-            u = UNITS - 1
-            planes = hp[u][:].rearrange("p t r -> p r t")
-            if engine == "scalar":
-                both["rest"] = work.tile([P, 2 * P, 4], BF16, name="rest", tag="rest", align_bytes=64, bufs=1)
-                nc.scalar.copy(out=both["rest"][:], in_=planes[:, 2 * P :])
-            else:
-                hg[u] = hg[u - 1][:, : 2 * P]
-                nc.gpsimd.tensor_scalar(out=hg[u], in0=planes[:, : 2 * P], scalar1=1.0, scalar2=0.0, op0=ALU.mult, op1=ALU.add)
-
-        def interleave_vector():
+        def interleave_vector(u):
             both["rest"] = work.tile([P, 2 * P, 4], BF16, name="rest", tag="rest", align_bytes=64, bufs=1)
             nc.vector.tensor_copy(
                 out=both["rest"][:].rearrange("p (c i) t -> p c t i", i=4),
-                in_=hp[0][:, :, 2 * P :].rearrange("p t (c i) -> p c t i", i=4),
+                in_=hp[u][:, :, 2 * P :].rearrange("p t (c i) -> p c t i", i=4),
             )
 
-        def quant_h(u):
-            codes, scales = code_tiles(T, "h", 5)
-            hc[u], hs[u] = codes[:], scales[:]
-            if u in (0, UNITS - 1):
-                quantize(both["rest"][:].rearrange("p r t -> p (r t)"), codes[:, 2 * P :], scales[:, 2 * P :])
-                quantize(hg[u].rearrange("p r t -> p (r t)"), codes[:, : 2 * P], scales[:, : 2 * P])
-            else:
+        def quant_h(u, *parts):
+            if u not in hc:
+                codes, scales = code_tiles(T, "h", 5)
+                hc[u], hs[u] = codes[:], scales[:]
+            if not parts:
                 quantize(hg[u].rearrange("p r t -> p (r t)"), hc[u], hs[u])
+            if "rest" in parts:
+                quantize(both["rest"][:].rearrange("p r t -> p (r t)"), hc[u][:, 2 * P :], hs[u][:, 2 * P :])
+            if "first" in parts:
+                quantize(hg[u].rearrange("p r t -> p (r t)"), hc[u][:, : 2 * P], hs[u][:, : 2 * P])
+            if "first" in parts or not parts:
+                ready_h.append(u)
 
         def ring_columns(c0, c1):
             start = c0 % (RING * BLK)
@@ -316,11 +308,6 @@ def tile_blockdiagmnistconvertible_pa_t_w4_kernel(tc, x_bytes, x_scale, W1_words
             cols = ring_columns((4 * u + a0) * BLK, (4 * u + a1) * BLK)
             nc.sync.dma_start(out=rows[:, a0:a1, :], in_=cols.rearrange("p (a c) -> p a c", c=BLK))
 
-        def store_tile(n):
-            g, r = divmod(n, 8)
-            rows = out[T * g : T * (g + 1), :].rearrange("(p a) c -> p (a c)", a=4)
-            nc.sync.dma_start(out=rows[:, r * BLK : (r + 1) * BLK], in_=ring_columns(n * BLK, (n + 1) * BLK))
-
         def store_rows(g, a0, a1):
             rows = out[T * g : T * (g + 1), :].rearrange("(p a) c -> p (a c)", a=4)
             nc.sync.dma_start(out=rows[:, a0 * HID : a1 * HID], in_=ring_columns((8 * g + 2 * a0) * BLK, (8 * g + 2 * a1) * BLK))
@@ -330,15 +317,24 @@ def tile_blockdiagmnistconvertible_pa_t_w4_kernel(tc, x_bytes, x_scale, W1_words
 
         cleared = [0] * TILES
 
+        late = []
+
         def relu(engine, c0, c1):
-            for j, lo, hi in cut(c0, c1, RING * BLK):
-                part = ring[:, lo:hi]
-                if engine == "vector":
-                    nc.vector.tensor_scalar(out=part, in0=part, scalar1=0.0, scalar2=None, op0=ALU.max)
-                elif engine == "gpsimd":
-                    nc.gpsimd.tensor_scalar(out=part, in0=part, scalar1=BIG, scalar2=0.0, op0=ALU.min, op1=ALU.max)
-                else:
-                    nc.scalar.activation(out=part, in_=part, func=ACT.Relu)
+            part = ring_columns(c0, c1)
+            if engine == "vector":
+                nc.vector.tensor_scalar(out=part, in0=part, scalar1=0.0, scalar2=None, op0=ALU.max)
+            elif engine == "gpsimd":
+                nc.gpsimd.tensor_scalar(out=part, in0=part, scalar1=BIG, scalar2=0.0, op0=ALU.min, op1=ALU.max)
+                late.append((c0, c1))
+                return
+            else:
+                nc.scalar.activation(out=part, in_=part, func=ACT.Relu)
+            store_cleared(c0, c1)
+
+        def store_late():
+            store_cleared(*late.pop())
+
+        def store_cleared(c0, c1):
             done = []
             for n, lo, hi in cut(c0, c1, BLK):
                 cleared[n] = cleared[n] + hi - lo
@@ -346,10 +342,7 @@ def tile_blockdiagmnistconvertible_pa_t_w4_kernel(tc, x_bytes, x_scale, W1_words
                     done.append(n)
             if done:
                 for g, lo, hi in cut(done[0], done[-1] + 1, 8):
-                    if 8 * g + hi > TILES - 2:
-                        for n in range(8 * g + lo, 8 * g + hi):
-                            store_tile(n)
-                    elif whole_rows(g):
+                    if whole_rows(g):
                         whole = [a for a in range(lo // 2, (hi + 1) // 2) if cleared[8 * g + 2 * a] + cleared[8 * g + 2 * a + 1] == HID]
                         if whole:
                             store_rows(g, whole[0], whole[-1] + 1)
@@ -371,6 +364,10 @@ def tile_blockdiagmnistconvertible_pa_t_w4_kernel(tc, x_bytes, x_scale, W1_words
                     waiting.insert(0, (c0 + cols, c1))
                 relu(engine, c0, min(c1, c0 + cols))
                 cols = cols - (c1 - c0)
+
+        def relu_tile():
+            if waiting:
+                relu_oldest("scalar", BLK - waiting[0][0] % BLK)
 
         def permute_words():
             nc.vector.tensor_copy(out=w1p[:], in_=w1r[:].rearrange("p (n m t b) -> p n t m b", n=2, t=4, b=2))
@@ -398,7 +395,17 @@ def tile_blockdiagmnistconvertible_pa_t_w4_kernel(tc, x_bytes, x_scale, W1_words
             made.add(n)
 
         def x_of(s):
-            return s + HEAD_X
+            if s + HEAD_X < UNITS - 2:
+                return s + HEAD_X
+            return {9: UNITS - 2, 11: UNITS - 1}.get(s, -1)
+
+        def widened_in(s):
+            if s + HEAD_WIDE < UNITS - 2:
+                return s + HEAD_WIDE
+            return {WIDE_14: UNITS - 2, WIDE_15: UNITS - 1}.get(s, -1)
+
+        def group_at(s):
+            return {2: (6, 7), 4: (8, 9), 6: (10, 11), 8: (12, 13), 10: (14,), 12: (15,)}.get(s)
 
         def do(f, *args):
             return (None, lambda: f(*args))
@@ -423,7 +430,7 @@ def tile_blockdiagmnistconvertible_pa_t_w4_kernel(tc, x_bytes, x_scale, W1_words
                 return 3 * BLK
             if live(x_of(s)):
                 return B_X if by_pe(s + 1) else A_X if by_pe(s) else AA_X
-            return B_LATE if by_pe(s + 1) else A_LATE
+            return A_SHORT if len(group_at(s) or ()) == 1 else A_LATE
 
         taken = [0, 0]
 
@@ -436,56 +443,54 @@ def tile_blockdiagmnistconvertible_pa_t_w4_kernel(tc, x_bytes, x_scale, W1_words
             return [do(relu_oldest, "scalar", cols)]
 
         steps = [do(warm), do(warm), do(widen_x, 0), do(widen_x, 1), do(permute_words), do(warm), do(widen_x, 2), do(widen_x, 3), do(warm)]
-        steps += X(0) + [do(widen_x, 4)] + X(1) + [do(permute_scales, 0), do(quant_x, 0), do(widen_x, 5), do(widen_x, 6), do(widen_x, 7)]
-        steps += X(2) + X(3) + [do(permute_scales, 1), do(quant_x, 1)] + H(0, 0, 1, 2, 3) + [do(interleave_gpsimd, 0)] + X(4) + X(5) + H(1, 0, 1)
-        steps += W(0, 0) + [do(interleave_vector)] + H(1, 2) + W(0, 1) + H(1, 3) + [do(quant_x, 2), do(widen_x, 8), do(widen_x, 9)]
+        steps += X(0) + [do(widen_x, 4)] + X(1) + [do(permute_scales, 0), do(quant_x, 0, 1), do(widen_x, 5), do(widen_x, 6), do(widen_x, 7)]
+        steps += X(2) + X(3) + [do(permute_scales, 1), do(quant_x, 2, 3)] + H(0, 0, 1, 2, 3) + [do(interleave_gpsimd, 0)] + X(4) + X(5) + H(1, 0, 1)
+        steps += W(0, 0) + [do(interleave_vector, 0)] + H(1, 2) + W(0, 1) + H(1, 3) + [do(quant_x, 4, 5), do(widen_x, 8), do(widen_x, 9)]
         for s in range(UNITS - 2):
             j = x_of(s)
             with_x = live(j)
             taken[1] = taken[0] + columns_of(s)
-            if s > 1 and live(s + 1) and not by_pe(s + 1):
-                steps += [do(relu_oldest, "vector", V_WIDE if live(s + HEAD_WIDE - 1) else V_X if with_x else V_TURN if live(x_of(s - 1)) else V_BEFORE)]
-            steps += [do(quant_h, s)]
+            if not by_pe(s + 1):
+                steps += [do(relu_oldest, "vector", V_BEFORE.get(s, 0))]
+            steps += [do(quant_h, s) if s else do(quant_h, 0, "rest", "first")]
             if s < 2:
                 steps += [do(quant_wb, s)]
-            elif s % 2 == 0 and s // 2 + 2 < GROUPS:
-                steps += [do(quant_x, s // 2 + 2)]
-            elif live(s + 1) and not by_pe(s + 1):
-                steps += [do(relu_oldest, "vector", V_LATE)]
+            elif group_at(s):
+                steps += [do(quant_x, *group_at(s))]
+            elif not by_pe(s + 1):
+                steps += [do(relu_oldest, "vector", V_AFTER[s])]
             if by_pe(s + 1):
-                steps += [do(relu_newest, "gpsimd", G_X if with_x else G_LATE)]
-            elif live(s + 1):
-                steps += [do(interleave_gpsimd, s + 1)]
-            wide = [do(widen_x, s + HEAD_WIDE)]
-            if s == 0:
-                steps += X(j) + H(2, 0, 1) + W(1, 0) + Y(1) + H(2, 2) + Y(9) + W(1, 1) + H(2, 3) + wide + S(S_EARLY)
-            elif by_pe(s + 1) and not with_x:
-                if LATE_B == 0:
-                    steps += H(s + 2, 0) + Y(1) + H(s + 2, 1) + M(s + 1, 0, 1, 2, 3) + E(s + 1, 0) + Y(1) + E(s + 1, 1) + Y(1) + H(s + 2, 2) + Y(1) + H(s + 2, 3) + Y(9)
-                else:
-                    steps += H(s + 2, 0) + Y(1) + M(s + 1, 0, 1) + H(s + 2, 1) + Y(2) + E(s + 1, 0) + M(s + 1, 2, 3) + Y(1) + E(s + 1, 1) + H(s + 2, 2) + Y(9) + H(s + 2, 3)
-                steps += S(S_B_LATE)
-            elif by_pe(s + 2) and not with_x:
-                steps += H(s + 2, 0) + Y(1) + H(s + 2, 1) + Y(1) + H(s + 2, 2) + Y(1) + H(s + 2, 3) + S(BLK) + S(S_A_LATE) + Y(9)
-            elif by_pe(s + 1):
-                steps += H(s + 2, 0) + Y(1) + H(s + 2, 1) + Y(1) + M(s + 1, 0, 1, 2, 3) + E(s + 1, 0) + X(j)
-                steps += E(s + 1, 1) + H(s + 2, 2) + Y(9) + H(s + 2, 3) + wide
-            elif with_x:
-                share = S(S_EARLY if s < 3 else S_WIDE if live(s + HEAD_WIDE) else S_A)
-                steps += H(s + 2, 0) + Y(1) + H(s + 2, 1) + X(j) + H(s + 2, 2) + Y(1) + H(s + 2, 3) + wide + share + Y(9)
+                steps += [do(relu_newest, "gpsimd", G_X)]
             else:
-                steps += H(s + 2, 0) + Y(1) + H(s + 2, 1) + Y(1) + H(s + 2, 2) + S(S_FIRST) + Y(1) + H(s + 2, 3) + S(BLK) + Y(9) + S(S_SECOND)
-        taken[1] = TILES * BLK
+                steps += [do(interleave_gpsimd, s + 1)]
+            wide = [do(widen_x, widened_in(s))]
+            share = S(S_SHARE.get(s, 0))
+            if s == 0:
+                steps += X(j) + H(2, 0, 1) + W(1, 0) + Y(1) + H(2, 2) + Y(9) + W(1, 1) + H(2, 3) + wide + share
+            elif by_pe(s + 1):
+                steps += H(s + 2, 0) + Y(1) + H(s + 2, 1) + Y(B_PRE) + M(s + 1, 0, 1, 2, 3) + E(s + 1, 0) + share + X(j)
+                steps += E(s + 1, 1) + Y(1) + H(s + 2, 2) + Y(9) + H(s + 2, 3) + wide + [do(store_late)]
+            elif with_x:
+                steps += H(s + 2, 0) + Y(1) + H(s + 2, 1) + X(j) + H(s + 2, 2) + Y(1) + H(s + 2, 3) + wide + share + Y(9)
+            elif by_pe(s + 2):
+                steps += H(s + 2, 0) + Y(1) + H(s + 2, 1) + Y(1) + H(s + 2, 2) + Y(1) + H(s + 2, 3) + wide + share + Y(9)
+            else:
+                steps += H(s + 2, 0, 1) + Y(1) + H(s + 2, 2) + Y(1) + [do(relu_tile)] + Y(1) + H(s + 2, 3) + [do(relu_tile)] + Y(9) + share
 
         def until(n):
             run = []
-            while taken[0] < n * BLK:
-                run += S(BLK) + Y(1)
+            taken[1] = n
+            while taken[0] < n:
+                run += [do(relu_tile)] + Y(1)
             return run
 
-        steps += [do(interleave_last, "scalar"), do(quant_h, UNITS - 2), do(relu_oldest, "vector", V_END), do(interleave_last, "gpsimd")] + until(END_A)
-        steps += [do(quant_h, UNITS - 1)]
-        steps += until(TILES - 1) + S(BLK) + Y(1) + [do(relu_newest, "vector", BLK)] + S(BLK) * 4
+        steps += [do(relu_tile)] * 2 + [do(relu_oldest, "vector", V_END), do(quant_h, UNITS - 2), do(interleave_vector, UNITS - 1), do(interleave_gpsimd, UNITS - 1)]
+        steps += until(END_A) + [do(quant_h, UNITS - 1, "rest", "first")]
+        steps += until((TILES - 1) * BLK) + [do(relu_tile)] * 3
+        taken[1] = TILES * BLK - LAST
+        steps += Y(1)
+        taken[1] = TILES * BLK
+        steps += Y(1) + [do(relu_oldest, "vector", BLK - LAST), do(relu_oldest, "vector", LAST)]
 
         keys = [key for key, run in steps if key is not None]
 
@@ -500,9 +505,9 @@ def tile_blockdiagmnistconvertible_pa_t_w4_kernel(tc, x_bytes, x_scale, W1_words
             if kind == "x":
                 ready = key[1] in xs
             elif kind == "h":
-                ready = key[1] // 2 in xc and key[1] % 2 in permuted
+                ready = (key[1] if by_tokens(key[1]) else key[1] | 1) in coded and key[1] % 2 in permuted
             elif kind == "y":
-                ready = place(key[1])[0] in hc and place(key[1])[1] in made
+                ready = place(key[1])[0] in ready_h and place(key[1])[1] in made
             elif kind == "m":
                 ready = ("h", key[1], 3) in emptied
                 need = (1 + live(x_of(key[1] - 1)), 0, 1, 0)[key[2]]

@@ -25,28 +25,17 @@ TILES = 4 * UNITS
 BANKS = 8
 RING = 64
 HEAD_X = 6
-HEAD_WIDE = 10
+WIDEN_LEAD = 4
 FIRST_PE = 4
-EVERY = 2
 LAST_PE = 12
-WIDE_14 = 5
-WIDE_15 = 7
-A_X = 1664
-AA_X = 1664
-B_X = 1920
-A_LATE = 2624
-A_SHORT = 2688
-G_X = 2560
-S_SHARE = {0: 384, 1: 640, 2: 896, 4: 512, 5: 512, 6: 768, 7: 256, 8: 1408, 10: 1536, 11: 256, 12: 512, 13: 512}
-V_BEFORE = {2: 256, 10: 768, 12: 1280}
-V_AFTER = {13: 1152}
-V_END = 0
-B_PRE = 2
-LAST = 256
-END_A = 29696
-PAIRED_FROM = 6
-SPLIT_FROM = 12
-BIG = 3.0e38
+SPLIT_FROM = UNITS - 2
+WINDOW = 2752
+LONG_X = 1792
+G_RELU = 2176
+S_EARLY = 640
+S_SHARE = 1536
+LEFT = 2 * BLK
+BIG = 3.4028234663852886e38
 
 
 def tile_blockdiagmnistconvertible_pa_t_w4_kernel(tc, x_bytes, x_scale, W1_words, W1_scales, b1, Wb, bb, out):
@@ -119,7 +108,7 @@ def tile_blockdiagmnistconvertible_pa_t_w4_kernel(tc, x_bytes, x_scale, W1_words
             return 0 <= u < UNITS
 
         def by_pe(u):
-            return live(u) and FIRST_PE <= u <= LAST_PE and (u - FIRST_PE) % EVERY == 0
+            return live(u) and FIRST_PE <= u <= LAST_PE and u % 2 == 0
 
         def single(name):
             return work.tile([P, T, 4], BF16, name=name, tag="single", align_bytes=64, bufs=2)
@@ -175,7 +164,7 @@ def tile_blockdiagmnistconvertible_pa_t_w4_kernel(tc, x_bytes, x_scale, W1_words
                 )
 
         def whole_rows(g):
-            return g >= PAIRED_FROM
+            return by_tokens(2 * g)
 
         def place(n):
             g, r = divmod(n, 8)
@@ -350,20 +339,27 @@ def tile_blockdiagmnistconvertible_pa_t_w4_kernel(tc, x_bytes, x_scale, W1_words
                         for u, a0, a1 in cut(8 * g + lo, 8 * g + hi, 4):
                             store(u, a0, a1)
 
-        def relu_newest(engine, cols):
-            if waiting and cols:
-                c0, c1 = waiting.pop()
-                if c1 - c0 > cols:
-                    waiting.append((c0, c1 - cols))
-                relu(engine, max(c0, c1 - cols), c1)
+        reach = [0]
 
-        def relu_oldest(engine, cols):
-            while waiting and cols > 0:
+        def relu_gpsimd():
+            c0, c1 = waiting.pop()
+            reach[0] = c1 - G_RELU
+            assert reach[0] >= c0
+            if reach[0] > c0:
+                waiting.append((c0, reach[0]))
+            relu("gpsimd", reach[0], c1)
+
+        def relu_oldest(engine, cols, below=TILES * BLK):
+            while waiting and cols > 0 and waiting[0][0] < below:
                 c0, c1 = waiting.pop(0)
-                if c1 - c0 > cols:
-                    waiting.insert(0, (c0 + cols, c1))
-                relu(engine, c0, min(c1, c0 + cols))
-                cols = cols - (c1 - c0)
+                end = min(c1, c0 + cols, below)
+                if end < c1:
+                    waiting.insert(0, (end, c1))
+                relu(engine, c0, end)
+                cols = cols - (end - c0)
+
+        def relu_skipped(engine, cols):
+            relu_oldest(engine, cols, reach[0])
 
         def relu_tile():
             if waiting:
@@ -395,17 +391,14 @@ def tile_blockdiagmnistconvertible_pa_t_w4_kernel(tc, x_bytes, x_scale, W1_words
             made.add(n)
 
         def x_of(s):
-            if s + HEAD_X < UNITS - 2:
+            if s + HEAD_X < SPLIT_FROM:
                 return s + HEAD_X
-            return {9: UNITS - 2, 11: UNITS - 1}.get(s, -1)
+            return SPLIT_FROM + (s - LAST_PE + 3) // 2 if by_pe(s + 1) else -1
 
-        def widened_in(s):
-            if s + HEAD_WIDE < UNITS - 2:
-                return s + HEAD_WIDE
-            return {WIDE_14: UNITS - 2, WIDE_15: UNITS - 1}.get(s, -1)
-
-        def group_at(s):
-            return {2: (6, 7), 4: (8, 9), 6: (10, 11), 8: (12, 13), 10: (14,), 12: (15,)}.get(s)
+        def halves_at(s):
+            if s % 2:
+                return ()
+            return (s + 4, s + 5) if s + 4 < SPLIT_FROM else (x_of(s - 1),)
 
         def do(f, *args):
             return (None, lambda: f(*args))
@@ -429,8 +422,8 @@ def tile_blockdiagmnistconvertible_pa_t_w4_kernel(tc, x_bytes, x_scale, W1_words
             if s < 2:
                 return 3 * BLK
             if live(x_of(s)):
-                return B_X if by_pe(s + 1) else A_X if by_pe(s) else AA_X
-            return A_SHORT if len(group_at(s) or ()) == 1 else A_LATE
+                return LONG_X if by_pe(s + 1) else WINDOW - 2 * BLK
+            return WINDOW
 
         taken = [0, 0]
 
@@ -439,9 +432,6 @@ def tile_blockdiagmnistconvertible_pa_t_w4_kernel(tc, x_bytes, x_scale, W1_words
             taken[0] = min((c0 // BLK + count) * BLK, taken[1])
             return [(("y", n), lambda n=n, lo=lo, hi=hi: bias_y(n, lo, hi)) for n, lo, hi in cut(c0, taken[0], BLK) if hi > lo]
 
-        def S(cols):
-            return [do(relu_oldest, "scalar", cols)]
-
         steps = [do(warm), do(warm), do(widen_x, 0), do(widen_x, 1), do(permute_words), do(warm), do(widen_x, 2), do(widen_x, 3), do(warm)]
         steps += X(0) + [do(widen_x, 4)] + X(1) + [do(permute_scales, 0), do(quant_x, 0, 1), do(widen_x, 5), do(widen_x, 6), do(widen_x, 7)]
         steps += X(2) + X(3) + [do(permute_scales, 1), do(quant_x, 2, 3)] + H(0, 0, 1, 2, 3) + [do(interleave_gpsimd, 0)] + X(4) + X(5) + H(1, 0, 1)
@@ -449,33 +439,33 @@ def tile_blockdiagmnistconvertible_pa_t_w4_kernel(tc, x_bytes, x_scale, W1_words
         for s in range(UNITS - 2):
             j = x_of(s)
             with_x = live(j)
-            taken[1] = taken[0] + columns_of(s)
-            if not by_pe(s + 1):
-                steps += [do(relu_oldest, "vector", V_BEFORE.get(s, 0))]
+            first = taken[0]
+            taken[1] = first + columns_of(s)
+            if by_pe(s):
+                steps += [do(relu_skipped, "vector", WINDOW) if by_pe(s + 2) else do(relu_oldest, "vector", WINDOW, first - LEFT)]
+            if s == 2:
+                steps += [do(relu_oldest, "vector", 2 * P)]
             steps += [do(quant_h, s) if s else do(quant_h, 0, "rest", "first")]
             if s < 2:
                 steps += [do(quant_wb, s)]
-            elif group_at(s):
-                steps += [do(quant_x, *group_at(s))]
+            elif halves_at(s):
+                steps += [do(quant_x, *halves_at(s))]
             elif not by_pe(s + 1):
-                steps += [do(relu_oldest, "vector", V_AFTER[s])]
-            if by_pe(s + 1):
-                steps += [do(relu_newest, "gpsimd", G_X)]
-            else:
-                steps += [do(interleave_gpsimd, s + 1)]
-            wide = [do(widen_x, widened_in(s))]
-            share = S(S_SHARE.get(s, 0))
+                steps += [do(relu_oldest, "vector", WINDOW, first - LEFT)]
+            steps += [do(relu_gpsimd) if by_pe(s + 1) else do(interleave_gpsimd, s + 1)]
+            wide = [do(widen_x, x_of(s + WIDEN_LEAD))]
+            share = [do(relu_oldest, "scalar", S_SHARE if by_pe(s) else S_EARLY, taken[1] - G_RELU if by_pe(s + 2) else taken[1])]
             if s == 0:
                 steps += X(j) + H(2, 0, 1) + W(1, 0) + Y(1) + H(2, 2) + Y(9) + W(1, 1) + H(2, 3) + wide + share
             elif by_pe(s + 1):
-                steps += H(s + 2, 0) + Y(1) + H(s + 2, 1) + Y(B_PRE) + M(s + 1, 0, 1, 2, 3) + E(s + 1, 0) + share + X(j)
+                steps += H(s + 2, 0) + Y(1) + H(s + 2, 1) + Y(2) + M(s + 1, 0, 1, 2, 3) + E(s + 1, 0) + [do(relu_skipped, "scalar", 0 if by_pe(s + 3) else BLK)] + X(j)
                 steps += E(s + 1, 1) + Y(1) + H(s + 2, 2) + Y(9) + H(s + 2, 3) + wide + [do(store_late)]
             elif with_x:
                 steps += H(s + 2, 0) + Y(1) + H(s + 2, 1) + X(j) + H(s + 2, 2) + Y(1) + H(s + 2, 3) + wide + share + Y(9)
             elif by_pe(s + 2):
                 steps += H(s + 2, 0) + Y(1) + H(s + 2, 1) + Y(1) + H(s + 2, 2) + Y(1) + H(s + 2, 3) + wide + share + Y(9)
             else:
-                steps += H(s + 2, 0, 1) + Y(1) + H(s + 2, 2) + Y(1) + [do(relu_tile)] + Y(1) + H(s + 2, 3) + [do(relu_tile)] + Y(9) + share
+                steps += H(s + 2, 0, 1) + Y(1) + H(s + 2, 2) + Y(1) + [do(relu_tile)] + Y(1) + H(s + 2, 3) + [do(relu_tile)] + Y(9) + [do(relu_tile)]
 
         def until(n):
             run = []
@@ -484,13 +474,13 @@ def tile_blockdiagmnistconvertible_pa_t_w4_kernel(tc, x_bytes, x_scale, W1_words
                 run += [do(relu_tile)] + Y(1)
             return run
 
-        steps += [do(relu_tile)] * 2 + [do(relu_oldest, "vector", V_END), do(quant_h, UNITS - 2), do(interleave_vector, UNITS - 1), do(interleave_gpsimd, UNITS - 1)]
-        steps += until(END_A) + [do(quant_h, UNITS - 1, "rest", "first")]
+        steps += [do(relu_tile)] * 2 + [do(quant_h, UNITS - 2), do(interleave_vector, UNITS - 1), do(interleave_gpsimd, UNITS - 1)]
+        steps += until((TILES - 6) * BLK) + [do(quant_h, UNITS - 1, "rest", "first")]
         steps += until((TILES - 1) * BLK) + [do(relu_tile)] * 3
-        taken[1] = TILES * BLK - LAST
+        taken[1] = TILES * BLK - 2 * P
         steps += Y(1)
         taken[1] = TILES * BLK
-        steps += Y(1) + [do(relu_oldest, "vector", BLK - LAST), do(relu_oldest, "vector", LAST)]
+        steps += Y(1) + [do(relu_oldest, "vector", 2 * P)] * 2
 
         keys = [key for key, run in steps if key is not None]
 

@@ -23,18 +23,15 @@ GROUPS = B // T
 UNITS = 2 * GROUPS
 TILES = 4 * UNITS
 BANKS = 8
-RING = 64
-HEAD_X = 6
-WIDEN_LEAD = 4
 FIRST_PE = 4
 LAST_PE = 12
-SPLIT_FROM = UNITS - 2
-WINDOW = 2752
-LONG_X = 1792
-G_RELU = 2176
-S_EARLY = 640
-S_SHARE = 1536
-LEFT = 2 * BLK
+HEAD_X = 8
+G_BASE = 1088
+G_HALF = 768
+S_RELU = 1408
+PIECE = 64
+V_RELU = 2048
+V_EARLY = 2048
 BIG = 3.4028234663852886e38
 
 
@@ -56,11 +53,14 @@ def tile_blockdiagmnistconvertible_pa_t_w4_kernel(tc, x_bytes, x_scale, W1_words
         wsp = keep.tile([P, 2, 4, P], U8, name="wsp", align_bytes=64)
         b1c = keep.tile([P, 2, 4], BF16, name="b1c")
         bbr = keep.tile([P, HID], BF16, name="bbr")
-        ring = keep.tile([P, RING * BLK], F32, name="ring")
+        ring = keep.tile([P, TILES * BLK], F32, name="ring")
         xb = [keep.tile([P, 4, IN], U8, name=f"xb{g}") for g in range(GROUPS)]
         wbc = [keep.tile([P, BLK], U32, name=f"wbc{n}", align_bytes=64) for n in range(2)]
         wbs = [keep.tile([P, BLK], U8, name=f"wbs{n}", align_bytes=64) for n in range(2)]
         wbr = [keep.tile([P, 4, BLK], BF16, name=f"wbr{n}") for n in range(2)]
+        hg = keep.tile([P, T, 4], BF16, name="hg", align_bytes=64)
+        hl = keep.tile([P, 2 * P, 4], BF16, name="hl", align_bytes=64)
+        rest = keep.tile([P, 2 * P, 4], BF16, name="rest", align_bytes=64)
 
         def load_x(g):
             nc.sync.dma_start(out=xb[g][:], in_=x_bytes[T * g : T * (g + 1), :].rearrange("(p a) k -> p a k", a=4))
@@ -95,434 +95,380 @@ def tile_blockdiagmnistconvertible_pa_t_w4_kernel(tc, x_bytes, x_scale, W1_words
             load_x(g)
 
         xs, xg, xc, xsc = {}, {}, {}, {}
-        hp, hg, hc, hs, wbg, both = {}, {}, {}, {}, {}, {}
+        hp, hw, hc, hs, wbg = {}, {}, {}, {}, {}
         filled = {}
-        order = []
-        emptied = set()
-        coded = []
-        ready_h = []
-        permuted = set()
-        woven = {}
-
-        def live(u):
-            return 0 <= u < UNITS
+        tenants = []
 
         def by_pe(u):
-            return live(u) and FIRST_PE <= u <= LAST_PE and u % 2 == 0
-
-        def single(name):
-            return work.tile([P, T, 4], BF16, name=name, tag="single", align_bytes=64, bufs=2)
+            return FIRST_PE <= u <= LAST_PE and u % 2 == 0
 
         def quantize(src, codes, scales):
             nc.vector.quantize_mx(out=codes.bitcast(FP8X4), scales=scales, in_=src)
 
-        def code_tiles(width, kind, bufs):
-            codes = work.tile([P, width], U32, name="codes", tag=f"codes_{kind}", align_bytes=64, bufs=bufs)
-            scales = work.tile([P, width], U8, name="scales", tag=f"scales_{kind}", align_bytes=64, bufs=bufs)
-            return codes, scales
+        def flat(view):
+            return view.rearrange("p r t -> p (r t)")
+
+        def code_tiles(kind, bufs):
+            codes = work.tile([P, T], U32, name="codes", tag=f"codes_{kind}", align_bytes=64, bufs=bufs)
+            scales = work.tile([P, T], U8, name="scales", tag=f"scales_{kind}", align_bytes=64, bufs=bufs)
+            return codes[:], scales[:]
 
         def bank(key, shape, dtype):
-            filled[key] = psum.tile(shape, dtype, name="bank", tag=f"bank{len(order) % BANKS}")
-            order.append(key)
+            filled[key] = psum.tile(shape, dtype, name="bank", tag=f"bank{tenants.index(key) % BANKS}")
             return filled[key]
 
-        def turns(dst, rows):
-            return [
-                (dst[:, u, a * P : (a + 1) * P], rows[:, a, :].bitcast(F32)[:, u : 2 * P : 2]) for a in (0, 1) for u in (0, 1)
-            ]
+        def turn(dst, rows, i):
+            a, u = divmod(i, 2)
+            nc.tensor.transpose(dst[:, u, a * P : (a + 1) * P], rows[:, a, :].bitcast(F32)[:, u : 2 * P : 2], ident[:])
 
-        def turn(pair):
-            nc.tensor.transpose(pair[0], pair[1], ident[:])
+        def turn_x(j, *parts):
+            if parts[0] == 0:
+                bank(("scale", j), [P, 2, 2 * P], F32)
+            for i in parts:
+                turn(filled["scale", j], xs[j], i)
 
-        def fill_x(j):
-            for pair in turns(bank(("x", j), [P, 2, 2 * P], F32), xs[j]):
-                turn(pair)
-
-        def fill_wb(n, h):
-            for pair in turns(bank(("wb", n, h), [P, 2, 2 * P], F32), wbr[n][:, 2 * h : 2 * h + 2, :]):
-                turn(pair)
-
-        def by_tokens(u):
-            return u >= SPLIT_FROM
-
-        def parts(u):
-            if by_tokens(u):
-                return [(n, slice(2 * P * n, 2 * P * (n + 1)), slice(2 * P * (u % 2), 2 * P * (u % 2 + 1))) for n in (0, 1)]
-            return [(u % 2, slice(0, T), slice(0, T))]
+        def turn_wb(n, h):
+            dst = bank(("unload_wb", n, h), [P, 2, 2 * P], F32)
+            for i in range(4):
+                turn(dst, wbr[n][:, 2 * h : 2 * h + 2, :], i)
 
         def fill_h(u, t):
-            acc = bank(("h", u, t), [P, T], F32)
-            for n, cols, tokens in parts(u):
-                nc.tensor.matmul_mx(
-                    out=acc[:, cols],
-                    lhsT=w1p[:, n, t].rearrange("p m b -> p (m b)").bitcast(FP4X4),
-                    lhsT_scale=wsp[:, n, t, :],
-                    rhs=xc[u // 2][:, tokens].bitcast(FP8X4),
-                    rhs_scale=xsc[u // 2][:, tokens],
-                    start=True,
-                    stop=True,
-                )
-
-        def whole_rows(g):
-            return by_tokens(2 * g)
-
-        def place(n):
-            g, r = divmod(n, 8)
-            if by_tokens(2 * g):
-                return 2 * g + r // 4, r % 2, (r % 2 * 2 + r % 4 // 2) * P
-            if whole_rows(g):
-                return 2 * g + r % 2, r % 2, r // 2 * P
-            return n // 4, n // 4 % 2, n % 4 * P
-
-        def fill_y(n):
-            u, chunk, first = place(n)
-            cols = slice(first, first + P)
             nc.tensor.matmul_mx(
-                out=bank(("y", n), [P, BLK], F32)[:],
-                lhsT=hc[u][:, cols].bitcast(FP8X4),
-                lhsT_scale=hs[u][:, cols],
-                rhs=wbc[chunk][:].bitcast(FP8X4),
-                rhs_scale=wbs[chunk][:],
+                out=bank(("relu_h", u, t), [P, T], F32)[:],
+                lhsT=w1p[:, u % 2, t].rearrange("p m b -> p (m b)").bitcast(FP4X4),
+                lhsT_scale=wsp[:, u % 2, t, :],
+                rhs=xc[u // 2].bitcast(FP8X4),
+                rhs_scale=xsc[u // 2],
                 start=True,
                 stop=True,
             )
 
-        def fill_m(u, a):
-            j = x_of(u - 1)
+        def place(n):
+            if n < 16:
+                return divmod(n, 4)
+            return n // 8 * 2 + n % 2, n % 8 // 2
+
+        def fill_y(n):
+            u, a = place(n)
+            cols = slice(a * P, (a + 1) * P)
+            nc.tensor.matmul_mx(
+                out=bank(("bias", n), [P, BLK], F32)[:],
+                lhsT=hc[u][:, cols].bitcast(FP8X4),
+                lhsT_scale=hs[u][:, cols],
+                rhs=wbc[u % 2][:].bitcast(FP8X4),
+                rhs_scale=wbs[u % 2][:],
+                start=True,
+                stop=True,
+            )
+
+        def weave(u, a):
             if a % 2 == 0:
-                bank(("e", u, a // 2), [P, 2, P, 4], BF16)
-            if a == 0 and live(j):
-                woven[u] = turns(bank(("x", j), [P, 2, 2 * P], F32), xs[j])
-            filled["m", u, a] = filled["e", u, a // 2]
-            if live(j):
-                turn(woven[u][a])
+                bank(("unload_h", u, a // 2), [P, 2, P, 4], BF16)
             nc.tensor.matmul(
-                out=filled["m", u, a][:, a % 2].rearrange("p r t -> p (r t)"),
+                out=flat(filled["unload_h", u, a // 2][:, a % 2]),
                 lhsT=identb[:],
                 rhs=hp[u][:, :, a * P : (a + 1) * P].rearrange("p t r -> p r t"),
                 start=True,
                 stop=True,
             )
 
-        def widen_x(j):
-            if live(j):
-                xs[j] = work.tile([P, 2, IN], BF16, name="xs", tag="xs", bufs=5)
-                src = xb[j // 2][:, 2 * (j % 2) : 2 * (j % 2) + 2, :].rearrange("p a k -> p (a k)").bitcast(FP8)
-                nc.scalar.copy(out=xs[j][:].rearrange("p a k -> p (a k)"), in_=src)
+        def warm(i):
+            idle = bank(("warm", i), [P, 2, P], F32)
+            nc.tensor.matmul(out=idle[:], lhsT=ident[:], rhs=ident[:].unsqueeze(1).to_broadcast([P, 2, P]), start=True, stop=True)
 
-        def scale_x(j):
+        def widen(j):
+            xs[j] = work.tile([P, 2, IN], BF16, name="xs", tag="xs", bufs=5)
+            src = xb[j // 2][:, 2 * (j % 2) : 2 * (j % 2) + 2, :].rearrange("p a k -> p (a k)").bitcast(FP8)
+            nc.scalar.copy(out=xs[j][:].rearrange("p a k -> p (a k)"), in_=src)
+
+        def scale(j):
             g, h = divmod(j, 2)
             if h == 0:
-                xg[g] = single("xg")[:]
+                xg[g] = work.tile([P, T, 4], BF16, name="xg", tag="xg", align_bytes=64, bufs=2)
             nc.vector.tensor_tensor(
                 out=xg[g][:, 2 * P * h : 2 * P * (h + 1), :].rearrange("p r (u e) -> p r u e", u=2),
-                in0=filled["x", j][:].bitcast(BF16).rearrange("p u (r e) -> p r u e", e=2),
+                in0=filled["scale", j][:].bitcast(BF16).rearrange("p u (r e) -> p r u e", e=2),
                 in1=sc[:].rearrange("p (u e) -> p u e", u=2).unsqueeze(1).to_broadcast([P, 2 * P, 2, 2]),
                 op=ALU.mult,
             )
 
-        def quant_x(*halves):
-            g = halves[0] // 2
-            if halves[0] % 2 == 0:
-                codes, scales = code_tiles(T, "x", 3)
-                xc[g], xsc[g] = codes[:], scales[:]
-            cols = slice(2 * P * (halves[0] % 2), 2 * P * (halves[-1] % 2 + 1))
-            quantize(xg[g][:, cols].rearrange("p r t -> p (r t)"), xc[g][:, cols], xsc[g][:, cols])
-            coded.extend(halves)
+        def quant_x(g):
+            xc[g], xsc[g] = code_tiles("x", 3)
+            quantize(flat(xg[g][:]), xc[g], xsc[g])
 
         def relu_h(u, t):
             if t == 0:
                 hp[u] = work.tile([P, 4, T], BF16, name="hp", tag="hp")
-            for n, cols, tokens in parts(u):
-                nc.scalar.activation(out=hp[u][:, t, cols], in_=filled["h", u, t][:, cols], func=ACT.Relu, bias=b1c[:, n, t : t + 1])
+            nc.scalar.activation(out=hp[u][:, t, :], in_=filled["relu_h", u, t][:], func=ACT.Relu, bias=b1c[:, u % 2, t : t + 1])
 
-        def unload_e(u, half):
+        def unload_h(u, half):
             if half == 0:
-                hg[u] = work.tile([P, T, 4], BF16, name="hw", tag="hw", align_bytes=64, bufs=2)[:]
+                hw[u] = work.tile([P, T, 4], BF16, name="hw", tag="hw", align_bytes=64, bufs=2)
             nc.scalar.copy(
-                out=hg[u][:, 2 * P * half : 2 * P * (half + 1), :].rearrange("p r t -> p (r t)").bitcast(F32),
-                in_=filled["e", u, half][:].rearrange("p a r t -> p (a r t)").bitcast(F32),
+                out=flat(hw[u][:, 2 * P * half : 2 * P * (half + 1), :]).bitcast(F32),
+                in_=filled["unload_h", u, half][:].rearrange("p a r t -> p (a r t)").bitcast(F32),
             )
 
-        def interleave_gpsimd(u):
-            cut = 2 * P if u in (0, UNITS - 1) else T
-            if u > 1:
-                hg[u] = hg[u - 1][:, :cut]
-            else:
-                hg[u] = work.tile([P, cut, 4], BF16, name="hg", tag="hg", align_bytes=64, bufs=1)[:]
+        def shared(u):
+            return u in (0, UNITS - 1)
+
+        def weave_gpsimd(u):
+            cut = 2 * P if shared(u) else T
             nc.gpsimd.tensor_scalar(
-                out=hg[u], in0=hp[u][:, :, :cut].rearrange("p t r -> p r t"), scalar1=1.0, scalar2=0.0, op0=ALU.mult, op1=ALU.add
+                out=hl[:] if u == UNITS - 1 else hg[:, :cut], in0=hp[u][:, :, :cut].rearrange("p t r -> p r t"), scalar1=1.0, scalar2=0.0, op0=ALU.mult, op1=ALU.add
             )
 
-        def interleave_vector(u):
-            both["rest"] = work.tile([P, 2 * P, 4], BF16, name="rest", tag="rest", align_bytes=64, bufs=1)
+        def weave_vector(u):
             nc.vector.tensor_copy(
-                out=both["rest"][:].rearrange("p (c i) t -> p c t i", i=4),
+                out=rest[:].rearrange("p (c i) t -> p c t i", i=4),
                 in_=hp[u][:, :, 2 * P :].rearrange("p t (c i) -> p c t i", i=4),
             )
 
-        def quant_h(u, *parts):
-            if u not in hc:
-                codes, scales = code_tiles(T, "h", 5)
-                hc[u], hs[u] = codes[:], scales[:]
-            if not parts:
-                quantize(hg[u].rearrange("p r t -> p (r t)"), hc[u], hs[u])
-            if "rest" in parts:
-                quantize(both["rest"][:].rearrange("p r t -> p (r t)"), hc[u][:, 2 * P :], hs[u][:, 2 * P :])
-            if "first" in parts:
-                quantize(hg[u].rearrange("p r t -> p (r t)"), hc[u][:, : 2 * P], hs[u][:, : 2 * P])
-            if "first" in parts or not parts:
-                ready_h.append(u)
-
-        def ring_columns(c0, c1):
-            start = c0 % (RING * BLK)
-            return ring[:, start : start + c1 - c0]
-
-        waiting = []
-
-        def bias_y(n, lo, hi):
-            first = place(n)[1] * BLK
-            c0, c1 = n * BLK + lo, n * BLK + hi
-            nc.vector.tensor_tensor(out=ring_columns(c0, c1), in0=filled["y", n][:, lo:hi], in1=bbr[:, first + lo : first + hi], op=ALU.add)
-            if waiting and waiting[-1][1] == c0:
-                waiting[-1] = (waiting[-1][0], c1)
+        def quant_h(u):
+            hc[u], hs[u] = code_tiles("h", 5)
+            if shared(u):
+                quantize(flat(rest[:]), hc[u][:, 2 * P :], hs[u][:, 2 * P :])
+                quantize(flat(hl[:] if u else hg[:, : 2 * P]), hc[u][:, : 2 * P], hs[u][:, : 2 * P])
             else:
-                waiting.append((c0, c1))
-            if hi == BLK:
-                emptied.add(("y", n))
+                quantize(flat(hw[u][:] if by_pe(u) else hg[:]), hc[u], hs[u])
 
-        def store(u, a0, a1):
-            g, n = divmod(u, 2)
-            rows = out[T * g : T * (g + 1), n * BLK : (n + 1) * BLK].rearrange("(p a) c -> p a c", a=4)
-            cols = ring_columns((4 * u + a0) * BLK, (4 * u + a1) * BLK)
-            nc.sync.dma_start(out=rows[:, a0:a1, :], in_=cols.rearrange("p (a c) -> p a c", c=BLK))
-
-        def store_rows(g, a0, a1):
-            rows = out[T * g : T * (g + 1), :].rearrange("(p a) c -> p (a c)", a=4)
-            nc.sync.dma_start(out=rows[:, a0 * HID : a1 * HID], in_=ring_columns((8 * g + 2 * a0) * BLK, (8 * g + 2 * a1) * BLK))
-
-        def cut(c0, c1, width):
-            return [(j, max(c0 - width * j, 0), min(c1 - width * j, width)) for j in range(c0 // width, -(-c1 // width))]
-
-        cleared = [0] * TILES
-
-        late = []
+        def bias(n, lo, hi):
+            first = place(n)[0] % 2 * BLK
+            nc.vector.tensor_tensor(
+                out=ring[:, n * BLK + lo : n * BLK + hi], in0=filled["bias", n][:, lo:hi], in1=bbr[:, first + lo : first + hi], op=ALU.add
+            )
 
         def relu(engine, c0, c1):
-            part = ring_columns(c0, c1)
+            part = ring[:, c0:c1]
             if engine == "vector":
                 nc.vector.tensor_scalar(out=part, in0=part, scalar1=0.0, scalar2=None, op0=ALU.max)
             elif engine == "gpsimd":
                 nc.gpsimd.tensor_scalar(out=part, in0=part, scalar1=BIG, scalar2=0.0, op0=ALU.min, op1=ALU.max)
-                late.append((c0, c1))
-                return
             else:
                 nc.scalar.activation(out=part, in_=part, func=ACT.Relu)
-            store_cleared(c0, c1)
 
-        def store_late():
-            store_cleared(*late.pop())
-
-        def store_cleared(c0, c1):
-            done = []
-            for n, lo, hi in cut(c0, c1, BLK):
-                cleared[n] = cleared[n] + hi - lo
-                if cleared[n] == BLK:
-                    done.append(n)
-            if done:
-                for g, lo, hi in cut(done[0], done[-1] + 1, 8):
-                    if whole_rows(g):
-                        whole = [a for a in range(lo // 2, (hi + 1) // 2) if cleared[8 * g + 2 * a] + cleared[8 * g + 2 * a + 1] == HID]
-                        if whole:
-                            store_rows(g, whole[0], whole[-1] + 1)
-                    else:
-                        for u, a0, a1 in cut(8 * g + lo, 8 * g + hi, 4):
-                            store(u, a0, a1)
-
-        reach = [0]
-
-        def relu_gpsimd():
-            c0, c1 = waiting.pop()
-            reach[0] = c1 - G_RELU
-            assert reach[0] >= c0
-            if reach[0] > c0:
-                waiting.append((c0, reach[0]))
-            relu("gpsimd", reach[0], c1)
-
-        def relu_oldest(engine, cols, below=TILES * BLK):
-            while waiting and cols > 0 and waiting[0][0] < below:
-                c0, c1 = waiting.pop(0)
-                end = min(c1, c0 + cols, below)
-                if end < c1:
-                    waiting.insert(0, (end, c1))
-                relu(engine, c0, end)
-                cols = cols - (end - c0)
-
-        def relu_skipped(engine, cols):
-            relu_oldest(engine, cols, reach[0])
-
-        def relu_tile():
-            if waiting:
-                relu_oldest("scalar", BLK - waiting[0][0] % BLK)
+        def store(c0, c1):
+            g = c0 // (8 * BLK)
+            rows = out[T * g : T * (g + 1), :]
+            if g < 2:
+                u, a = place(c0 // BLK)
+                nc.sync.dma_start(out=rows.rearrange("(p a) (n c) -> p n a c", a=4, n=2)[:, u % 2, a : a + (c1 - c0) // BLK, :], in_=ring[:, c0:c1].rearrange("p (a c) -> p a c", c=BLK))
+            else:
+                first = g * 8 * BLK
+                nc.sync.dma_start(out=rows.rearrange("(p a) c -> p (a c)", a=4)[:, c0 - first : c1 - first], in_=ring[:, c0:c1])
 
         def permute_words():
             nc.vector.tensor_copy(out=w1p[:], in_=w1r[:].rearrange("p (n m t b) -> p n t m b", n=2, t=4, b=2))
 
         def permute_scales(n):
             nc.vector.tensor_copy(out=wsp[:, n], in_=wsr[:].rearrange("p (n m t) -> p n t m", n=2, t=4)[:, n])
-            permuted.add(n)
 
         def unload_wb(n, h):
             if h == 0:
-                wbg[n] = work.tile([P, BLK, 4], BF16, name="wbg", tag="wbg", align_bytes=64, bufs=2)
-            words = wbg[n][:].rearrange("p o t -> p (o t)").bitcast(F32).rearrange("p (r a u) -> p r a u", a=4, u=2)
-            nc.scalar.copy(out=words[:, :, 2 * h : 2 * h + 2, :], in_=filled["wb", n, h][:].rearrange("p u (a r) -> p r a u", a=2))
-
-        made = set()
-
-        def warm():
-            key = ("idle", len(order))
-            idle = bank(key, [P, 2, P], F32)
-            nc.tensor.matmul(out=idle[:], lhsT=ident[:], rhs=ident[:].unsqueeze(1).to_broadcast([P, 2, P]), start=True, stop=True)
-            emptied.add(key)
+                wbg[n] = work.tile([P, BLK, 4], BF16, name="wbg", tag="hw", align_bytes=64, bufs=2)
+            words = flat(wbg[n][:]).bitcast(F32).rearrange("p (r a u) -> p r a u", a=4, u=2)
+            nc.scalar.copy(out=words[:, :, 2 * h : 2 * h + 2, :], in_=filled["unload_wb", n, h][:].rearrange("p u (a r) -> p r a u", a=2))
 
         def quant_wb(n):
-            quantize(wbg[n][:].rearrange("p r t -> p (r t)"), wbc[n][:], wbs[n][:])
-            made.add(n)
+            quantize(flat(wbg[n][:]), wbc[n][:], wbs[n][:])
 
-        def x_of(s):
-            if s + HEAD_X < SPLIT_FROM:
-                return s + HEAD_X
-            return SPLIT_FROM + (s - LAST_PE + 3) // 2 if by_pe(s + 1) else -1
+        vector, scalar, gpsimd, tensor, sync = [], [], [], [], []
+        waiting = [(0, TILES * BLK)]
+        cleared = [0] * (TILES * 2)
 
-        def halves_at(s):
-            if s % 2:
-                return ()
-            return (s + 4, s + 5) if s + 4 < SPLIT_FROM else (x_of(s - 1),)
+        def take(queue, engine, c0, c1, grain):
+            queue.append(("relu", engine, c0, c1))
+            for i in range(c0 // 256, -(-c1 // 256)):
+                cleared[i] = cleared[i] + min(c1, 256 * (i + 1)) - max(c0, 256 * i)
+            step = grain // 256
+            whole = [i for i in range(c0 // grain * step, -(-c1 // grain) * step, step) if sum(cleared[i : i + step]) == grain]
+            while whole:
+                run = 8 if whole[0] < 32 else 16
+                part = [i for i in whole if i // run == whole[0] // run]
+                sync.append(("store", part[0] * 256, (part[-1] + step) * 256))
+                whole = whole[len(part) :]
 
-        def do(f, *args):
-            return (None, lambda: f(*args))
+        def clear(queue, engine, cols, below, grain=BLK):
+            while cols > 0 and waiting and waiting[0][0] < below * BLK:
+                c0, end = waiting.pop(0)
+                c1 = min(c0 + cols, below * BLK, end)
+                if c1 < end:
+                    waiting.insert(0, (c1, end))
+                take(queue, engine, c0, c1, grain)
+                cols = cols - (c1 - c0)
 
-        def X(j):
-            return [(("x", j), lambda: scale_x(j))] if live(j) else []
+        def clear_newest(queue, cols, c1):
+            start, end = waiting.pop()
+            c0 = max(start, c1 - cols)
+            if c0 > start:
+                waiting.append((start, c0))
+            waiting.append((c1, end))
+            take(queue, "gpsimd", c0, c1, BLK)
+
+        def Y(n0, n1):
+            return [("bias", n, 0, BLK) for n in range(n0, n1)]
 
         def H(u, *planes):
-            return [(("h", u, t), lambda t=t: relu_h(u, t)) for t in planes] if live(u) else []
+            return [("relu_h", u, t) for t in planes]
 
-        def E(u, half):
-            return [(("e", u, half), lambda: unload_e(u, half))] if by_pe(u) else []
+        def MH(u, *planes):
+            return [("fill_h", u, t) for t in planes]
 
-        def M(u, *parts):
-            return [(("m", u, a), lambda: None) for a in parts] if by_pe(u) else []
+        def MY(*tiles):
+            return [("fill_y", n) for n in tiles]
 
-        def W(n, h):
-            return [(("wb", n, h), lambda: unload_wb(n, h))]
+        def TX(j):
+            return [("turn_x", j, 0, 1, 2, 3)]
 
-        def columns_of(s):
-            if s < 2:
-                return 3 * BLK
-            if live(x_of(s)):
-                return LONG_X if by_pe(s + 1) else WINDOW - 2 * BLK
-            return WINDOW
+        def halves(k):
+            return [j for j in (2 * k + 6, 2 * k + 7) if HEAD_X < j < UNITS]
 
-        taken = [0, 0]
-
-        def Y(count):
-            c0 = taken[0]
-            taken[0] = min((c0 // BLK + count) * BLK, taken[1])
-            return [(("y", n), lambda n=n, lo=lo, hi=hi: bias_y(n, lo, hi)) for n, lo, hi in cut(c0, taken[0], BLK) if hi > lo]
-
-        steps = [do(warm), do(warm), do(widen_x, 0), do(widen_x, 1), do(permute_words), do(warm), do(widen_x, 2), do(widen_x, 3), do(warm)]
-        steps += X(0) + [do(widen_x, 4)] + X(1) + [do(permute_scales, 0), do(quant_x, 0, 1), do(widen_x, 5), do(widen_x, 6), do(widen_x, 7)]
-        steps += X(2) + X(3) + [do(permute_scales, 1), do(quant_x, 2, 3)] + H(0, 0, 1, 2, 3) + [do(interleave_gpsimd, 0)] + X(4) + X(5) + H(1, 0, 1)
-        steps += W(0, 0) + [do(interleave_vector, 0)] + H(1, 2) + W(0, 1) + H(1, 3) + [do(quant_x, 4, 5), do(widen_x, 8), do(widen_x, 9)]
-        for s in range(UNITS - 2):
-            j = x_of(s)
-            with_x = live(j)
-            first = taken[0]
-            taken[1] = first + columns_of(s)
-            if by_pe(s):
-                steps += [do(relu_skipped, "vector", WINDOW) if by_pe(s + 2) else do(relu_oldest, "vector", WINDOW, first - LEFT)]
-            if s == 2:
-                steps += [do(relu_oldest, "vector", 2 * P)]
-            steps += [do(quant_h, s) if s else do(quant_h, 0, "rest", "first")]
-            if s < 2:
-                steps += [do(quant_wb, s)]
-            elif halves_at(s):
-                steps += [do(quant_x, *halves_at(s))]
-            elif not by_pe(s + 1):
-                steps += [do(relu_oldest, "vector", WINDOW, first - LEFT)]
-            steps += [do(relu_gpsimd) if by_pe(s + 1) else do(interleave_gpsimd, s + 1)]
-            wide = [do(widen_x, x_of(s + WIDEN_LEAD))]
-            share = [do(relu_oldest, "scalar", S_SHARE if by_pe(s) else S_EARLY, taken[1] - G_RELU if by_pe(s + 2) else taken[1])]
-            if s == 0:
-                steps += X(j) + H(2, 0, 1) + W(1, 0) + Y(1) + H(2, 2) + Y(9) + W(1, 1) + H(2, 3) + wide + share
-            elif by_pe(s + 1):
-                steps += H(s + 2, 0) + Y(1) + H(s + 2, 1) + Y(2) + M(s + 1, 0, 1, 2, 3) + E(s + 1, 0) + [do(relu_skipped, "scalar", 0 if by_pe(s + 3) else BLK)] + X(j)
-                steps += E(s + 1, 1) + Y(1) + H(s + 2, 2) + Y(9) + H(s + 2, 3) + wide + [do(store_late)]
-            elif with_x:
-                steps += H(s + 2, 0) + Y(1) + H(s + 2, 1) + X(j) + H(s + 2, 2) + Y(1) + H(s + 2, 3) + wide + share + Y(9)
-            elif by_pe(s + 2):
-                steps += H(s + 2, 0) + Y(1) + H(s + 2, 1) + Y(1) + H(s + 2, 2) + Y(1) + H(s + 2, 3) + wide + share + Y(9)
-            else:
-                steps += H(s + 2, 0, 1) + Y(1) + H(s + 2, 2) + Y(1) + [do(relu_tile)] + Y(1) + H(s + 2, 3) + [do(relu_tile)] + Y(9) + [do(relu_tile)]
-
-        def until(n):
+        def passes(u, pair):
             run = []
-            taken[1] = n
-            while taken[0] < n:
-                run += [do(relu_tile)] + Y(1)
+            for a in range(4):
+                j = pair[a // 2] if a // 2 < len(pair) else -1
+                run += [("weave", u, a)]
+                if j >= 0:
+                    run += [("turn_x", j, 2 * (a % 2), 2 * (a % 2) + 1)]
             return run
 
-        steps += [do(relu_tile)] * 2 + [do(quant_h, UNITS - 2), do(interleave_vector, UNITS - 1), do(interleave_gpsimd, UNITS - 1)]
-        steps += until((TILES - 6) * BLK) + [do(quant_h, UNITS - 1, "rest", "first")]
-        steps += until((TILES - 1) * BLK) + [do(relu_tile)] * 3
-        taken[1] = TILES * BLK - 2 * P
-        steps += Y(1)
-        taken[1] = TILES * BLK
-        steps += Y(1) + [do(relu_oldest, "vector", 2 * P)] * 2
+        vector += [("permute_words",), ("scale", 0), ("scale", 1), ("permute_scales", 0), ("quant_x", 0), ("scale", 2), ("scale", 3)]
+        vector += [("permute_scales", 1), ("quant_x", 1), ("scale", 4), ("scale", 5), ("weave_vector", 0), ("quant_x", 2), ("quant_h", 0), ("quant_wb", 0)]
+        vector += [("scale", 6)] + Y(0, 3) + [("quant_h", 1), ("quant_wb", 1)] + Y(3, 4) + [("scale", 7)] + Y(4, 6)
+        vector += [("quant_h", 2), ("quant_x", 3)] + Y(6, 7) + [("scale", 8)] + Y(7, 9)
+        scalar += [("widen", j) for j in range(8)] + H(0, 0, 1, 2, 3) + H(1, 0, 1) + [("unload_wb", 0, 0)] + H(1, 2) + [("unload_wb", 0, 1)] + H(1, 3)
+        scalar += [("widen", 8)] + H(2, 0, 1) + [("unload_wb", 1, 0)] + H(2, 2) + [("unload_wb", 1, 1)] + H(2, 3)
+        scalar += H(3, 0, 1, 2, 3) + [("widen", 9)] + H(4, 0, 1, 2, 3)
+        clear(scalar, "scalar", S_RELU, 6)
+        gpsimd += [("weave_gpsimd", u) for u in range(4)]
+        tensor += [("warm", 0), ("warm", 1)] + TX(0) + TX(1) + [("warm", 2)] + TX(2) + TX(3) + [("warm", 3)] + MH(0, 0, 1, 2, 3) + TX(4) + TX(5)
+        tensor += MH(1, 0, 1) + [("turn_wb", 0, 0)] + MH(1, 2) + [("turn_wb", 0, 1)] + MH(1, 3) + TX(6) + MH(2, 0, 1) + [("turn_wb", 1, 0)]
+        tensor += MY(0) + MH(2, 2) + MY(1, 2) + [("turn_wb", 1, 1)] + MH(2, 3) + MH(3, 0) + MY(3) + MH(3, 1) + TX(7) + MH(3, 2) + MY(4) + MH(3, 3) + MY(5)
+        tensor += MH(4, 0) + MY(6) + MH(4, 1) + TX(8) + MH(4, 2, 3) + MY(7, 8) + MH(5, 0) + MY(9) + MH(5, 1)
 
-        keys = [key for key, run in steps if key is not None]
-
-        def fill_next():
-            for key in keys:
-                if key not in filled:
-                    break
+        for k in range(1, GROUPS):
+            first, end = (9 if k == 1 else 8 * k - 1), 8 * k + 7
+            pair = halves(k)
+            odd, even = 2 * k + 3, 2 * k + 4
+            if k == 2:
+                clear(vector, "vector", V_EARLY, first - 1)
+            if not pair and by_pe(even - 2):
+                clear(vector, "vector", V_RELU, first - 1)
+            if 3 < k + 2 < GROUPS:
+                vector += [("quant_x", k + 2)]
+            if odd > UNITS:
+                vector += [("weave_vector", UNITS - 1)]
+            piece = PIECE if by_pe(even - 2) else 0
+            if k > 1:
+                vector += [("quant_h", 2 * k)]
+            if piece:
+                vector += [("bias", first, 0, piece)]
+            vector += [("quant_h", 2 * k + 1)]
+            if odd == UNITS - 1:
+                clear(vector, "vector", BLK, first - 1)
+            vector += [("bias", first, piece, BLK)] + [("scale", j) for j in pair] + Y(first + 1, end)
+            ys = [MY(n) for n in range(first + 1, end + 1)]
+            ys = ys + [[]] * (8 - len(ys))
+            if by_pe(even - 2):
+                clear_newest(gpsimd, G_BASE + G_HALF * (len(pair) if k > 1 else 0), first * BLK + PIECE)
+                gpsimd += [("weave_gpsimd", odd)]
+                wide = [[("widen", j)] for j in halves(k + 1)] + [[], []]
+                scalar += H(odd, 0, 1) + [("unload_h", even - 2, 0)] + wide[0] + [("unload_h", even - 2, 1)] + H(odd, 2, 3)
+                tensor += passes(even - 2, pair) + MH(odd, 2) + ys[0] + MH(odd, 3) + ys[1]
+                scalar += H(even, 0, 1, 2, 3) + wide[1]
+                if pair:
+                    clear(scalar, "scalar", S_RELU, end - 2)
+                for t in range(4):
+                    tensor += MH(even, t) + ys[2 + t]
+                tensor += ys[6] + MH(odd + 2, 0) + ys[7] + MH(odd + 2, 1)
+            elif odd < UNITS:
+                gpsimd += [("weave_gpsimd", odd - 1), ("weave_gpsimd", odd)]
+                scalar += H(odd, 0, 1, 2, 3)
+                tensor += MH(odd, 2, 3)
+                for n in range(8):
+                    tensor += ys[n]
             else:
-                return False
-            kind = key[0]
-            need = 1
-            if kind == "x":
-                ready = key[1] in xs
-            elif kind == "h":
-                ready = (key[1] if by_tokens(key[1]) else key[1] | 1) in coded and key[1] % 2 in permuted
-            elif kind == "y":
-                ready = place(key[1])[0] in ready_h and place(key[1])[1] in made
-            elif kind == "m":
-                ready = ("h", key[1], 3) in emptied
-                need = (1 + live(x_of(key[1] - 1)), 0, 1, 0)[key[2]]
-            else:
-                ready = True
-            for k in range(len(order), len(order) + need):
-                ready = ready and (k < BANKS or order[k - BANKS] in emptied)
-            if not ready:
-                return False
-            if kind == "x":
-                fill_x(key[1])
-            elif kind == "h":
-                fill_h(key[1], key[2])
-            elif kind == "y":
-                fill_y(key[1])
-            elif kind == "m":
-                fill_m(key[1], key[2])
-            else:
-                fill_wb(key[1], key[2])
-            return True
-
-        for key, run in steps:
-            while fill_next():
-                pass
-            run()
-            if key is not None and key[0] != "y":
-                emptied.add(key)
+                for n in range(8):
+                    tensor += ys[n]
+        vector += [("bias", TILES - 1, 0, 2 * P), ("bias", TILES - 1, 2 * P, BLK)]
+        while waiting[0][0] < (TILES - 1) * BLK:
+            clear(scalar, "scalar", BLK - waiting[0][0] % BLK, TILES - 1, HID if waiting[0][0] < (TILES - 2) * BLK else BLK)
+        clear(vector, "vector", 2 * P, TILES, 2 * P)
+        clear(vector, "vector", 2 * P, TILES, 2 * P)
         assert not waiting
+
+        def tenant(step):
+            if step[0] == "turn_x":
+                return ("scale", step[1]) if step[2] == 0 else None
+            if step[0] == "weave":
+                return ("unload_h", step[1], step[2] // 2) if step[2] % 2 == 0 else None
+            return ({"turn_wb": "unload_wb", "fill_h": "relu_h", "fill_y": "bias", "warm": "warm"}[step[0]],) + step[1:]
+
+        tenants.extend([tenant(step) for step in tensor if tenant(step)])
+        by_gpsimd = [u for u in range(UNITS) if not by_pe(u)]
+        wide_tiles = [("quant_wb", 0), ("quant_wb", 1)] + [("quant_h", u) for u in range(UNITS) if by_pe(u)]
+        plane_tiles = [step[1] for step in scalar if step[0] == "relu_h" and step[2] == 0]
+        relus = [step for step in vector + scalar + gpsimd if step[0] == "relu"]
+
+        def woven(u):
+            if by_pe(u):
+                return [("weave", u, 3)]
+            return [("weave_gpsimd", u)] + ([("weave_vector", u)] if shared(u) else [])
+
+        def needs(step):
+            kind, i = step[0], step[1] if len(step) > 1 else None
+            before = []
+            if step in tensor and tenant(step) and tenants.index(tenant(step)) >= BANKS:
+                before += [tenants[tenants.index(tenant(step)) - BANKS]]
+            if kind == "widen" and i >= 5:
+                before += [("turned", i - 5)]
+            elif kind == "turn_x":
+                before += [("widen", i)]
+            elif kind == "scale":
+                before += [("turned", i)] + ([("quant_x", i // 2 - 2)] if i >= 4 else [])
+            elif kind == "quant_x" and i >= 3:
+                before += MH(2 * i - 5, 3)
+            elif kind == "fill_h":
+                before += [("quant_x", i // 2), ("permute_scales", i % 2)]
+            elif kind == "relu_h":
+                before += MH(i, step[2]) + (woven(plane_tiles[plane_tiles.index(i) - 3]) if i >= 3 else [])
+            elif kind == "weave" or kind == "weave_vector":
+                before += H(i, 3)
+            elif kind == "weave_gpsimd":
+                before += H(i, 3) + ([("quant_h", by_gpsimd[by_gpsimd.index(i) - 1])] if not shared(i) else [])
+            elif kind == "unload_h":
+                before += [("weave", i, 2 * step[2] + 1), wide_tiles[wide_tiles.index(("quant_h", i)) - 2]]
+            elif kind == "unload_wb":
+                before += [("turn_wb", i, step[2])]
+            elif kind == "quant_wb":
+                before += [("unload_wb", i, 1)]
+            elif kind == "quant_h":
+                before += ([("unload_h", i, 1)] if by_pe(i) else woven(i)) + [("fill_y", n) for n in range(TILES) if place(n)[0] == i - 5]
+            elif kind == "fill_y":
+                before += [("quant_h", place(i)[0]), ("quant_wb", place(i)[0] % 2)]
+            elif kind == "bias":
+                before += MY(i)
+            elif kind == "relu":
+                before += [b for b in vector if b[0] == "bias" and b[1] * BLK + b[2] < step[3] and b[1] * BLK + b[3] > step[2]]
+            elif kind == "store":
+                before += [r for r in relus if r[2] < step[2] and r[3] > step[1]]
+            return before
+
+        calls = {
+            "permute_words": permute_words, "permute_scales": permute_scales, "scale": scale, "quant_x": quant_x, "quant_h": quant_h,
+            "quant_wb": quant_wb, "weave_vector": weave_vector, "weave_gpsimd": weave_gpsimd, "weave": weave, "bias": bias, "relu": relu,
+            "widen": widen, "relu_h": relu_h, "unload_h": unload_h, "unload_wb": unload_wb, "warm": warm, "turn_x": turn_x,
+            "turn_wb": turn_wb, "fill_h": fill_h, "fill_y": fill_y, "store": store,
+        }
+        written = set()
+        queues = [list(queue) for queue in (tensor, vector, scalar, gpsimd, sync)]
+        while any(queues):
+            ready = [queue for queue in queues if queue and all(b in written for b in needs(queue[0]))]
+            assert ready
+            step = ready[0].pop(0)
+            calls[step[0]](*step[1:])
+            written.add(step)
+            if step[0] == "turn_x" and step[-1] == 3:
+                written.add(("turned", step[1]))
+            if step[0] == "bias" and step[3] == BLK:
+                written.add(step[:2])

@@ -25,13 +25,13 @@ TILES = 4 * UNITS
 BANKS = 8
 FIRST_PE = 4
 LAST_PE = 12
-HEAD_X = 8
 G_BASE = 1088
 G_HALF = 768
-S_RELU = 1408
+S_RELU = 1536
 PIECE = 64
-V_RELU = 2048
-V_EARLY = 2048
+V_RELU = 1536
+V_LATE = 1024
+S_LATE = 1024
 BIG = 3.4028234663852886e38
 
 
@@ -59,7 +59,6 @@ def tile_blockdiagmnistconvertible_pa_t_w4_kernel(tc, x_bytes, x_scale, W1_words
         wbs = [keep.tile([P, BLK], U8, name=f"wbs{n}", align_bytes=64) for n in range(2)]
         wbr = [keep.tile([P, 4, BLK], BF16, name=f"wbr{n}") for n in range(2)]
         hg = keep.tile([P, T, 4], BF16, name="hg", align_bytes=64)
-        hl = keep.tile([P, 2 * P, 4], BF16, name="hl", align_bytes=64)
         rest = keep.tile([P, 2 * P, 4], BF16, name="rest", align_bytes=64)
 
         def load_x(g):
@@ -144,7 +143,7 @@ def tile_blockdiagmnistconvertible_pa_t_w4_kernel(tc, x_bytes, x_scale, W1_words
             )
 
         def place(n):
-            if n < 16:
+            if n < 16 or n >= TILES - 8:
                 return divmod(n, 4)
             return n // 8 * 2 + n % 2, n % 8 // 2
 
@@ -215,7 +214,7 @@ def tile_blockdiagmnistconvertible_pa_t_w4_kernel(tc, x_bytes, x_scale, W1_words
         def weave_gpsimd(u):
             cut = 2 * P if shared(u) else T
             nc.gpsimd.tensor_scalar(
-                out=hl[:] if u == UNITS - 1 else hg[:, :cut], in0=hp[u][:, :, :cut].rearrange("p t r -> p r t"), scalar1=1.0, scalar2=0.0, op0=ALU.mult, op1=ALU.add
+                out=hg[:, :cut], in0=hp[u][:, :, :cut].rearrange("p t r -> p r t"), scalar1=1.0, scalar2=0.0, op0=ALU.mult, op1=ALU.add
             )
 
         def weave_vector(u):
@@ -228,7 +227,7 @@ def tile_blockdiagmnistconvertible_pa_t_w4_kernel(tc, x_bytes, x_scale, W1_words
             hc[u], hs[u] = code_tiles("h", 5)
             if shared(u):
                 quantize(flat(rest[:]), hc[u][:, 2 * P :], hs[u][:, 2 * P :])
-                quantize(flat(hl[:] if u else hg[:, : 2 * P]), hc[u][:, : 2 * P], hs[u][:, : 2 * P])
+                quantize(flat(hg[:, : 2 * P]), hc[u][:, : 2 * P], hs[u][:, : 2 * P])
             else:
                 quantize(flat(hw[u][:] if by_pe(u) else hg[:]), hc[u], hs[u])
 
@@ -250,9 +249,11 @@ def tile_blockdiagmnistconvertible_pa_t_w4_kernel(tc, x_bytes, x_scale, W1_words
         def store(c0, c1):
             g = c0 // (8 * BLK)
             rows = out[T * g : T * (g + 1), :]
-            if g < 2:
+            if g < 2 or g == GROUPS - 1:
                 u, a = place(c0 // BLK)
-                nc.sync.dma_start(out=rows.rearrange("(p a) (n c) -> p n a c", a=4, n=2)[:, u % 2, a : a + (c1 - c0) // BLK, :], in_=ring[:, c0:c1].rearrange("p (a c) -> p a c", c=BLK))
+                lo, width = c0 % BLK, min(BLK, c1 - c0)
+                count = (c1 - c0) // width
+                nc.sync.dma_start(out=rows.rearrange("(p a) (n c) -> p n a c", a=4, n=2)[:, u % 2, a : a + count, lo : lo + width], in_=ring[:, c0:c1].rearrange("p (a c) -> p a c", c=width))
             else:
                 first = g * 8 * BLK
                 nc.sync.dma_start(out=rows.rearrange("(p a) c -> p (a c)", a=4)[:, c0 - first : c1 - first], in_=ring[:, c0:c1])
@@ -283,7 +284,7 @@ def tile_blockdiagmnistconvertible_pa_t_w4_kernel(tc, x_bytes, x_scale, W1_words
             step = grain // 256
             whole = [i for i in range(c0 // grain * step, -(-c1 // grain) * step, step) if sum(cleared[i : i + step]) == grain]
             while whole:
-                run = 8 if whole[0] < 32 else 16
+                run = 8 if whole[0] < 32 or whole[0] >= 112 else 16
                 part = [i for i in whole if i // run == whole[0] // run]
                 sync.append(("store", part[0] * 256, (part[-1] + step) * 256))
                 whole = whole[len(part) :]
@@ -297,13 +298,13 @@ def tile_blockdiagmnistconvertible_pa_t_w4_kernel(tc, x_bytes, x_scale, W1_words
                 take(queue, engine, c0, c1, grain)
                 cols = cols - (c1 - c0)
 
-        def clear_newest(queue, cols, c1):
+        def clear_newest(queue, cols, c1, engine="gpsimd"):
             start, end = waiting.pop()
             c0 = max(start, c1 - cols)
             if c0 > start:
                 waiting.append((start, c0))
             waiting.append((c1, end))
-            take(queue, "gpsimd", c0, c1, BLK)
+            take(queue, engine, c0, c1, BLK)
 
         def Y(n0, n1):
             return [("bias", n, 0, BLK) for n in range(n0, n1)]
@@ -321,7 +322,7 @@ def tile_blockdiagmnistconvertible_pa_t_w4_kernel(tc, x_bytes, x_scale, W1_words
             return [("turn_x", j, 0, 1, 2, 3)]
 
         def halves(k):
-            return [j for j in (2 * k + 6, 2 * k + 7) if HEAD_X < j < UNITS]
+            return [j for j in (2 * k + 7, 2 * k + 8) if j < UNITS]
 
         def passes(u, pair):
             run = []
@@ -335,64 +336,75 @@ def tile_blockdiagmnistconvertible_pa_t_w4_kernel(tc, x_bytes, x_scale, W1_words
         vector += [("permute_words",), ("scale", 0), ("scale", 1), ("permute_scales", 0), ("quant_x", 0), ("scale", 2), ("scale", 3)]
         vector += [("permute_scales", 1), ("quant_x", 1), ("scale", 4), ("scale", 5), ("weave_vector", 0), ("quant_x", 2), ("quant_h", 0), ("quant_wb", 0)]
         vector += [("scale", 6)] + Y(0, 3) + [("quant_h", 1), ("quant_wb", 1)] + Y(3, 4) + [("scale", 7)] + Y(4, 6)
-        vector += [("quant_h", 2), ("quant_x", 3)] + Y(6, 7) + [("scale", 8)] + Y(7, 9)
+        vector += [("quant_h", 2), ("quant_x", 3)] + Y(6, 7) + [("scale", 8)] + Y(7, 8) + [("bias", 8, 0, BLK - PIECE)]
         scalar += [("widen", j) for j in range(8)] + H(0, 0, 1, 2, 3) + H(1, 0, 1) + [("unload_wb", 0, 0)] + H(1, 2) + [("unload_wb", 0, 1)] + H(1, 3)
         scalar += [("widen", 8)] + H(2, 0, 1) + [("unload_wb", 1, 0)] + H(2, 2) + [("unload_wb", 1, 1)] + H(2, 3)
-        scalar += H(3, 0, 1, 2, 3) + [("widen", 9)] + H(4, 0, 1, 2, 3)
-        clear(scalar, "scalar", S_RELU, 6)
+        scalar += H(3, 0, 1, 2, 3) + [("widen", 9)] + H(4, 0, 1, 2, 3) + [("widen", 10)]
         gpsimd += [("weave_gpsimd", u) for u in range(4)]
         tensor += [("warm", 0), ("warm", 1)] + TX(0) + TX(1) + [("warm", 2)] + TX(2) + TX(3) + [("warm", 3)] + MH(0, 0, 1, 2, 3) + TX(4) + TX(5)
         tensor += MH(1, 0, 1) + [("turn_wb", 0, 0)] + MH(1, 2) + [("turn_wb", 0, 1)] + MH(1, 3) + TX(6) + MH(2, 0, 1) + [("turn_wb", 1, 0)]
         tensor += MY(0) + MH(2, 2) + MY(1, 2) + [("turn_wb", 1, 1)] + MH(2, 3) + MH(3, 0) + MY(3) + MH(3, 1) + TX(7) + MH(3, 2) + MY(4) + MH(3, 3) + MY(5)
-        tensor += MH(4, 0) + MY(6) + MH(4, 1) + TX(8) + MH(4, 2, 3) + MY(7, 8) + MH(5, 0) + MY(9) + MH(5, 1)
+        tensor += MH(4, 0) + MY(6) + MH(4, 1) + TX(8) + MH(4, 2, 3) + MY(7) + MH(5, 0) + MY(8) + MH(5, 1)
 
-        for k in range(1, GROUPS):
+        for k in range(1, GROUPS - 1):
             first, end = (9 if k == 1 else 8 * k - 1), 8 * k + 7
             pair = halves(k)
             odd, even = 2 * k + 3, 2 * k + 4
-            if k == 2:
-                clear(vector, "vector", V_EARLY, first - 1)
-            if not pair and by_pe(even - 2):
-                clear(vector, "vector", V_RELU, first - 1)
-            if 3 < k + 2 < GROUPS:
-                vector += [("quant_x", k + 2)]
-            if odd > UNITS:
-                vector += [("weave_vector", UNITS - 1)]
-            piece = PIECE if by_pe(even - 2) else 0
-            if k > 1:
-                vector += [("quant_h", 2 * k)]
-            if piece:
-                vector += [("bias", first, 0, piece)]
-            vector += [("quant_h", 2 * k + 1)]
-            if odd == UNITS - 1:
-                clear(vector, "vector", BLK, first - 1)
-            vector += [("bias", first, piece, BLK)] + [("scale", j) for j in pair] + Y(first + 1, end)
             ys = [MY(n) for n in range(first + 1, end + 1)]
             ys = ys + [[]] * (8 - len(ys))
-            if by_pe(even - 2):
-                clear_newest(gpsimd, G_BASE + G_HALF * (len(pair) if k > 1 else 0), first * BLK + PIECE)
+            if even < UNITS:
+                if len(pair) < 2:
+                    clear(vector, "vector", V_RELU, first - 1)
+                if k > 1:
+                    vector += [("quant_x", k + 2), ("quant_h", 2 * k), ("bias", first, 0, PIECE), ("quant_h", 2 * k + 1), ("bias", first, PIECE, BLK)]
+                    vector += [("scale", j) for j in pair] + Y(first + 1, end)
+                    clear_newest(gpsimd, G_BASE + G_HALF * len(pair), first * BLK + PIECE)
+                else:
+                    vector += [("quant_h", 3), ("bias", 8, BLK - PIECE, BLK)] + [("scale", j) for j in pair] + Y(first, end)
+                    clear_newest(gpsimd, 3 * BLK, first * BLK)
+                    ys = [MY(first)] + ys[:-1]
                 gpsimd += [("weave_gpsimd", odd)]
                 wide = [[("widen", j)] for j in halves(k + 1)] + [[], []]
-                scalar += H(odd, 0, 1) + [("unload_h", even - 2, 0)] + wide[0] + [("unload_h", even - 2, 1)] + H(odd, 2, 3)
-                tensor += passes(even - 2, pair) + MH(odd, 2) + ys[0] + MH(odd, 3) + ys[1]
-                scalar += H(even, 0, 1, 2, 3) + wide[1]
+                scalar += H(odd, 0, 1)
+                if k == 1:
+                    clear(scalar, "scalar", BLK, 6)
+                scalar += [("unload_h", even - 2, 0)] + wide[0]
+                if not wide[0]:
+                    clear(scalar, "scalar", BLK - waiting[0][0] % BLK, first - 1)
+                scalar += [("unload_h", even - 2, 1)] + H(odd, 2, 3)
                 if pair:
-                    clear(scalar, "scalar", S_RELU, end - 2)
+                    scalar += H(even, 0, 1, 2, 3) + wide[1]
+                    clear(scalar, "scalar", S_RELU if len(pair) == 2 else S_LATE, end - 2)
+                else:
+                    for t in range(4):
+                        if t == 3:
+                            clear(vector, "vector", V_LATE, end - 1)
+                        scalar += H(even, t)
+                        clear(scalar, "scalar", BLK - waiting[0][0] % BLK, first + 1 + t if t < 3 else end - 1)
+                    clear(scalar, "scalar", BLK, end - 1)
+                tensor += passes(even - 2, pair) + MH(odd, 2) + ys[0] + MH(odd, 3) + ys[1]
                 for t in range(4):
                     tensor += MH(even, t) + ys[2 + t]
-                tensor += ys[6] + MH(odd + 2, 0) + ys[7] + MH(odd + 2, 1)
-            elif odd < UNITS:
-                gpsimd += [("weave_gpsimd", odd - 1), ("weave_gpsimd", odd)]
-                scalar += H(odd, 0, 1, 2, 3)
-                tensor += MH(odd, 2, 3)
-                for n in range(8):
-                    tensor += ys[n]
+                tensor += ys[6] + (MH(odd + 2, 0) + ys[7] + MH(odd + 2, 1) if pair else ys[7])
             else:
-                for n in range(8):
+                vector += [("quant_h", 2 * k), ("quant_h", 2 * k + 1)]
+                clear_newest(vector, BLK, first * BLK, "vector")
+                vector += Y(first, end)
+                gpsimd += [("weave_gpsimd", odd - 1)]
+                for t in range(4):
+                    if t == 3:
+                        clear(gpsimd, "gpsimd", HID, first + 5)
+                    scalar += H(odd, t)
+                    clear(scalar, "scalar", BLK - waiting[0][0] % BLK, first + 1 + t + 2 * (t == 3))
+                tensor += MH(odd, 0, 1) + ys[0] + ys[1] + MH(odd, 2) + ys[2] + MH(odd, 3)
+                for n in range(3, 8):
                     tensor += ys[n]
+        gpsimd += [("weave_gpsimd", UNITS - 1)]
+        vector += [("quant_h", UNITS - 2), ("weave_vector", UNITS - 1)] + Y(TILES - 9, TILES - 6) + [("quant_h", UNITS - 1)] + Y(TILES - 6, TILES - 1)
+        tensor += MY(*range(TILES - 8, TILES))
         vector += [("bias", TILES - 1, 0, 2 * P), ("bias", TILES - 1, 2 * P, BLK)]
         while waiting[0][0] < (TILES - 1) * BLK:
-            clear(scalar, "scalar", BLK - waiting[0][0] % BLK, TILES - 1, HID if waiting[0][0] < (TILES - 2) * BLK else BLK)
+            clear(scalar, "scalar", BLK - waiting[0][0] % BLK, TILES - 1, HID if waiting[0][0] < (TILES - 8) * BLK else BLK)
         clear(vector, "vector", 2 * P, TILES, 2 * P)
         clear(vector, "vector", 2 * P, TILES, 2 * P)
         assert not waiting
@@ -435,7 +447,7 @@ def tile_blockdiagmnistconvertible_pa_t_w4_kernel(tc, x_bytes, x_scale, W1_words
             elif kind == "weave" or kind == "weave_vector":
                 before += H(i, 3)
             elif kind == "weave_gpsimd":
-                before += H(i, 3) + ([("quant_h", by_gpsimd[by_gpsimd.index(i) - 1])] if not shared(i) else [])
+                before += H(i, 3) + ([("quant_h", by_gpsimd[by_gpsimd.index(i) - 1])] if i else [])
             elif kind == "unload_h":
                 before += [("weave", i, 2 * step[2] + 1), wide_tiles[wide_tiles.index(("quant_h", i)) - 2]]
             elif kind == "unload_wb":

@@ -27,11 +27,11 @@ FIRST_PE = 4
 LAST_PE = 12
 G_BASE = 1088
 G_HALF = 768
-S_RELU = 1536
+S_RELU = 1408
 PIECE = 64
 V_RELU = 1536
 V_LATE = 1024
-S_LATE = 1024
+S_LATE = 768
 BIG = 3.4028234663852886e38
 
 
@@ -79,14 +79,14 @@ def tile_blockdiagmnistconvertible_pa_t_w4_kernel(tc, x_bytes, x_scale, W1_words
         load_first(1)
         nc.sync.dma_start(out=sc[:], in_=x_scale.rearrange("o (p t) -> p (o t)", t=4))
         load_x(1)
+        load_x(2)
         for q in range(4):
             nc.sync.dma_start(
                 out=wsr[32 * q : 32 * q + 4, :].bitcast(I32), in_=W1_scales[0, 4 * q : 4 * q + 4, :].bitcast(I32)
             )
-        load_x(2)
         load_x(3)
-        nc.sync.dma_start(out=b1c[:], in_=b1.rearrange("(n p t) -> p n t", n=2, t=4))
         load_x(4)
+        nc.sync.dma_start(out=b1c[:], in_=b1.rearrange("(n p t) -> p n t", n=2, t=4))
         load_wb(0)
         load_wb(1)
         nc.sync.dma_start(out=bbr[:], in_=bb.partition_broadcast(P))
@@ -298,13 +298,13 @@ def tile_blockdiagmnistconvertible_pa_t_w4_kernel(tc, x_bytes, x_scale, W1_words
                 take(queue, engine, c0, c1, grain)
                 cols = cols - (c1 - c0)
 
-        def clear_newest(queue, cols, c1, engine="gpsimd"):
+        def clear_newest(queue, cols, c1):
             start, end = waiting.pop()
             c0 = max(start, c1 - cols)
             if c0 > start:
                 waiting.append((start, c0))
             waiting.append((c1, end))
-            take(queue, engine, c0, c1, BLK)
+            take(queue, "gpsimd", c0, c1, BLK)
 
         def Y(n0, n1):
             return [("bias", n, 0, BLK) for n in range(n0, n1)]
@@ -337,9 +337,10 @@ def tile_blockdiagmnistconvertible_pa_t_w4_kernel(tc, x_bytes, x_scale, W1_words
         vector += [("permute_scales", 1), ("quant_x", 1), ("scale", 4), ("scale", 5), ("weave_vector", 0), ("quant_x", 2), ("quant_h", 0), ("quant_wb", 0)]
         vector += [("scale", 6)] + Y(0, 3) + [("quant_h", 1), ("quant_wb", 1)] + Y(3, 4) + [("scale", 7)] + Y(4, 6)
         vector += [("quant_h", 2), ("quant_x", 3)] + Y(6, 7) + [("scale", 8)] + Y(7, 8) + [("bias", 8, 0, BLK - PIECE)]
-        scalar += [("widen", j) for j in range(8)] + H(0, 0, 1, 2, 3) + H(1, 0, 1) + [("unload_wb", 0, 0)] + H(1, 2) + [("unload_wb", 0, 1)] + H(1, 3)
-        scalar += [("widen", 8)] + H(2, 0, 1) + [("unload_wb", 1, 0)] + H(2, 2) + [("unload_wb", 1, 1)] + H(2, 3)
-        scalar += H(3, 0, 1, 2, 3) + [("widen", 9)] + H(4, 0, 1, 2, 3) + [("widen", 10)]
+        scalar += [("widen", j) for j in range(9)] + H(0, 0, 1, 2, 3) + H(1, 0, 1) + [("unload_wb", 0, 0)] + H(1, 2) + [("unload_wb", 0, 1)] + H(1, 3)
+        scalar += H(2, 0, 1) + [("unload_wb", 1, 0)] + H(2, 2)
+        clear(scalar, "scalar", BLK, 1)
+        scalar += [("unload_wb", 1, 1)] + H(2, 3) + H(3, 0, 1, 2, 3) + [("widen", 9)] + H(4, 0, 1, 2, 3) + [("widen", 10)]
         gpsimd += [("weave_gpsimd", u) for u in range(4)]
         tensor += [("warm", 0), ("warm", 1)] + TX(0) + TX(1) + [("warm", 2)] + TX(2) + TX(3) + [("warm", 3)] + MH(0, 0, 1, 2, 3) + TX(4) + TX(5)
         tensor += MH(1, 0, 1) + [("turn_wb", 0, 0)] + MH(1, 2) + [("turn_wb", 0, 1)] + MH(1, 3) + TX(6) + MH(2, 0, 1) + [("turn_wb", 1, 0)]
@@ -354,7 +355,7 @@ def tile_blockdiagmnistconvertible_pa_t_w4_kernel(tc, x_bytes, x_scale, W1_words
             ys = ys + [[]] * (8 - len(ys))
             if even < UNITS:
                 if len(pair) < 2:
-                    clear(vector, "vector", V_RELU, first - 1)
+                    clear(vector, "vector", V_RELU, first - 2 - 2 * len(pair))
                 if k > 1:
                     vector += [("quant_x", k + 2), ("quant_h", 2 * k), ("bias", first, 0, PIECE), ("quant_h", 2 * k + 1), ("bias", first, PIECE, BLK)]
                     vector += [("scale", j) for j in pair] + Y(first + 1, end)
@@ -369,7 +370,7 @@ def tile_blockdiagmnistconvertible_pa_t_w4_kernel(tc, x_bytes, x_scale, W1_words
                 if k == 1:
                     clear(scalar, "scalar", BLK, 6)
                 scalar += [("unload_h", even - 2, 0)] + wide[0]
-                if not wide[0]:
+                if not wide[0] or k == 1:
                     clear(scalar, "scalar", BLK - waiting[0][0] % BLK, first - 1)
                 scalar += [("unload_h", even - 2, 1)] + H(odd, 2, 3)
                 if pair:
@@ -378,24 +379,22 @@ def tile_blockdiagmnistconvertible_pa_t_w4_kernel(tc, x_bytes, x_scale, W1_words
                 else:
                     for t in range(4):
                         if t == 3:
-                            clear(vector, "vector", V_LATE, end - 1)
+                            clear(vector, "vector", V_LATE, end - 2)
                         scalar += H(even, t)
-                        clear(scalar, "scalar", BLK - waiting[0][0] % BLK, first + 1 + t if t < 3 else end - 1)
-                    clear(scalar, "scalar", BLK, end - 1)
+                        clear(scalar, "scalar", BLK - waiting[0][0] % BLK, first + 1 + t if t < 3 else end - 2)
+                    clear(scalar, "scalar", BLK, end - 2)
                 tensor += passes(even - 2, pair) + MH(odd, 2) + ys[0] + MH(odd, 3) + ys[1]
                 for t in range(4):
                     tensor += MH(even, t) + ys[2 + t]
                 tensor += ys[6] + (MH(odd + 2, 0) + ys[7] + MH(odd + 2, 1) if pair else ys[7])
             else:
-                vector += [("quant_h", 2 * k), ("quant_h", 2 * k + 1)]
-                clear_newest(vector, BLK, first * BLK, "vector")
-                vector += Y(first, end)
+                vector += [("quant_h", 2 * k), ("bias", first, 0, PIECE), ("quant_h", 2 * k + 1), ("bias", first, PIECE, BLK)] + Y(first + 1, end)
+                clear_newest(gpsimd, G_BASE, first * BLK + PIECE)
                 gpsimd += [("weave_gpsimd", odd - 1)]
                 for t in range(4):
-                    if t == 3:
-                        clear(gpsimd, "gpsimd", HID, first + 5)
                     scalar += H(odd, t)
-                    clear(scalar, "scalar", BLK - waiting[0][0] % BLK, first + 1 + t + 2 * (t == 3))
+                    clear(scalar, "scalar", BLK - waiting[0][0] % BLK, first + 1 + t)
+                clear(vector, "vector", BLK, end - 1)
                 tensor += MH(odd, 0, 1) + ys[0] + ys[1] + MH(odd, 2) + ys[2] + MH(odd, 3)
                 for n in range(3, 8):
                     tensor += ys[n]
@@ -404,7 +403,7 @@ def tile_blockdiagmnistconvertible_pa_t_w4_kernel(tc, x_bytes, x_scale, W1_words
         tensor += MY(*range(TILES - 8, TILES))
         vector += [("bias", TILES - 1, 0, 2 * P), ("bias", TILES - 1, 2 * P, BLK)]
         while waiting[0][0] < (TILES - 1) * BLK:
-            clear(scalar, "scalar", BLK - waiting[0][0] % BLK, TILES - 1, HID if waiting[0][0] < (TILES - 8) * BLK else BLK)
+            clear(scalar, "scalar", BLK - waiting[0][0] % BLK, TILES - 1, HID if waiting[0][0] < (TILES - 10) * BLK else BLK)
         clear(vector, "vector", 2 * P, TILES, 2 * P)
         clear(vector, "vector", 2 * P, TILES, 2 * P)
         assert not waiting

@@ -26,12 +26,12 @@ BANKS = 8
 FIRST_PE = 4
 LAST_PE = 12
 G_BASE = 1088
-G_HALF = 768
-S_RELU = 1408
+G_HALF = 832
+S_RELU = 1536
 PIECE = 64
-V_RELU = 1536
+V_RELU = 2048
 V_LATE = 1024
-S_LATE = 768
+S_LATE = 1024
 BIG = 3.4028234663852886e38
 
 
@@ -79,14 +79,14 @@ def tile_blockdiagmnistconvertible_pa_t_w4_kernel(tc, x_bytes, x_scale, W1_words
         load_first(1)
         nc.sync.dma_start(out=sc[:], in_=x_scale.rearrange("o (p t) -> p (o t)", t=4))
         load_x(1)
-        load_x(2)
         for q in range(4):
             nc.sync.dma_start(
                 out=wsr[32 * q : 32 * q + 4, :].bitcast(I32), in_=W1_scales[0, 4 * q : 4 * q + 4, :].bitcast(I32)
             )
+        load_x(2)
         load_x(3)
-        load_x(4)
         nc.sync.dma_start(out=b1c[:], in_=b1.rearrange("(n p t) -> p n t", n=2, t=4))
+        load_x(4)
         load_wb(0)
         load_wb(1)
         nc.sync.dma_start(out=bbr[:], in_=bb.partition_broadcast(P))
@@ -324,6 +324,12 @@ def tile_blockdiagmnistconvertible_pa_t_w4_kernel(tc, x_bytes, x_scale, W1_words
         def halves(k):
             return [j for j in (2 * k + 7, 2 * k + 8) if j < UNITS]
 
+        def share(k):
+            return G_BASE + G_HALF * len(halves(k))
+
+        def below_share(k):
+            return ((8 * k - 1) * BLK + PIECE - share(k)) // BLK
+
         def passes(u, pair):
             run = []
             for a in range(4):
@@ -335,11 +341,14 @@ def tile_blockdiagmnistconvertible_pa_t_w4_kernel(tc, x_bytes, x_scale, W1_words
 
         vector += [("permute_words",), ("scale", 0), ("scale", 1), ("permute_scales", 0), ("quant_x", 0), ("scale", 2), ("scale", 3)]
         vector += [("permute_scales", 1), ("quant_x", 1), ("scale", 4), ("scale", 5), ("weave_vector", 0), ("quant_x", 2), ("quant_h", 0), ("quant_wb", 0)]
-        vector += [("scale", 6)] + Y(0, 3) + [("quant_h", 1), ("quant_wb", 1)] + Y(3, 4) + [("scale", 7)] + Y(4, 6)
+        vector += [("scale", 6)] + Y(0, 3)
+        scalar += [("widen", j) for j in range(8)] + H(0, 0, 1, 2, 3) + H(1, 0, 1) + [("unload_wb", 0, 0)] + H(1, 2) + [("unload_wb", 0, 1)] + H(1, 3)
+        scalar += [("widen", 8)] + H(2, 0, 1) + [("unload_wb", 1, 0)] + H(2, 2)
+        clear(vector, "vector", BLK, 2)
+        vector += [("quant_h", 1), ("quant_wb", 1)] + Y(3, 4) + [("scale", 7)] + Y(4, 6)
+        clear(vector, "vector", BLK, 5)
         vector += [("quant_h", 2), ("quant_x", 3)] + Y(6, 7) + [("scale", 8)] + Y(7, 8) + [("bias", 8, 0, BLK - PIECE)]
-        scalar += [("widen", j) for j in range(9)] + H(0, 0, 1, 2, 3) + H(1, 0, 1) + [("unload_wb", 0, 0)] + H(1, 2) + [("unload_wb", 0, 1)] + H(1, 3)
-        scalar += H(2, 0, 1) + [("unload_wb", 1, 0)] + H(2, 2)
-        clear(scalar, "scalar", BLK, 1)
+        clear(vector, "vector", BLK, 6)
         scalar += [("unload_wb", 1, 1)] + H(2, 3) + H(3, 0, 1, 2, 3) + [("widen", 9)] + H(4, 0, 1, 2, 3) + [("widen", 10)]
         gpsimd += [("weave_gpsimd", u) for u in range(4)]
         tensor += [("warm", 0), ("warm", 1)] + TX(0) + TX(1) + [("warm", 2)] + TX(2) + TX(3) + [("warm", 3)] + MH(0, 0, 1, 2, 3) + TX(4) + TX(5)
@@ -354,12 +363,12 @@ def tile_blockdiagmnistconvertible_pa_t_w4_kernel(tc, x_bytes, x_scale, W1_words
             ys = [MY(n) for n in range(first + 1, end + 1)]
             ys = ys + [[]] * (8 - len(ys))
             if even < UNITS:
-                if len(pair) < 2:
-                    clear(vector, "vector", V_RELU, first - 2 - 2 * len(pair))
+                if not pair:
+                    clear(vector, "vector", V_RELU, below_share(k))
                 if k > 1:
                     vector += [("quant_x", k + 2), ("quant_h", 2 * k), ("bias", first, 0, PIECE), ("quant_h", 2 * k + 1), ("bias", first, PIECE, BLK)]
                     vector += [("scale", j) for j in pair] + Y(first + 1, end)
-                    clear_newest(gpsimd, G_BASE + G_HALF * len(pair), first * BLK + PIECE)
+                    clear_newest(gpsimd, share(k), first * BLK + PIECE)
                 else:
                     vector += [("quant_h", 3), ("bias", 8, BLK - PIECE, BLK)] + [("scale", j) for j in pair] + Y(first, end)
                     clear_newest(gpsimd, 3 * BLK, first * BLK)
@@ -370,12 +379,12 @@ def tile_blockdiagmnistconvertible_pa_t_w4_kernel(tc, x_bytes, x_scale, W1_words
                 if k == 1:
                     clear(scalar, "scalar", BLK, 6)
                 scalar += [("unload_h", even - 2, 0)] + wide[0]
-                if not wide[0] or k == 1:
+                if not wide[0]:
                     clear(scalar, "scalar", BLK - waiting[0][0] % BLK, first - 1)
                 scalar += [("unload_h", even - 2, 1)] + H(odd, 2, 3)
                 if pair:
                     scalar += H(even, 0, 1, 2, 3) + wide[1]
-                    clear(scalar, "scalar", S_RELU if len(pair) == 2 else S_LATE, end - 2)
+                    clear(scalar, "scalar", S_RELU if len(pair) == 2 else S_LATE, below_share(k + 1))
                 else:
                     for t in range(4):
                         if t == 3:

@@ -29,6 +29,7 @@ G_BASE = 1088
 G_HALF = 832
 S_RELU = 1536
 PIECE = 64
+SHORT = 2
 V_RELU = 2048
 V_LATE = 1024
 S_LATE = 1024
@@ -304,7 +305,10 @@ def tile_blockdiagmnistconvertible_pa_t_w4_kernel(tc, x_bytes, x_scale, W1_words
             if c0 > start:
                 waiting.append((start, c0))
             waiting.append((c1, end))
-            take(queue, "gpsimd", c0, c1, BLK)
+            middle = (c0 + c1) // 2 // HID * HID if c1 - c0 > 3 * BLK else c0
+            take(queue, "gpsimd", middle, c1, BLK)
+            if middle > c0:
+                take(queue, "gpsimd", c0, middle, BLK)
 
         def Y(n0, n1):
             return [("bias", n, 0, BLK) for n in range(n0, n1)]
@@ -322,7 +326,9 @@ def tile_blockdiagmnistconvertible_pa_t_w4_kernel(tc, x_bytes, x_scale, W1_words
             return [("turn_x", j, 0, 1, 2, 3)]
 
         def halves(k):
-            return [j for j in (2 * k + 7, 2 * k + 8) if j < UNITS]
+            if k < SHORT:
+                return [2 * k + 7, 2 * k + 8]
+            return [j for j in (2 * k + 6, 2 * k + 7) if 2 * SHORT + 6 < j < UNITS]
 
         def share(k):
             return G_BASE + G_HALF * len(halves(k))
@@ -384,7 +390,7 @@ def tile_blockdiagmnistconvertible_pa_t_w4_kernel(tc, x_bytes, x_scale, W1_words
                 scalar += [("unload_h", even - 2, 1)] + H(odd, 2, 3)
                 if pair:
                     scalar += H(even, 0, 1, 2, 3) + wide[1]
-                    clear(scalar, "scalar", S_RELU if len(pair) == 2 else S_LATE, below_share(k + 1))
+                    clear(scalar, "scalar", S_RELU if k > SHORT else S_LATE, below_share(k + 1))
                 else:
                     for t in range(4):
                         if t == 3:

@@ -22,18 +22,16 @@ T = 512
 GROUPS = B // T
 UNITS = 2 * GROUPS
 TILES = 4 * UNITS
-BANKS = 8
-FIRST_PE = 4
-LAST_PE = 12
+PIECE = 64
 G_BASE = 1088
 G_HALF = 832
 S_RELU = 1536
-PIECE = 64
-SHORT = 2
+S_EARLY = 1024
 V_RELU = 2048
 V_LATE = 1024
-S_LATE = 1024
+SHORT = 2
 BIG = 3.4028234663852886e38
+BUFS = {"bank": 8, "xs": 5, "xg": 2, "xc": 3, "hp": 3, "hg": 1, "hw": 2, "hv": 1, "late": 1, "hc": 5}
 
 
 def tile_blockdiagmnistconvertible_pa_t_w4_kernel(tc, x_bytes, x_scale, W1_words, W1_scales, b1, Wb, bb, out):
@@ -41,7 +39,7 @@ def tile_blockdiagmnistconvertible_pa_t_w4_kernel(tc, x_bytes, x_scale, W1_words
 
     with ExitStack() as ctx:
         keep = ctx.enter_context(tc.tile_pool(name="keep", bufs=1))
-        work = ctx.enter_context(tc.tile_pool(name="work", bufs=3))
+        work = ctx.enter_context(tc.tile_pool(name="work", bufs=1))
         psum = ctx.enter_context(tc.psum_pool(name="psum", bufs=1))
         ctx.enter_context(tc.manual_schedule())
 
@@ -59,15 +57,10 @@ def tile_blockdiagmnistconvertible_pa_t_w4_kernel(tc, x_bytes, x_scale, W1_words
         wbc = [keep.tile([P, BLK], U32, name=f"wbc{n}", align_bytes=64) for n in range(2)]
         wbs = [keep.tile([P, BLK], U8, name=f"wbs{n}", align_bytes=64) for n in range(2)]
         wbr = [keep.tile([P, 4, BLK], BF16, name=f"wbr{n}") for n in range(2)]
-        hg = keep.tile([P, T, 4], BF16, name="hg", align_bytes=64)
-        rest = keep.tile([P, 2 * P, 4], BF16, name="rest", align_bytes=64)
 
-        def load_x(g):
-            nc.sync.dma_start(out=xb[g][:], in_=x_bytes[T * g : T * (g + 1), :].rearrange("(p a) k -> p a k", a=4))
-
-        def load_first(h):
-            rows = x_bytes[:T, :].rearrange("(p a) k -> p a k", a=4)
-            nc.sync.dma_start(out=xb[0][:, 2 * h : 2 * h + 2, :], in_=rows[:, 2 * h : 2 * h + 2, :])
+        def load_x(g, a0=0, a1=4):
+            rows = x_bytes[T * g : T * (g + 1), :].rearrange("(p a) k -> p a k", a=4)
+            nc.sync.dma_start(out=xb[g][:, a0:a1, :], in_=rows[:, a0:a1, :])
 
         def load_wb(n):
             nc.sync.dma_start(out=wbr[n][:], in_=Wb[n].rearrange("(p a) k -> p a k", a=4))
@@ -75,9 +68,9 @@ def tile_blockdiagmnistconvertible_pa_t_w4_kernel(tc, x_bytes, x_scale, W1_words
         nc.vector.memset(wsr[:].bitcast(I32), 0)
         make_identity(nc, ident[:])
         make_identity(nc, identb[:])
-        load_first(0)
+        load_x(0, 0, 2)
         nc.sync.dma_start(out=w1r[:], in_=W1_words[0])
-        load_first(1)
+        load_x(0, 2, 4)
         nc.sync.dma_start(out=sc[:], in_=x_scale.rearrange("o (p t) -> p (o t)", t=4))
         load_x(1)
         for q in range(4):
@@ -94,67 +87,74 @@ def tile_blockdiagmnistconvertible_pa_t_w4_kernel(tc, x_bytes, x_scale, W1_words
         for g in range(5, GROUPS):
             load_x(g)
 
-        xs, xg, xc, xsc = {}, {}, {}, {}
-        hp, hw, hc, hs, wbg = {}, {}, {}, {}, {}
-        filled = {}
-        tenants = []
+        held = {}
+        order = {kind: [] for kind in BUFS}
 
         def by_pe(u):
-            return FIRST_PE <= u <= LAST_PE and u % 2 == 0
+            return u % 2 == 0 and 4 <= u <= UNITS - 4
 
-        def quantize(src, codes, scales):
-            nc.vector.quantize_mx(out=codes.bitcast(FP8X4), scales=scales, in_=src)
-
-        def flat(view):
-            return view.rearrange("p r t -> p (r t)")
-
-        def code_tiles(kind, bufs):
-            codes = work.tile([P, T], U32, name="codes", tag=f"codes_{kind}", align_bytes=64, bufs=bufs)
-            scales = work.tile([P, T], U8, name="scales", tag=f"scales_{kind}", align_bytes=64, bufs=bufs)
-            return codes[:], scales[:]
-
-        def bank(key, shape, dtype):
-            filled[key] = psum.tile(shape, dtype, name="bank", tag=f"bank{tenants.index(key) % BANKS}")
-            return filled[key]
-
-        def turn(dst, rows, i):
-            a, u = divmod(i, 2)
-            nc.tensor.transpose(dst[:, u, a * P : (a + 1) * P], rows[:, a, :].bitcast(F32)[:, u : 2 * P : 2], ident[:])
-
-        def turn_x(j, *parts):
-            if parts[0] == 0:
-                bank(("scale", j), [P, 2, 2 * P], F32)
-            for i in parts:
-                turn(filled["scale", j], xs[j], i)
-
-        def turn_wb(n, h):
-            dst = bank(("unload_wb", n, h), [P, 2, 2 * P], F32)
-            for i in range(4):
-                turn(dst, wbr[n][:, 2 * h : 2 * h + 2, :], i)
-
-        def fill_h(u, t):
-            nc.tensor.matmul_mx(
-                out=bank(("relu_h", u, t), [P, T], F32)[:],
-                lhsT=w1p[:, u % 2, t].rearrange("p m b -> p (m b)").bitcast(FP4X4),
-                lhsT_scale=wsp[:, u % 2, t, :],
-                rhs=xc[u // 2].bitcast(FP8X4),
-                rhs_scale=xsc[u // 2],
-                start=True,
-                stop=True,
-            )
+        def shared(u):
+            return u in (0, UNITS - 1)
 
         def place(n):
             if n < 16 or n >= TILES - 8:
                 return divmod(n, 4)
             return n // 8 * 2 + n % 2, n % 8 // 2
 
+        def kind(key):
+            return "late" if key in (("xg", 0), ("xs", half(7))) else key[0]
+
+        def fresh(key, shape, dtype):
+            if key not in held:
+                if key[0] == "bank":
+                    held[key] = psum.tile(shape, dtype, name="bank", tag=f"bank{order['bank'].index(key) % BUFS['bank']}")
+                else:
+                    held[key] = work.tile(shape, dtype, name=kind(key), tag=kind(key), align_bytes=64, bufs=BUFS[kind(key)])
+            return held[key]
+
+        def flat(view):
+            return view.rearrange("p r t -> p (r t)")
+
+        def codes(key, cols):
+            return held[key][:, :T][:, cols].bitcast(FP8X4)
+
+        def scales(key, cols):
+            return held[key][:, T:].bitcast(U8)[:, cols]
+
+        def quantize(src, key, cols=slice(0, T)):
+            fresh(key, [P, T + T // 4], U32)
+            nc.vector.quantize_mx(out=codes(key, cols), scales=scales(key, cols), in_=flat(src))
+
+        def turn(dst, rows, i):
+            a, u = divmod(i, 2)
+            nc.tensor.transpose(dst[:, u, a * P : (a + 1) * P], rows[:, a, :].bitcast(F32)[:, u : 2 * P : 2], ident[:])
+
+        def turn_x(rows, *parts):
+            for i in parts:
+                turn(fresh(("bank", "x", rows), [P, 2, rows[2] * P], F32), held["xs", rows], i)
+
+        def turn_wb(n, h):
+            for i in range(4):
+                turn(fresh(("bank", "wb", n, h), [P, 2, 2 * P], F32), wbr[n][:, 2 * h : 2 * h + 2, :], i)
+
+        def fill_h(u, t):
+            nc.tensor.matmul_mx(
+                out=fresh(("bank", "h", u, t), [P, T], F32)[:],
+                lhsT=w1p[:, u % 2, t].rearrange("p m b -> p (m b)").bitcast(FP4X4),
+                lhsT_scale=wsp[:, u % 2, t, :],
+                rhs=codes(("xc", u // 2), slice(0, T)),
+                rhs_scale=scales(("xc", u // 2), slice(0, T)),
+                start=True,
+                stop=True,
+            )
+
         def fill_y(n):
             u, a = place(n)
             cols = slice(a * P, (a + 1) * P)
             nc.tensor.matmul_mx(
-                out=bank(("bias", n), [P, BLK], F32)[:],
-                lhsT=hc[u][:, cols].bitcast(FP8X4),
-                lhsT_scale=hs[u][:, cols],
+                out=fresh(("bank", "y", n), [P, BLK], F32)[:],
+                lhsT=codes(("hc", u), cols),
+                lhsT_scale=scales(("hc", u), cols),
                 rhs=wbc[u % 2][:].bitcast(FP8X4),
                 rhs_scale=wbs[u % 2][:],
                 start=True,
@@ -162,80 +162,74 @@ def tile_blockdiagmnistconvertible_pa_t_w4_kernel(tc, x_bytes, x_scale, W1_words
             )
 
         def weave(u, a):
-            if a % 2 == 0:
-                bank(("unload_h", u, a // 2), [P, 2, P, 4], BF16)
             nc.tensor.matmul(
-                out=flat(filled["unload_h", u, a // 2][:, a % 2]),
+                out=flat(fresh(("bank", "w", u, a // 2), [P, 2, P, 4], BF16)[:, a % 2]),
                 lhsT=identb[:],
-                rhs=hp[u][:, :, a * P : (a + 1) * P].rearrange("p t r -> p r t"),
+                rhs=held["hp", u][:, :, a * P : (a + 1) * P].rearrange("p t r -> p r t"),
                 start=True,
                 stop=True,
             )
 
         def warm(i):
-            idle = bank(("warm", i), [P, 2, P], F32)
+            idle = fresh(("bank", "warm", i), [P, 2, P], F32)
             nc.tensor.matmul(out=idle[:], lhsT=ident[:], rhs=ident[:].unsqueeze(1).to_broadcast([P, 2, P]), start=True, stop=True)
 
-        def widen(j):
-            xs[j] = work.tile([P, 2, IN], BF16, name="xs", tag="xs", bufs=5)
-            src = xb[j // 2][:, 2 * (j % 2) : 2 * (j % 2) + 2, :].rearrange("p a k -> p (a k)").bitcast(FP8)
-            nc.scalar.copy(out=xs[j][:].rearrange("p a k -> p (a k)"), in_=src)
+        def widen(rows):
+            g, a, count = rows
+            copy = nc.gpsimd.tensor_copy if rows == half(7) else nc.scalar.copy
+            copy(out=flat(fresh(("xs", rows), [P, count, IN], BF16)[:]), in_=flat(xb[g][:, a : a + count, :]).bitcast(FP8))
 
-        def scale(j):
-            g, h = divmod(j, 2)
-            if h == 0:
-                xg[g] = work.tile([P, T, 4], BF16, name="xg", tag="xg", align_bytes=64, bufs=2)
+        def scale(rows):
+            g, a, count = rows
             nc.vector.tensor_tensor(
-                out=xg[g][:, 2 * P * h : 2 * P * (h + 1), :].rearrange("p r (u e) -> p r u e", u=2),
-                in0=filled["scale", j][:].bitcast(BF16).rearrange("p u (r e) -> p r u e", e=2),
-                in1=sc[:].rearrange("p (u e) -> p u e", u=2).unsqueeze(1).to_broadcast([P, 2 * P, 2, 2]),
+                out=fresh(("xg", g), [P, T, 4], BF16)[:, a * P : (a + count) * P, :].rearrange("p r (u e) -> p r u e", u=2),
+                in0=held["bank", "x", rows][:].bitcast(BF16).rearrange("p u (r e) -> p r u e", e=2),
+                in1=sc[:].rearrange("p (u e) -> p u e", u=2).unsqueeze(1).to_broadcast([P, count * P, 2, 2]),
                 op=ALU.mult,
             )
 
         def quant_x(g):
-            xc[g], xsc[g] = code_tiles("x", 3)
-            quantize(flat(xg[g][:]), xc[g], xsc[g])
+            for cols in (slice(0, 2 * P), slice(2 * P, T)) if g < 2 else (slice(0, T),):
+                quantize(held["xg", g][:, cols], ("xc", g), cols)
 
         def relu_h(u, t):
-            if t == 0:
-                hp[u] = work.tile([P, 4, T], BF16, name="hp", tag="hp")
-            nc.scalar.activation(out=hp[u][:, t, :], in_=filled["relu_h", u, t][:], func=ACT.Relu, bias=b1c[:, u % 2, t : t + 1])
+            planes = fresh(("hp", u), [P, 4, T], BF16)
+            nc.scalar.activation(out=planes[:, t, :], in_=held["bank", "h", u, t][:], func=ACT.Relu, bias=b1c[:, u % 2, t : t + 1])
 
         def unload_h(u, half):
-            if half == 0:
-                hw[u] = work.tile([P, T, 4], BF16, name="hw", tag="hw", align_bytes=64, bufs=2)
             nc.scalar.copy(
-                out=flat(hw[u][:, 2 * P * half : 2 * P * (half + 1), :]).bitcast(F32),
-                in_=filled["unload_h", u, half][:].rearrange("p a r t -> p (a r t)").bitcast(F32),
+                out=flat(fresh(("hw", u), [P, T, 4], BF16)[:, 2 * P * half : 2 * P * (half + 1), :]).bitcast(F32),
+                in_=held["bank", "w", u, half][:].rearrange("p a r t -> p (a r t)").bitcast(F32),
             )
-
-        def shared(u):
-            return u in (0, UNITS - 1)
 
         def weave_gpsimd(u):
             cut = 2 * P if shared(u) else T
             nc.gpsimd.tensor_scalar(
-                out=hg[:, :cut], in0=hp[u][:, :, :cut].rearrange("p t r -> p r t"), scalar1=1.0, scalar2=0.0, op0=ALU.mult, op1=ALU.add
+                out=fresh(("hg", u), [P, cut, 4], BF16)[:],
+                in0=held["hp", u][:, :, :cut].rearrange("p t r -> p r t"),
+                scalar1=1.0,
+                scalar2=0.0,
+                op0=ALU.mult,
+                op1=ALU.add,
             )
 
         def weave_vector(u):
             nc.vector.tensor_copy(
-                out=rest[:].rearrange("p (c i) t -> p c t i", i=4),
-                in_=hp[u][:, :, 2 * P :].rearrange("p t (c i) -> p c t i", i=4),
+                out=fresh(("hv", u), [P, 2 * P, 4], BF16)[:].rearrange("p (c i) t -> p c t i", i=4),
+                in_=held["hp", u][:, :, 2 * P :].rearrange("p t (c i) -> p c t i", i=4),
             )
 
         def quant_h(u):
-            hc[u], hs[u] = code_tiles("h", 5)
             if shared(u):
-                quantize(flat(rest[:]), hc[u][:, 2 * P :], hs[u][:, 2 * P :])
-                quantize(flat(hg[:, : 2 * P]), hc[u][:, : 2 * P], hs[u][:, : 2 * P])
+                quantize(held["hv", u][:], ("hc", u), slice(2 * P, T))
+                quantize(held["hg", u][:], ("hc", u), slice(0, 2 * P))
             else:
-                quantize(flat(hw[u][:] if by_pe(u) else hg[:]), hc[u], hs[u])
+                quantize(held["hw" if by_pe(u) else "hg", u][:], ("hc", u))
 
         def bias(n, lo, hi):
             first = place(n)[0] % 2 * BLK
             nc.vector.tensor_tensor(
-                out=ring[:, n * BLK + lo : n * BLK + hi], in0=filled["bias", n][:, lo:hi], in1=bbr[:, first + lo : first + hi], op=ALU.add
+                out=ring[:, n * BLK + lo : n * BLK + hi], in0=held["bank", "y", n][:, lo:hi], in1=bbr[:, first + lo : first + hi], op=ALU.add
             )
 
         def relu(engine, c0, c1):
@@ -250,36 +244,34 @@ def tile_blockdiagmnistconvertible_pa_t_w4_kernel(tc, x_bytes, x_scale, W1_words
         def store(c0, c1):
             g = c0 // (8 * BLK)
             rows = out[T * g : T * (g + 1), :]
-            if g < 2 or g == GROUPS - 1:
-                u, a = place(c0 // BLK)
-                lo, width = c0 % BLK, min(BLK, c1 - c0)
-                count = (c1 - c0) // width
-                nc.sync.dma_start(out=rows.rearrange("(p a) (n c) -> p n a c", a=4, n=2)[:, u % 2, a : a + count, lo : lo + width], in_=ring[:, c0:c1].rearrange("p (a c) -> p a c", c=width))
-            else:
+            if 2 <= g < GROUPS - 1:
                 first = g * 8 * BLK
                 nc.sync.dma_start(out=rows.rearrange("(p a) c -> p (a c)", a=4)[:, c0 - first : c1 - first], in_=ring[:, c0:c1])
+            else:
+                u, a = place(c0 // BLK)
+                lo, width = c0 % BLK, min(BLK, c1 - c0)
+                planes = rows.rearrange("(p a) (n c) -> p n a c", a=4, n=2)[:, u % 2]
+                nc.sync.dma_start(out=planes[:, a : a + (c1 - c0) // width, lo : lo + width], in_=ring[:, c0:c1].rearrange("p (a c) -> p a c", c=width))
 
         def permute_words():
             nc.vector.tensor_copy(out=w1p[:], in_=w1r[:].rearrange("p (n m t b) -> p n t m b", n=2, t=4, b=2))
 
-        def permute_scales(n):
-            nc.vector.tensor_copy(out=wsp[:, n], in_=wsr[:].rearrange("p (n m t) -> p n t m", n=2, t=4)[:, n])
+        def permute_scales():
+            nc.gpsimd.tensor_copy(out=wsp[:], in_=wsr[:].rearrange("p (n m t) -> p n t m", n=2, t=4))
 
         def unload_wb(n, h):
-            if h == 0:
-                wbg[n] = work.tile([P, BLK, 4], BF16, name="wbg", tag="hw", align_bytes=64, bufs=2)
-            words = flat(wbg[n][:]).bitcast(F32).rearrange("p (r a u) -> p r a u", a=4, u=2)
-            nc.scalar.copy(out=words[:, :, 2 * h : 2 * h + 2, :], in_=filled["unload_wb", n, h][:].rearrange("p u (a r) -> p r a u", a=2))
+            words = flat(fresh(("hw", "wb", n), [P, BLK, 4], BF16)[:]).bitcast(F32).rearrange("p (r a u) -> p r a u", a=4, u=2)
+            nc.scalar.copy(out=words[:, :, 2 * h : 2 * h + 2, :], in_=held["bank", "wb", n, h][:].rearrange("p u (a r) -> p r a u", a=2))
 
         def quant_wb(n):
-            quantize(flat(wbg[n][:]), wbc[n][:], wbs[n][:])
+            nc.vector.quantize_mx(out=wbc[n][:].bitcast(FP8X4), scales=wbs[n][:], in_=flat(held["hw", "wb", n][:]))
 
         vector, scalar, gpsimd, tensor, sync = [], [], [], [], []
         waiting = [(0, TILES * BLK)]
         cleared = [0] * (TILES * 2)
 
         def take(queue, engine, c0, c1, grain):
-            queue.append(("relu", engine, c0, c1))
+            queue.append((relu, engine, c0, c1))
             for i in range(c0 // 256, -(-c1 // 256)):
                 cleared[i] = cleared[i] + min(c1, 256 * (i + 1)) - max(c0, 256 * i)
             step = grain // 256
@@ -287,43 +279,87 @@ def tile_blockdiagmnistconvertible_pa_t_w4_kernel(tc, x_bytes, x_scale, W1_words
             while whole:
                 run = 8 if whole[0] < 32 or whole[0] >= 112 else 16
                 part = [i for i in whole if i // run == whole[0] // run]
-                sync.append(("store", part[0] * 256, (part[-1] + step) * 256))
+                sync.append((store, part[0] * 256, (part[-1] + step) * 256))
                 whole = whole[len(part) :]
 
         def clear(queue, engine, cols, below, grain=BLK):
-            while cols > 0 and waiting and waiting[0][0] < below * BLK:
+            while cols > 0 and waiting and waiting[0][0] < below:
                 c0, end = waiting.pop(0)
-                c1 = min(c0 + cols, below * BLK, end)
+                c1 = min(c0 + cols, below, end)
                 if c1 < end:
                     waiting.insert(0, (c1, end))
                 take(queue, engine, c0, c1, grain)
                 cols = cols - (c1 - c0)
 
-        def clear_newest(queue, cols, c1):
+        def clear_newest(cols, c1):
             start, end = waiting.pop()
             c0 = max(start, c1 - cols)
             if c0 > start:
                 waiting.append((start, c0))
             waiting.append((c1, end))
-            middle = (c0 + c1) // 2 // HID * HID if c1 - c0 > 3 * BLK else c0
-            take(queue, "gpsimd", middle, c1, BLK)
+            middle = (c0 + c1) // 2 // BLK * BLK if c1 - c0 > 3 * BLK else c0
+            take(gpsimd, "gpsimd", middle, c1, BLK)
             if middle > c0:
-                take(queue, "gpsimd", c0, middle, BLK)
+                take(gpsimd, "gpsimd", c0, middle, BLK)
+
+        def clear_tiles(count, below):
+            while count > 0 and waiting[0][0] < below:
+                c0, end = waiting[0]
+                if count > 1 and c0 % HID == 0 and c0 + HID <= min(end, below, (TILES - 2) * BLK):
+                    clear(scalar, "scalar", BLK, below, HID)
+                    clear(scalar, "scalar", BLK, below, HID)
+                    count = count - 2
+                else:
+                    clear(scalar, "scalar", BLK - c0 % BLK, below)
+                    count = count - 1
 
         def Y(n0, n1):
-            return [("bias", n, 0, BLK) for n in range(n0, n1)]
+            return [(bias, n, 0, BLK) for n in range(n0, n1)]
 
         def H(u, *planes):
-            return [("relu_h", u, t) for t in planes]
+            return [(relu_h, u, t) for t in planes or range(4)]
 
         def MH(u, *planes):
-            return [("fill_h", u, t) for t in planes]
+            return [(fill_h, u, t) for t in planes or range(4)]
 
         def MY(*tiles):
-            return [("fill_y", n) for n in tiles]
+            return [(fill_y, n) for n in tiles]
 
-        def TX(j):
-            return [("turn_x", j, 0, 1, 2, 3)]
+        def half(j):
+            return (j // 2, j % 2 * 2, 2)
+
+        def TX(*halves):
+            return [(turn_x, half(j), 0, 1, 2, 3) for j in halves]
+
+        def W(*halves):
+            return [(widen, half(j)) for j in halves]
+
+        def X(*halves):
+            return [(scale, half(j)) for j in halves]
+
+        def passes(u, pair):
+            run = []
+            for a in range(4):
+                run += [(weave, u, a)]
+                if a // 2 < len(pair):
+                    run += [(turn_x, half(pair[a // 2]), 2 * (a % 2), 2 * (a % 2) + 1)]
+            return run
+
+        vector += [(permute_words,)] + X(0, 1) + [(quant_x, 0)] + X(2, 3) + [(quant_x, 1)] + X(4, 5)
+        vector += [(weave_vector, 0), (quant_x, 2), (quant_h, 0), (quant_wb, 0)] + X(6) + Y(0, 3)
+        scalar += W(*range(7)) + H(0) + H(1, 0, 1) + [(unload_wb, 0, 0), (unload_wb, 0, 1)] + H(1, 2, 3)
+        scalar += W(8) + H(2, 0, 1) + [(unload_wb, 1, 0)] + H(2, 2)
+        clear(vector, "vector", BLK, 2 * BLK)
+        vector += [(quant_h, 1), (quant_wb, 1)] + Y(3, 4) + X(7) + Y(4, 6)
+        clear(vector, "vector", BLK, 5 * BLK)
+        vector += [(quant_h, 2), (quant_x, 3)] + Y(6, 7) + X(8) + Y(7, 8) + [(bias, 8, 0, BLK - PIECE)]
+        clear(vector, "vector", BLK, 6 * BLK)
+        scalar += [(unload_wb, 1, 1)] + H(2, 3) + H(3) + W(9) + H(4) + W(10)
+        gpsimd += [(permute_scales,)] + W(7) + [(weave_gpsimd, u) for u in range(4)]
+        tensor += [(warm, 0), (warm, 1)] + TX(0, 1) + [(warm, 2)] + TX(2, 3) + [(warm, 3)] + MH(0) + TX(4, 5)
+        tensor += MH(1, 0, 1) + [(turn_wb, 0, 0), (turn_wb, 0, 1)] + MH(1, 2, 3) + TX(6) + MH(2, 0, 1) + [(turn_wb, 1, 0)]
+        tensor += MY(0) + MH(2, 2) + MY(1, 2) + [(turn_wb, 1, 1)] + MH(2, 3) + MH(3, 0) + MY(3) + MH(3, 1) + TX(7) + MH(3, 2) + MY(4) + MH(3, 3) + MY(5)
+        tensor += MH(4, 0) + MY(6) + MH(4, 1) + TX(8) + MH(4, 2, 3) + MY(7) + MH(5, 0) + MY(8) + MH(5, 1)
 
         def halves(k):
             if k < SHORT:
@@ -334,167 +370,136 @@ def tile_blockdiagmnistconvertible_pa_t_w4_kernel(tc, x_bytes, x_scale, W1_words
             return G_BASE + G_HALF * len(halves(k))
 
         def below_share(k):
-            return ((8 * k - 1) * BLK + PIECE - share(k)) // BLK
+            return ((8 * k - 1) * BLK + PIECE - share(k)) // BLK * BLK
 
-        def passes(u, pair):
-            run = []
-            for a in range(4):
-                j = pair[a // 2] if a // 2 < len(pair) else -1
-                run += [("weave", u, a)]
-                if j >= 0:
-                    run += [("turn_x", j, 2 * (a % 2), 2 * (a % 2) + 1)]
-            return run
-
-        vector += [("permute_words",), ("scale", 0), ("scale", 1), ("permute_scales", 0), ("quant_x", 0), ("scale", 2), ("scale", 3)]
-        vector += [("permute_scales", 1), ("quant_x", 1), ("scale", 4), ("scale", 5), ("weave_vector", 0), ("quant_x", 2), ("quant_h", 0), ("quant_wb", 0)]
-        vector += [("scale", 6)] + Y(0, 3)
-        scalar += [("widen", j) for j in range(8)] + H(0, 0, 1, 2, 3) + H(1, 0, 1) + [("unload_wb", 0, 0)] + H(1, 2) + [("unload_wb", 0, 1)] + H(1, 3)
-        scalar += [("widen", 8)] + H(2, 0, 1) + [("unload_wb", 1, 0)] + H(2, 2)
-        clear(vector, "vector", BLK, 2)
-        vector += [("quant_h", 1), ("quant_wb", 1)] + Y(3, 4) + [("scale", 7)] + Y(4, 6)
-        clear(vector, "vector", BLK, 5)
-        vector += [("quant_h", 2), ("quant_x", 3)] + Y(6, 7) + [("scale", 8)] + Y(7, 8) + [("bias", 8, 0, BLK - PIECE)]
-        clear(vector, "vector", BLK, 6)
-        scalar += [("unload_wb", 1, 1)] + H(2, 3) + H(3, 0, 1, 2, 3) + [("widen", 9)] + H(4, 0, 1, 2, 3) + [("widen", 10)]
-        gpsimd += [("weave_gpsimd", u) for u in range(4)]
-        tensor += [("warm", 0), ("warm", 1)] + TX(0) + TX(1) + [("warm", 2)] + TX(2) + TX(3) + [("warm", 3)] + MH(0, 0, 1, 2, 3) + TX(4) + TX(5)
-        tensor += MH(1, 0, 1) + [("turn_wb", 0, 0)] + MH(1, 2) + [("turn_wb", 0, 1)] + MH(1, 3) + TX(6) + MH(2, 0, 1) + [("turn_wb", 1, 0)]
-        tensor += MY(0) + MH(2, 2) + MY(1, 2) + [("turn_wb", 1, 1)] + MH(2, 3) + MH(3, 0) + MY(3) + MH(3, 1) + TX(7) + MH(3, 2) + MY(4) + MH(3, 3) + MY(5)
-        tensor += MH(4, 0) + MY(6) + MH(4, 1) + TX(8) + MH(4, 2, 3) + MY(7) + MH(5, 0) + MY(8) + MH(5, 1)
+        def tile_rest(below, grain=BLK):
+            clear(scalar, "scalar", BLK - waiting[0][0] % BLK, below * BLK, grain)
 
         for k in range(1, GROUPS - 1):
-            first, end = (9 if k == 1 else 8 * k - 1), 8 * k + 7
+            first, end = (8 if k == 1 else 8 * k - 1), 8 * k + 7
             pair = halves(k)
             odd, even = 2 * k + 3, 2 * k + 4
-            ys = [MY(n) for n in range(first + 1, end + 1)]
-            ys = ys + [[]] * (8 - len(ys))
+            ys = [MY(n) for n in range(first + 1, end + 1)] + [[]]
             if even < UNITS:
                 if not pair:
                     clear(vector, "vector", V_RELU, below_share(k))
-                if k > 1:
-                    vector += [("quant_x", k + 2), ("quant_h", 2 * k), ("bias", first, 0, PIECE), ("quant_h", 2 * k + 1), ("bias", first, PIECE, BLK)]
-                    vector += [("scale", j) for j in pair] + Y(first + 1, end)
-                    clear_newest(gpsimd, share(k), first * BLK + PIECE)
+                if k == 1:
+                    vector += [(quant_h, 3), (bias, 8, BLK - PIECE, BLK)] + X(*pair) + Y(first + 1, end)
+                    clear_newest(3 * BLK, 9 * BLK)
                 else:
-                    vector += [("quant_h", 3), ("bias", 8, BLK - PIECE, BLK)] + [("scale", j) for j in pair] + Y(first, end)
-                    clear_newest(gpsimd, 3 * BLK, first * BLK)
-                    ys = [MY(first)] + ys[:-1]
-                gpsimd += [("weave_gpsimd", odd)]
-                wide = [[("widen", j)] for j in halves(k + 1)] + [[], []]
+                    vector += [(quant_x, k + 2), (quant_h, 2 * k), (bias, first, 0, PIECE), (quant_h, 2 * k + 1), (bias, first, PIECE, BLK)] + X(*pair) + Y(first + 1, end)
+                    clear_newest(share(k), first * BLK + PIECE)
+                gpsimd += [(weave_gpsimd, odd)]
+                wide = [W(j) for j in halves(k + 1)] + [[], []]
                 scalar += H(odd, 0, 1)
                 if k == 1:
-                    clear(scalar, "scalar", BLK, 6)
-                scalar += [("unload_h", even - 2, 0)] + wide[0]
+                    clear(scalar, "scalar", BLK, 6 * BLK)
+                scalar += [(unload_h, even - 2, 0)] + wide[0]
                 if not wide[0]:
-                    clear(scalar, "scalar", BLK - waiting[0][0] % BLK, first - 1)
-                scalar += [("unload_h", even - 2, 1)] + H(odd, 2, 3)
+                    tile_rest(first - 1)
+                scalar += [(unload_h, even - 2, 1)] + H(odd, 2, 3)
                 if pair:
-                    scalar += H(even, 0, 1, 2, 3) + wide[1]
-                    clear(scalar, "scalar", S_RELU if k > SHORT else S_LATE, below_share(k + 1))
+                    scalar += H(even) + wide[1]
+                    clear(scalar, "scalar", S_RELU if k > SHORT else S_EARLY, below_share(k + 1))
                 else:
                     for t in range(4):
                         if t == 3:
-                            clear(vector, "vector", V_LATE, end - 2)
+                            clear(vector, "vector", V_LATE, (end - 2) * BLK)
                         scalar += H(even, t)
-                        clear(scalar, "scalar", BLK - waiting[0][0] % BLK, first + 1 + t if t < 3 else end - 2)
-                    clear(scalar, "scalar", BLK, end - 2)
+                        tile_rest(first + 1 + t if t < 3 else end - 2)
+                    tile_rest(end - 2)
                 tensor += passes(even - 2, pair) + MH(odd, 2) + ys[0] + MH(odd, 3) + ys[1]
                 for t in range(4):
                     tensor += MH(even, t) + ys[2 + t]
                 tensor += ys[6] + (MH(odd + 2, 0) + ys[7] + MH(odd + 2, 1) if pair else ys[7])
             else:
-                vector += [("quant_h", 2 * k), ("bias", first, 0, PIECE), ("quant_h", 2 * k + 1), ("bias", first, PIECE, BLK)] + Y(first + 1, end)
-                clear_newest(gpsimd, G_BASE, first * BLK + PIECE)
-                gpsimd += [("weave_gpsimd", odd - 1)]
+                vector += [(quant_h, 2 * k), (bias, first, 0, PIECE), (quant_h, 2 * k + 1), (bias, first, PIECE, BLK)] + Y(first + 1, end)
+                clear_newest(G_BASE, first * BLK + PIECE)
+                gpsimd += [(weave_gpsimd, odd - 1)]
                 for t in range(4):
                     scalar += H(odd, t)
-                    clear(scalar, "scalar", BLK - waiting[0][0] % BLK, first + 1 + t)
-                clear(vector, "vector", BLK, end - 1)
-                tensor += MH(odd, 0, 1) + ys[0] + ys[1] + MH(odd, 2) + ys[2] + MH(odd, 3)
-                for n in range(3, 8):
-                    tensor += ys[n]
-        gpsimd += [("weave_gpsimd", UNITS - 1)]
-        vector += [("quant_h", UNITS - 2), ("weave_vector", UNITS - 1)] + Y(TILES - 9, TILES - 6) + [("quant_h", UNITS - 1)] + Y(TILES - 6, TILES - 1)
+                    tile_rest(first + 1 + t)
+                clear(vector, "vector", BLK, (end - 1) * BLK)
+                tensor += MH(odd) + MY(*range(first + 1, end + 1))
+        gpsimd += [(weave_gpsimd, UNITS - 1)]
+        vector += [(quant_h, UNITS - 2), (weave_vector, UNITS - 1)] + Y(TILES - 9, TILES - 6) + [(quant_h, UNITS - 1)] + Y(TILES - 6, TILES - 1)
         tensor += MY(*range(TILES - 8, TILES))
-        vector += [("bias", TILES - 1, 0, 2 * P), ("bias", TILES - 1, 2 * P, BLK)]
+        vector += [(bias, TILES - 1, 0, 2 * P), (bias, TILES - 1, 2 * P, BLK)]
         while waiting[0][0] < (TILES - 1) * BLK:
-            clear(scalar, "scalar", BLK - waiting[0][0] % BLK, TILES - 1, HID if waiting[0][0] < (TILES - 10) * BLK else BLK)
-        clear(vector, "vector", 2 * P, TILES, 2 * P)
-        clear(vector, "vector", 2 * P, TILES, 2 * P)
+            tile_rest(TILES - 1, HID if waiting[0][0] < (TILES - 10) * BLK else BLK)
+        clear(vector, "vector", 2 * P, TILES * BLK, 2 * P)
+        clear(vector, "vector", 2 * P, TILES * BLK, 2 * P)
         assert not waiting
 
-        def tenant(step):
-            if step[0] == "turn_x":
-                return ("scale", step[1]) if step[2] == 0 else None
-            if step[0] == "weave":
-                return ("unload_h", step[1], step[2] // 2) if step[2] % 2 == 0 else None
-            return ({"turn_wb": "unload_wb", "fill_h": "relu_h", "fill_y": "bias", "warm": "warm"}[step[0]],) + step[1:]
 
-        tenants.extend([tenant(step) for step in tensor if tenant(step)])
-        by_gpsimd = [u for u in range(UNITS) if not by_pe(u)]
-        wide_tiles = [("quant_wb", 0), ("quant_wb", 1)] + [("quant_h", u) for u in range(UNITS) if by_pe(u)]
-        plane_tiles = [step[1] for step in scalar if step[0] == "relu_h" and step[2] == 0]
-        relus = [step for step in vector + scalar + gpsimd if step[0] == "relu"]
+        def uses(step):
+            call, i = step[0], step[1:]
+            if call == widen:
+                return [("xs",) + i], []
+            if call == turn_x:
+                return [("bank", "x", i[0])], [("xs", i[0])]
+            if call == scale:
+                return [("xg", i[0][0])], [("bank", "x") + i]
+            if call == quant_x:
+                return [("xc",) + i], [("xg",) + i]
+            if call == fill_h:
+                return [("bank", "h") + i], [("xc", i[0] // 2), ("w1",)]
+            if call == relu_h:
+                return [("hp", i[0])], [("bank", "h") + i]
+            if call == weave:
+                return [("bank", "w", i[0], i[1] // 2)], [("hp", i[0])]
+            if call == unload_h:
+                return [("hw", i[0])], [("bank", "w") + i]
+            if call == weave_gpsimd:
+                return [("hg",) + i], [("hp",) + i]
+            if call == weave_vector:
+                return [("hv",) + i], [("hp",) + i]
+            if call == quant_h:
+                return [("hc",) + i], [("hw" if by_pe(i[0]) else "hg",) + i] + ([("hv",) + i] if shared(i[0]) else [])
+            if call == turn_wb:
+                return [("bank", "wb") + i], []
+            if call == unload_wb:
+                return [("hw", "wb", i[0])], [("bank", "wb") + i]
+            if call == quant_wb:
+                return [("wb",) + i], [("hw", "wb") + i]
+            if call == fill_y:
+                return [("bank", "y") + i], [("hc", place(i[0])[0]), ("wb", place(i[0])[0] % 2)]
+            if call == bias:
+                return [], [("bank", "y", i[0])]
+            if call == permute_scales or call == permute_words:
+                return [("w1",)], []
+            if call == warm:
+                return [("bank", "warm") + i], []
+            return [], []
 
-        def woven(u):
-            if by_pe(u):
-                return [("weave", u, 3)]
-            return [("weave_gpsimd", u)] + ([("weave_vector", u)] if shared(u) else [])
+        queues = [tensor, vector, scalar, gpsimd, sync]
+        steps = [step for queue in queues for step in queue]
+        makers, takers = {}, {}
+        for step in steps:
+            for key in uses(step)[0]:
+                if key not in makers and kind(key) in order:
+                    order[kind(key)].append(key)
+                makers.setdefault(key, []).append(step)
+            for key in uses(step)[1]:
+                takers.setdefault(key, []).append(step)
 
         def needs(step):
-            kind, i = step[0], step[1] if len(step) > 1 else None
-            before = []
-            if step in tensor and tenant(step) and tenants.index(tenant(step)) >= BANKS:
-                before += [tenants[tenants.index(tenant(step)) - BANKS]]
-            if kind == "widen" and i >= 5:
-                before += [("turned", i - 5)]
-            elif kind == "turn_x":
-                before += [("widen", i)]
-            elif kind == "scale":
-                before += [("turned", i)] + ([("quant_x", i // 2 - 2)] if i >= 4 else [])
-            elif kind == "quant_x" and i >= 3:
-                before += MH(2 * i - 5, 3)
-            elif kind == "fill_h":
-                before += [("quant_x", i // 2), ("permute_scales", i % 2)]
-            elif kind == "relu_h":
-                before += MH(i, step[2]) + (woven(plane_tiles[plane_tiles.index(i) - 3]) if i >= 3 else [])
-            elif kind == "weave" or kind == "weave_vector":
-                before += H(i, 3)
-            elif kind == "weave_gpsimd":
-                before += H(i, 3) + ([("quant_h", by_gpsimd[by_gpsimd.index(i) - 1])] if i else [])
-            elif kind == "unload_h":
-                before += [("weave", i, 2 * step[2] + 1), wide_tiles[wide_tiles.index(("quant_h", i)) - 2]]
-            elif kind == "unload_wb":
-                before += [("turn_wb", i, step[2])]
-            elif kind == "quant_wb":
-                before += [("unload_wb", i, 1)]
-            elif kind == "quant_h":
-                before += ([("unload_h", i, 1)] if by_pe(i) else woven(i)) + [("fill_y", n) for n in range(TILES) if place(n)[0] == i - 5]
-            elif kind == "fill_y":
-                before += [("quant_h", place(i)[0]), ("quant_wb", place(i)[0] % 2)]
-            elif kind == "bias":
-                before += MY(i)
-            elif kind == "relu":
-                before += [b for b in vector if b[0] == "bias" and b[1] * BLK + b[2] < step[3] and b[1] * BLK + b[3] > step[2]]
-            elif kind == "store":
-                before += [r for r in relus if r[2] < step[2] and r[3] > step[1]]
+            makes, takes = uses(step)
+            before = [maker for key in takes for maker in makers[key]]
+            for key in makes:
+                if kind(key) in order and order[kind(key)].index(key) >= BUFS[kind(key)]:
+                    before += takers.get(order[kind(key)][order[kind(key)].index(key) - BUFS[kind(key)]], [])
+            if step[0] == relu:
+                before += [b for b in vector if b[0] == bias and b[1] * BLK + b[2] < step[3] and b[1] * BLK + b[3] > step[2]]
+            if step[0] == store:
+                before += [r for r in steps if r[0] == relu and r[2] < step[2] and r[3] > step[1]]
             return before
 
-        calls = {
-            "permute_words": permute_words, "permute_scales": permute_scales, "scale": scale, "quant_x": quant_x, "quant_h": quant_h,
-            "quant_wb": quant_wb, "weave_vector": weave_vector, "weave_gpsimd": weave_gpsimd, "weave": weave, "bias": bias, "relu": relu,
-            "widen": widen, "relu_h": relu_h, "unload_h": unload_h, "unload_wb": unload_wb, "warm": warm, "turn_x": turn_x,
-            "turn_wb": turn_wb, "fill_h": fill_h, "fill_y": fill_y, "store": store,
-        }
         written = set()
-        queues = [list(queue) for queue in (tensor, vector, scalar, gpsimd, sync)]
+        queues = [list(queue) for queue in queues]
         while any(queues):
             ready = [queue for queue in queues if queue and all(b in written for b in needs(queue[0]))]
             assert ready
             step = ready[0].pop(0)
-            calls[step[0]](*step[1:])
+            step[0](*step[1:])
             written.add(step)
-            if step[0] == "turn_x" and step[-1] == 3:
-                written.add(("turned", step[1]))
-            if step[0] == "bias" and step[3] == BLK:
-                written.add(step[:2])

@@ -30,6 +30,7 @@ S_EARLY = 1024
 V_RELU = 2048
 V_LATE = 1024
 SHORT = 2
+PAIRS_FROM = 36
 BIG = 3.4028234663852886e38
 BUFS = {"bank": 8, "xs": 5, "xg": 2, "xc": 3, "hp": 3, "hg": 1, "hw": 2, "hv": 1, "late": 1, "hc": 5}
 
@@ -272,6 +273,8 @@ def tile_blockdiagmnistconvertible_pa_t_w4_kernel(tc, x_bytes, x_scale, W1_words
 
         def take(queue, engine, c0, c1, grain):
             queue.append((relu, engine, c0, c1))
+            if PAIRS_FROM * BLK <= c0 < (TILES - 2) * BLK:
+                grain = HID
             for i in range(c0 // 256, -(-c1 // 256)):
                 cleared[i] = cleared[i] + min(c1, 256 * (i + 1)) - max(c0, 256 * i)
             step = grain // 256

@@ -24,13 +24,14 @@ UNITS = 2 * GROUPS
 TILES = 4 * UNITS
 PIECE = 64
 G_BASE = 1088
-G_HALF = 832
+G_HALF = 768
 S_RELU = 1536
 S_EARLY = 1024
 V_RELU = 2048
 V_LATE = 1024
 SHORT = 2
 PAIRS_FROM = 36
+PAIRS_TO = 64
 BIG = 3.4028234663852886e38
 BUFS = {"bank": 8, "xs": 5, "xg": 2, "xc": 3, "hp": 3, "hg": 1, "hw": 2, "hv": 1, "late": 1, "hc": 5}
 
@@ -273,7 +274,7 @@ def tile_blockdiagmnistconvertible_pa_t_w4_kernel(tc, x_bytes, x_scale, W1_words
 
         def take(queue, engine, c0, c1, grain):
             queue.append((relu, engine, c0, c1))
-            if PAIRS_FROM * BLK <= c0 < (TILES - 2) * BLK:
+            if PAIRS_FROM * BLK <= c0 < PAIRS_TO * BLK:
                 grain = HID
             for i in range(c0 // 256, -(-c1 // 256)):
                 cleared[i] = cleared[i] + min(c1, 256 * (i + 1)) - max(c0, 256 * i)
@@ -427,11 +428,10 @@ def tile_blockdiagmnistconvertible_pa_t_w4_kernel(tc, x_bytes, x_scale, W1_words
         gpsimd += [(weave_gpsimd, UNITS - 1)]
         vector += [(quant_h, UNITS - 2), (weave_vector, UNITS - 1)] + Y(TILES - 9, TILES - 6) + [(quant_h, UNITS - 1)] + Y(TILES - 6, TILES - 1)
         tensor += MY(*range(TILES - 8, TILES))
-        vector += [(bias, TILES - 1, 0, 2 * P), (bias, TILES - 1, 2 * P, BLK)]
+        vector += Y(TILES - 1, TILES)
         while waiting[0][0] < (TILES - 1) * BLK:
             tile_rest(TILES - 1, HID if waiting[0][0] < (TILES - 10) * BLK else BLK)
-        clear(vector, "vector", 2 * P, TILES * BLK, 2 * P)
-        clear(vector, "vector", 2 * P, TILES * BLK, 2 * P)
+        clear(vector, "vector", BLK, TILES * BLK)
         assert not waiting
 
 

@@ -30,10 +30,10 @@ S_EARLY = 1024
 V_RELU = 2048
 V_LATE = 1024
 SHORT = 2
+SPLIT_FROM = 24
 PAIRS_FROM = 36
-PAIRS_TO = 64
 BIG = 3.4028234663852886e38
-BUFS = {"bank": 8, "xs": 5, "xg": 2, "xc": 3, "hp": 3, "hg": 1, "hw": 2, "hv": 1, "late": 1, "hc": 5}
+BUFS = {"bank": 8, "xs": 5, "xg": 2, "xc": 3, "hp": 3, "hg": 1, "hw": 2, "hv": 1, "late": 1, "third": 1, "hc": 5}
 
 
 def tile_blockdiagmnistconvertible_pa_t_w4_kernel(tc, x_bytes, x_scale, W1_words, W1_scales, b1, Wb, bb, out):
@@ -104,7 +104,9 @@ def tile_blockdiagmnistconvertible_pa_t_w4_kernel(tc, x_bytes, x_scale, W1_words
             return n // 8 * 2 + n % 2, n % 8 // 2
 
         def kind(key):
-            return "late" if key in (("xg", 0), ("xs", half(7))) else key[0]
+            if key in (("xg", 0), ("xs", half(7))):
+                return "late"
+            return "third" if key in (("xg", 3), ("hg", 3)) else key[0]
 
         def fresh(key, shape, dtype):
             if key not in held:
@@ -274,7 +276,7 @@ def tile_blockdiagmnistconvertible_pa_t_w4_kernel(tc, x_bytes, x_scale, W1_words
 
         def take(queue, engine, c0, c1, grain):
             queue.append((relu, engine, c0, c1))
-            if PAIRS_FROM * BLK <= c0 < PAIRS_TO * BLK:
+            if PAIRS_FROM * BLK <= c0 and not (TILES - 6) * BLK <= c0 < (TILES - 2) * BLK:
                 grain = HID
             for i in range(c0 // 256, -(-c1 // 256)):
                 cleared[i] = cleared[i] + min(c1, 256 * (i + 1)) - max(c0, 256 * i)
@@ -301,7 +303,7 @@ def tile_blockdiagmnistconvertible_pa_t_w4_kernel(tc, x_bytes, x_scale, W1_words
             if c0 > start:
                 waiting.append((start, c0))
             waiting.append((c1, end))
-            middle = (c0 + c1) // 2 // BLK * BLK if c1 - c0 > 3 * BLK else c0
+            middle = (c0 + c1) // 2 // BLK * BLK if c1 - c0 > 3 * BLK and c1 > SPLIT_FROM * BLK else c0
             take(gpsimd, "gpsimd", middle, c1, BLK)
             if middle > c0:
                 take(gpsimd, "gpsimd", c0, middle, BLK)
@@ -355,15 +357,16 @@ def tile_blockdiagmnistconvertible_pa_t_w4_kernel(tc, x_bytes, x_scale, W1_words
         scalar += W(8) + H(2, 0, 1) + [(unload_wb, 1, 0)] + H(2, 2)
         clear(vector, "vector", BLK, 2 * BLK)
         vector += [(quant_h, 1), (quant_wb, 1)] + Y(3, 4) + X(7) + Y(4, 6)
-        clear(vector, "vector", BLK, 5 * BLK)
-        vector += [(quant_h, 2), (quant_x, 3)] + Y(6, 7) + X(8) + Y(7, 8) + [(bias, 8, 0, BLK - PIECE)]
+        vector += [(quant_x, 3), (quant_h, 2)] + Y(6, 7) + X(8) + Y(7, 8) + [(bias, 8, 0, BLK - PIECE)]
+        scalar += [(unload_wb, 1, 1)] + H(2, 3) + H(3, 0, 1)
+        clear(scalar, "scalar", BLK, 3 * BLK)
         clear(vector, "vector", BLK, 6 * BLK)
-        scalar += [(unload_wb, 1, 1)] + H(2, 3) + H(3) + W(9) + H(4) + W(10)
+        scalar += H(3, 2, 3) + W(9) + H(4) + W(10)
         gpsimd += [(permute_scales,)] + W(7) + [(weave_gpsimd, u) for u in range(4)]
         tensor += [(warm, 0), (warm, 1)] + TX(0, 1) + [(warm, 2)] + TX(2, 3) + [(warm, 3)] + MH(0) + TX(4, 5)
         tensor += MH(1, 0, 1) + [(turn_wb, 0, 0), (turn_wb, 0, 1)] + MH(1, 2, 3) + TX(6) + MH(2, 0, 1) + [(turn_wb, 1, 0)]
         tensor += MY(0) + MH(2, 2) + MY(1, 2) + [(turn_wb, 1, 1)] + MH(2, 3) + MH(3, 0) + MY(3) + MH(3, 1) + TX(7) + MH(3, 2) + MY(4) + MH(3, 3) + MY(5)
-        tensor += MH(4, 0) + MY(6) + MH(4, 1) + TX(8) + MH(4, 2, 3) + MY(7) + MH(5, 0) + MY(8) + MH(5, 1)
+        tensor += MH(4, 0, 1, 2) + MY(6) + TX(8) + MH(4, 3) + MY(7) + MH(5, 0) + MY(8) + MH(5, 1)
 
         def halves(k):
             if k < SHORT:
@@ -420,8 +423,9 @@ def tile_blockdiagmnistconvertible_pa_t_w4_kernel(tc, x_bytes, x_scale, W1_words
                 vector += [(quant_h, 2 * k), (bias, first, 0, PIECE), (quant_h, 2 * k + 1), (bias, first, PIECE, BLK)] + Y(first + 1, end)
                 clear_newest(G_BASE, first * BLK + PIECE)
                 gpsimd += [(weave_gpsimd, odd - 1)]
+                scalar += H(odd, 0)
                 for t in range(4):
-                    scalar += H(odd, t)
+                    scalar += H(odd, t + 1) if t < 3 else []
                     tile_rest(first + 1 + t)
                 clear(vector, "vector", BLK, (end - 1) * BLK)
                 tensor += MH(odd) + MY(*range(first + 1, end + 1))

from contextlib import ExitStack

import concourse.mybir as mybir
from concourse.masks import make_identity

B, IN, HID, BLK = 4096, 512, 1024, 512
FLOPS = 2 * B * IN * HID + 2 * B * HID * BLK

F32 = mybir.dt.float32
BF16 = mybir.dt.bfloat16
U32 = mybir.dt.uint32
I32 = mybir.dt.int32
U8 = mybir.dt.uint8
FP8 = mybir.dt.float8_e4m3fn
FP8X4 = mybir.dt.float8_e4m3fn_x4
FP4X4 = mybir.dt.float4_e2m1fn_x4
ALU = mybir.AluOpType
ACT = mybir.ActivationFunctionType

P = 128
T = 512
GROUPS = B // T
UNITS = 2 * GROUPS
TILES = 4 * UNITS
PIECE = 64
G_BASE = 1088
G_HALF = 768
S_RELU = 1536
S_EARLY = 1024
V_RELU = 2048
V_LATE = 1024
SHORT = 2
SPLIT_FROM = 24
PAIRS_FROM = 36
BIG = 3.4028234663852886e38
BUFS = {"bank": 8, "xs": 5, "xg": 2, "xc": 3, "hp": 3, "hg": 1, "hw": 2, "hv": 1, "late": 1, "third": 1, "hc": 5}


def tile_blockdiagmnistconvertible_pa_t_w4_kernel(tc, x_bytes, x_scale, W1_words, W1_scales, b1, Wb, bb, out):
    nc = tc.nc

    with ExitStack() as ctx:
        keep = ctx.enter_context(tc.tile_pool(name="keep", bufs=1))
        work = ctx.enter_context(tc.tile_pool(name="work", bufs=1))
        psum = ctx.enter_context(tc.psum_pool(name="psum", bufs=1))
        ctx.enter_context(tc.manual_schedule())

        ident = keep.tile([P, P], F32, name="ident")
        identb = keep.tile([P, P], BF16, name="identb")
        sc = keep.tile([P, 4], F32, name="sc")
        w1r = keep.tile([P, 2048], U8, name="w1r")
        w1p = keep.tile([P, 2, 4, P, 2], U8, name="w1p", align_bytes=64)
        wsr = keep.tile([P, HID], U8, name="wsr", align_bytes=64)
        wsp = keep.tile([P, 2, 4, P], U8, name="wsp", align_bytes=64)
        b1c = keep.tile([P, 2, 4], BF16, name="b1c")
        bbr = keep.tile([P, HID], BF16, name="bbr")
        ring = keep.tile([P, TILES * BLK], F32, name="ring")
        xb = [keep.tile([P, 4, IN], U8, name=f"xb{g}") for g in range(GROUPS)]
        wbc = [keep.tile([P, BLK], U32, name=f"wbc{n}", align_bytes=64) for n in range(2)]
        wbs = [keep.tile([P, BLK], U8, name=f"wbs{n}", align_bytes=64) for n in range(2)]
        wbr = [keep.tile([P, 4, BLK], BF16, name=f"wbr{n}") for n in range(2)]

        def load_x(g, a0=0, a1=4):
            rows = x_bytes[T * g : T * (g + 1), :].rearrange("(p a) k -> p a k", a=4)
            nc.sync.dma_start(out=xb[g][:, a0:a1, :], in_=rows[:, a0:a1, :])

        def load_wb(n):
            nc.sync.dma_start(out=wbr[n][:], in_=Wb[n].rearrange("(p a) k -> p a k", a=4))

        nc.vector.memset(wsr[:].bitcast(I32), 0)
        make_identity(nc, ident[:])
        make_identity(nc, identb[:])
        load_x(0, 0, 2)
        nc.sync.dma_start(out=w1r[:], in_=W1_words[0])
        load_x(0, 2, 4)
        nc.sync.dma_start(out=sc[:], in_=x_scale.rearrange("o (p t) -> p (o t)", t=4))
        load_x(1)
        for q in range(4):
            nc.sync.dma_start(
                out=wsr[32 * q : 32 * q + 4, :].bitcast(I32), in_=W1_scales[0, 4 * q : 4 * q + 4, :].bitcast(I32)
            )
        load_x(2)
        load_x(3)
        nc.sync.dma_start(out=b1c[:], in_=b1.rearrange("(n p t) -> p n t", n=2, t=4))
        load_x(4)
        load_wb(0)
        load_wb(1)
        nc.sync.dma_start(out=bbr[:], in_=bb.partition_broadcast(P))
        for g in range(5, GROUPS):
            load_x(g)

        held = {}
        order = {kind: [] for kind in BUFS}

        def by_pe(u):
            return u % 2 == 0 and 4 <= u <= UNITS - 4

        def shared(u):
            return u in (0, UNITS - 1)

        def place(n):
            if n < 16 or n >= TILES - 8:
                return divmod(n, 4)
            return n // 8 * 2 + n % 2, n % 8 // 2

        def kind(key):
            if key in (("xg", 0), ("xs", half(7))):
                return "late"
            return "third" if key in (("xg", 3), ("hg", 3)) else key[0]

        def fresh(key, shape, dtype):
            if key not in held:
                if key[0] == "bank":
                    held[key] = psum.tile(shape, dtype, name="bank", tag=f"bank{order['bank'].index(key) % BUFS['bank']}")
                else:
                    held[key] = work.tile(shape, dtype, name=kind(key), tag=kind(key), align_bytes=64, bufs=BUFS[kind(key)])
            return held[key]

        def flat(view):
            return view.rearrange("p r t -> p (r t)")

        def codes(key, cols):
            return held[key][:, :T][:, cols].bitcast(FP8X4)

        def scales(key, cols):
            return held[key][:, T:].bitcast(U8)[:, cols]

        def quantize(src, key, cols=slice(0, T)):
            fresh(key, [P, T + T // 4], U32)
            nc.vector.quantize_mx(out=codes(key, cols), scales=scales(key, cols), in_=flat(src))

        def turn(dst, rows, i):
            a, u = divmod(i, 2)
            nc.tensor.transpose(dst[:, u, a * P : (a + 1) * P], rows[:, a, :].bitcast(F32)[:, u : 2 * P : 2], ident[:])

        def turn_x(rows, *parts):
            for i in parts:
                turn(fresh(("bank", "x", rows), [P, 2, rows[2] * P], F32), held["xs", rows], i)

        def turn_wb(n, h):
            for i in range(4):
                turn(fresh(("bank", "wb", n, h), [P, 2, 2 * P], F32), wbr[n][:, 2 * h : 2 * h + 2, :], i)

        def fill_h(u, t):
            nc.tensor.matmul_mx(
                out=fresh(("bank", "h", u, t), [P, T], F32)[:],
                lhsT=w1p[:, u % 2, t].rearrange("p m b -> p (m b)").bitcast(FP4X4),
                lhsT_scale=wsp[:, u % 2, t, :],
                rhs=codes(("xc", u // 2), slice(0, T)),
                rhs_scale=scales(("xc", u // 2), slice(0, T)),
                start=True,
                stop=True,
            )

        def fill_y(n):
            u, a = place(n)
            cols = slice(a * P, (a + 1) * P)
            nc.tensor.matmul_mx(
                out=fresh(("bank", "y", n), [P, BLK], F32)[:],
                lhsT=codes(("hc", u), cols),
                lhsT_scale=scales(("hc", u), cols),
                rhs=wbc[u % 2][:].bitcast(FP8X4),
                rhs_scale=wbs[u % 2][:],
                start=True,
                stop=True,
            )

        def weave(u, a):
            nc.tensor.matmul(
                out=flat(fresh(("bank", "w", u, a // 2), [P, 2, P, 4], BF16)[:, a % 2]),
                lhsT=identb[:],
                rhs=held["hp", u][:, :, a * P : (a + 1) * P].rearrange("p t r -> p r t"),
                start=True,
                stop=True,
            )

        def warm(i):
            idle = fresh(("bank", "warm", i), [P, 2, P], F32)
            nc.tensor.matmul(out=idle[:], lhsT=ident[:], rhs=ident[:].unsqueeze(1).to_broadcast([P, 2, P]), start=True, stop=True)

        def widen(rows):
            g, a, count = rows
            copy = nc.gpsimd.tensor_copy if rows == half(7) else nc.scalar.copy
            copy(out=flat(fresh(("xs", rows), [P, count, IN], BF16)[:]), in_=flat(xb[g][:, a : a + count, :]).bitcast(FP8))

        def scale(rows):
            g, a, count = rows
            nc.vector.tensor_tensor(
                out=fresh(("xg", g), [P, T, 4], BF16)[:, a * P : (a + count) * P, :].rearrange("p r (u e) -> p r u e", u=2),
                in0=held["bank", "x", rows][:].bitcast(BF16).rearrange("p u (r e) -> p r u e", e=2),
                in1=sc[:].rearrange("p (u e) -> p u e", u=2).unsqueeze(1).to_broadcast([P, count * P, 2, 2]),
                op=ALU.mult,
            )

        def quant_x(g):
            for cols in (slice(0, 2 * P), slice(2 * P, T)) if g < 2 else (slice(0, T),):
                quantize(held["xg", g][:, cols], ("xc", g), cols)

        def relu_h(u, t):
            planes = fresh(("hp", u), [P, 4, T], BF16)
            nc.scalar.activation(out=planes[:, t, :], in_=held["bank", "h", u, t][:], func=ACT.Relu, bias=b1c[:, u % 2, t : t + 1])

        def unload_h(u, half):
            nc.scalar.copy(
                out=flat(fresh(("hw", u), [P, T, 4], BF16)[:, 2 * P * half : 2 * P * (half + 1), :]).bitcast(F32),
                in_=held["bank", "w", u, half][:].rearrange("p a r t -> p (a r t)").bitcast(F32),
            )

        def weave_gpsimd(u):
            cut = 2 * P if shared(u) else T
            nc.gpsimd.tensor_scalar(
                out=fresh(("hg", u), [P, cut, 4], BF16)[:],
                in0=held["hp", u][:, :, :cut].rearrange("p t r -> p r t"),
                scalar1=1.0,
                scalar2=0.0,
                op0=ALU.mult,
                op1=ALU.add,
            )

        def weave_vector(u):
            nc.vector.tensor_copy(
                out=fresh(("hv", u), [P, 2 * P, 4], BF16)[:].rearrange("p (c i) t -> p c t i", i=4),
                in_=held["hp", u][:, :, 2 * P :].rearrange("p t (c i) -> p c t i", i=4),
            )

        def quant_h(u):
            if shared(u):
                quantize(held["hv", u][:], ("hc", u), slice(2 * P, T))
                quantize(held["hg", u][:], ("hc", u), slice(0, 2 * P))
            else:
                quantize(held["hw" if by_pe(u) else "hg", u][:], ("hc", u))

        def bias(n, lo, hi):
            first = place(n)[0] % 2 * BLK
            nc.vector.tensor_tensor(
                out=ring[:, n * BLK + lo : n * BLK + hi], in0=held["bank", "y", n][:, lo:hi], in1=bbr[:, first + lo : first + hi], op=ALU.add
            )

        def relu(engine, c0, c1):
            part = ring[:, c0:c1]
            if engine == "vector":
                nc.vector.tensor_scalar(out=part, in0=part, scalar1=0.0, scalar2=None, op0=ALU.max)
            elif engine == "gpsimd":
                nc.gpsimd.tensor_scalar(out=part, in0=part, scalar1=BIG, scalar2=0.0, op0=ALU.min, op1=ALU.max)
            else:
                nc.scalar.activation(out=part, in_=part, func=ACT.Relu)

        def store(c0, c1):
            g = c0 // (8 * BLK)
            rows = out[T * g : T * (g + 1), :]
            if 2 <= g < GROUPS - 1:
                first = g * 8 * BLK
                nc.sync.dma_start(out=rows.rearrange("(p a) c -> p (a c)", a=4)[:, c0 - first : c1 - first], in_=ring[:, c0:c1])
            else:
                u, a = place(c0 // BLK)
                lo, width = c0 % BLK, min(BLK, c1 - c0)
                planes = rows.rearrange("(p a) (n c) -> p n a c", a=4, n=2)[:, u % 2]
                nc.sync.dma_start(out=planes[:, a : a + (c1 - c0) // width, lo : lo + width], in_=ring[:, c0:c1].rearrange("p (a c) -> p a c", c=width))

        def permute_words():
            nc.vector.tensor_copy(out=w1p[:], in_=w1r[:].rearrange("p (n m t b) -> p n t m b", n=2, t=4, b=2))

        def permute_scales():
            nc.gpsimd.tensor_copy(out=wsp[:], in_=wsr[:].rearrange("p (n m t) -> p n t m", n=2, t=4))

        def unload_wb(n, h):
            words = flat(fresh(("hw", "wb", n), [P, BLK, 4], BF16)[:]).bitcast(F32).rearrange("p (r a u) -> p r a u", a=4, u=2)
            nc.scalar.copy(out=words[:, :, 2 * h : 2 * h + 2, :], in_=held["bank", "wb", n, h][:].rearrange("p u (a r) -> p r a u", a=2))

        def quant_wb(n):
            nc.vector.quantize_mx(out=wbc[n][:].bitcast(FP8X4), scales=wbs[n][:], in_=flat(held["hw", "wb", n][:]))

        vector, scalar, gpsimd, tensor, sync = [], [], [], [], []
        waiting = [(0, TILES * BLK)]
        cleared = [0] * (TILES * 2)

        def take(queue, engine, c0, c1, grain):
            queue.append((relu, engine, c0, c1))
            if PAIRS_FROM * BLK <= c0 and not (TILES - 6) * BLK <= c0 < (TILES - 2) * BLK:
                grain = HID
            for i in range(c0 // 256, -(-c1 // 256)):
                cleared[i] = cleared[i] + min(c1, 256 * (i + 1)) - max(c0, 256 * i)
            step = grain // 256
            whole = [i for i in range(c0 // grain * step, -(-c1 // grain) * step, step) if sum(cleared[i : i + step]) == grain]
            while whole:
                run = 8 if whole[0] < 32 or whole[0] >= 112 else 16
                part = [i for i in whole if i // run == whole[0] // run]
                sync.append((store, part[0] * 256, (part[-1] + step) * 256))
                whole = whole[len(part) :]

        def clear(queue, engine, cols, below, grain=BLK):
            while cols > 0 and waiting and waiting[0][0] < below:
                c0, end = waiting.pop(0)
                c1 = min(c0 + cols, below, end)
                if c1 < end:
                    waiting.insert(0, (c1, end))
                take(queue, engine, c0, c1, grain)
                cols = cols - (c1 - c0)

        def clear_newest(cols, c1):
            start, end = waiting.pop()
            c0 = max(start, c1 - cols)
            if c0 > start:
                waiting.append((start, c0))
            waiting.append((c1, end))
            middle = (c0 + c1) // 2 // BLK * BLK if c1 - c0 > 3 * BLK and c1 > SPLIT_FROM * BLK else c0
            take(gpsimd, "gpsimd", middle, c1, BLK)
            if middle > c0:
                take(gpsimd, "gpsimd", c0, middle, BLK)

        def clear_tiles(count, below):
            while count > 0 and waiting[0][0] < below:
                c0, end = waiting[0]
                if count > 1 and c0 % HID == 0 and c0 + HID <= min(end, below, (TILES - 2) * BLK):
                    clear(scalar, "scalar", BLK, below, HID)
                    clear(scalar, "scalar", BLK, below, HID)
                    count = count - 2
                else:
                    clear(scalar, "scalar", BLK - c0 % BLK, below)
                    count = count - 1

        def Y(n0, n1):
            return [(bias, n, 0, BLK) for n in range(n0, n1)]

        def H(u, *planes):
            return [(relu_h, u, t) for t in planes or range(4)]

        def MH(u, *planes):
            return [(fill_h, u, t) for t in planes or range(4)]

        def MY(*tiles):
            return [(fill_y, n) for n in tiles]

        def half(j):
            return (j // 2, j % 2 * 2, 2)

        def TX(*halves):
            return [(turn_x, half(j), 0, 1, 2, 3) for j in halves]

        def W(*halves):
            return [(widen, half(j)) for j in halves]

        def X(*halves):
            return [(scale, half(j)) for j in halves]

        def passes(u, pair):
            run = []
            for a in range(4):
                run += [(weave, u, a)]
                if a // 2 < len(pair):
                    run += [(turn_x, half(pair[a // 2]), 2 * (a % 2), 2 * (a % 2) + 1)]
            return run

        vector += [(permute_words,)] + X(0, 1) + [(quant_x, 0)] + X(2, 3) + [(quant_x, 1)] + X(4, 5)
        vector += [(weave_vector, 0), (quant_x, 2), (quant_h, 0), (quant_wb, 0)] + X(6) + Y(0, 3)
        scalar += W(*range(7)) + H(0) + H(1, 0, 1) + [(unload_wb, 0, 0), (unload_wb, 0, 1)] + H(1, 2, 3)
        scalar += W(8) + H(2, 0, 1) + [(unload_wb, 1, 0)] + H(2, 2)
        clear(vector, "vector", BLK, 2 * BLK)
        vector += [(quant_h, 1), (quant_wb, 1)] + Y(3, 4) + X(7) + Y(4, 6)
        vector += [(quant_x, 3), (quant_h, 2)] + Y(6, 7) + X(8) + Y(7, 8) + [(bias, 8, 0, BLK - PIECE)]
        scalar += [(unload_wb, 1, 1)] + H(2, 3) + H(3, 0, 1)
        clear(scalar, "scalar", BLK, 3 * BLK)
        clear(vector, "vector", BLK, 6 * BLK)
        scalar += H(3, 2, 3) + W(9) + H(4) + W(10)
        gpsimd += [(permute_scales,)] + W(7) + [(weave_gpsimd, u) for u in range(4)]
        tensor += [(warm, 0), (warm, 1)] + TX(0, 1) + [(warm, 2)] + TX(2, 3) + [(warm, 3)] + MH(0) + TX(4, 5)
        tensor += MH(1, 0, 1) + [(turn_wb, 0, 0), (turn_wb, 0, 1)] + MH(1, 2, 3) + TX(6) + MH(2, 0, 1) + [(turn_wb, 1, 0)]
        tensor += MY(0) + MH(2, 2) + MY(1, 2) + [(turn_wb, 1, 1)] + MH(2, 3) + MH(3, 0) + MY(3) + MH(3, 1) + TX(7) + MH(3, 2) + MY(4) + MH(3, 3) + MY(5)
        tensor += MH(4, 0, 1, 2) + MY(6) + TX(8) + MH(4, 3) + MY(7) + MH(5, 0) + MY(8) + MH(5, 1)

        def halves(k):
            if k < SHORT:
                return [2 * k + 7, 2 * k + 8]
            return [j for j in (2 * k + 6, 2 * k + 7) if 2 * SHORT + 6 < j < UNITS]

        def share(k):
            return G_BASE + G_HALF * len(halves(k))

        def below_share(k):
            return ((8 * k - 1) * BLK + PIECE - share(k)) // BLK * BLK

        def tile_rest(below, grain=BLK):
            clear(scalar, "scalar", BLK - waiting[0][0] % BLK, below * BLK, grain)

        for k in range(1, GROUPS - 1):
            first, end = (8 if k == 1 else 8 * k - 1), 8 * k + 7
            pair = halves(k)
            odd, even = 2 * k + 3, 2 * k + 4
            ys = [MY(n) for n in range(first + 1, end + 1)] + [[]]
            if even < UNITS:
                if not pair:
                    clear(vector, "vector", V_RELU, below_share(k))
                if k == 1:
                    vector += [(quant_h, 3), (bias, 8, BLK - PIECE, BLK)] + X(*pair) + Y(first + 1, end)
                    clear_newest(3 * BLK, 9 * BLK)
                else:
                    vector += [(quant_x, k + 2), (quant_h, 2 * k), (bias, first, 0, PIECE), (quant_h, 2 * k + 1), (bias, first, PIECE, BLK)] + X(*pair) + Y(first + 1, end)
                    clear_newest(share(k), first * BLK + PIECE)
                gpsimd += [(weave_gpsimd, odd)]
                wide = [W(j) for j in halves(k + 1)] + [[], []]
                scalar += H(odd, 0, 1)
                if k == 1:
                    clear(scalar, "scalar", BLK, 6 * BLK)
                scalar += [(unload_h, even - 2, 0)] + wide[0]
                if not wide[0]:
                    tile_rest(first - 1)
                scalar += [(unload_h, even - 2, 1)] + H(odd, 2, 3)
                if pair:
                    scalar += H(even) + wide[1]
                    clear(scalar, "scalar", S_RELU if k > SHORT else S_EARLY, below_share(k + 1))
                else:
                    for t in range(4):
                        if t == 3:
                            clear(vector, "vector", V_LATE, (end - 2) * BLK)
                        scalar += H(even, t)
                        tile_rest(first + 1 + t if t < 3 else end - 2)
                    tile_rest(end - 2)
                tensor += passes(even - 2, pair) + MH(odd, 2) + ys[0] + MH(odd, 3) + ys[1]
                for t in range(4):
                    tensor += MH(even, t) + ys[2 + t]
                tensor += ys[6] + (MH(odd + 2, 0) + ys[7] + MH(odd + 2, 1) if pair else ys[7])
            else:
                vector += [(quant_h, 2 * k), (bias, first, 0, PIECE), (quant_h, 2 * k + 1), (bias, first, PIECE, BLK)] + Y(first + 1, end)
                clear_newest(G_BASE, first * BLK + PIECE)
                gpsimd += [(weave_gpsimd, odd - 1)]
                scalar += H(odd, 0)
                for t in range(4):
                    scalar += H(odd, t + 1) if t < 3 else []
                    tile_rest(first + 1 + t)
                clear(vector, "vector", BLK, (end - 1) * BLK)
                tensor += MH(odd) + MY(*range(first + 1, end + 1))
        gpsimd += [(weave_gpsimd, UNITS - 1)]
        vector += [(quant_h, UNITS - 2), (weave_vector, UNITS - 1)] + Y(TILES - 9, TILES - 6) + [(quant_h, UNITS - 1)] + Y(TILES - 6, TILES - 1)
        tensor += MY(*range(TILES - 8, TILES))
        vector += Y(TILES - 1, TILES)
        while waiting[0][0] < (TILES - 1) * BLK:
            tile_rest(TILES - 1, HID if waiting[0][0] < (TILES - 10) * BLK else BLK)
        clear(vector, "vector", BLK, TILES * BLK)
        assert not waiting


        def uses(step):
            call, i = step[0], step[1:]
            if call == widen:
                return [("xs",) + i], []
            if call == turn_x:
                return [("bank", "x", i[0])], [("xs", i[0])]
            if call == scale:
                return [("xg", i[0][0])], [("bank", "x") + i]
            if call == quant_x:
                return [("xc",) + i], [("xg",) + i]
            if call == fill_h:
                return [("bank", "h") + i], [("xc", i[0] // 2), ("w1",)]
            if call == relu_h:
                return [("hp", i[0])], [("bank", "h") + i]
            if call == weave:
                return [("bank", "w", i[0], i[1] // 2)], [("hp", i[0])]
            if call == unload_h:
                return [("hw", i[0])], [("bank", "w") + i]
            if call == weave_gpsimd:
                return [("hg",) + i], [("hp",) + i]
            if call == weave_vector:
                return [("hv",) + i], [("hp",) + i]
            if call == quant_h:
                return [("hc",) + i], [("hw" if by_pe(i[0]) else "hg",) + i] + ([("hv",) + i] if shared(i[0]) else [])
            if call == turn_wb:
                return [("bank", "wb") + i], []
            if call == unload_wb:
                return [("hw", "wb", i[0])], [("bank", "wb") + i]
            if call == quant_wb:
                return [("wb",) + i], [("hw", "wb") + i]
            if call == fill_y:
                return [("bank", "y") + i], [("hc", place(i[0])[0]), ("wb", place(i[0])[0] % 2)]
            if call == bias:
                return [], [("bank", "y", i[0])]
            if call == permute_scales or call == permute_words:
                return [("w1",)], []
            if call == warm:
                return [("bank", "warm") + i], []
            return [], []

        queues = [tensor, vector, scalar, gpsimd, sync]
        steps = [step for queue in queues for step in queue]
        makers, takers = {}, {}
        for step in steps:
            for key in uses(step)[0]:
                if key not in makers and kind(key) in order:
                    order[kind(key)].append(key)
                makers.setdefault(key, []).append(step)
            for key in uses(step)[1]:
                takers.setdefault(key, []).append(step)

        def needs(step):
            makes, takes = uses(step)
            before = [maker for key in takes for maker in makers[key]]
            for key in makes:
                if kind(key) in order and order[kind(key)].index(key) >= BUFS[kind(key)]:
                    before += takers.get(order[kind(key)][order[kind(key)].index(key) - BUFS[kind(key)]], [])
            if step[0] == relu:
                before += [b for b in vector if b[0] == bias and b[1] * BLK + b[2] < step[3] and b[1] * BLK + b[3] > step[2]]
            if step[0] == store:
                before += [r for r in steps if r[0] == relu and r[2] < step[2] and r[3] > step[1]]
            return before

        written = set()
        queues = [list(queue) for queue in queues]
        while any(queues):
            ready = [queue for queue in queues if queue and all(b in written for b in needs(queue[0]))]
            assert ready
            step = ready[0].pop(0)
            step[0](*step[1:])
            written.add(step)
